import numpy as np
import ml_dtypes


def mxq(x, axis, fmt="e4m3"):
    dtype, down = {"e4m3": (ml_dtypes.float8_e4m3fn, 7), "e5m2": (ml_dtypes.float8_e5m2, 14)}[fmt]
    v = np.moveaxis(np.asarray(x, np.float32).astype(ml_dtypes.bfloat16).astype(np.float64), axis, -1)
    blocks = v.reshape(v.shape[:-1] + (-1, 32))
    amax = np.abs(blocks).max(-1, keepdims=True)
    byte = np.maximum(np.where(amax > 0, np.frexp(amax)[1] - 1 + 127, 0) - down, 1)
    scale = np.exp2(byte - 127.0)
    codes = (blocks / scale).astype(np.float32).astype(dtype).astype(np.float64)
    return np.moveaxis((codes * scale).reshape(v.shape), -1, axis)


WIDE = False


def mx_kscale(k):
    if not WIDE:
        return np.ones(k)
    levels = np.array([20, -20, 10, -10, 0])
    a = np.random.permutation(np.resize(levels, k // 512 * 4)).reshape(k // 512, 4)
    idx = np.arange(k)
    return np.exp2(a[idx // 512, idx % 128 // 32])


BF16 = ml_dtypes.bfloat16


def bf(x):
    return np.asarray(x, np.float32).astype(BF16)


def f64(x):
    return np.asarray(x).astype(np.float64)


B, I, U = 1024, 1024, 512
G_SCALE = 4.0


def hard_sigmoid(v):
    return np.clip(0.2 * v + 0.5, 0.0, 1.0)


def hard_sigmoid_grad(v):
    return np.where(np.abs(v) < 2.5, 0.2, 0.0)


def setup_inputs():
    s = mx_kscale(B)[:, None]
    bias = np.random.standard_normal(4 * U) * 0.1
    bias[U:2 * U] += 1.0
    bias = bf(bias)
    inputs0 = bf(np.random.standard_normal((B, I)))
    h_tm1 = bf(np.random.standard_normal((B, U)))
    c_tm1 = bf(np.random.standard_normal((B, U)))
    z_tm1 = bf(np.random.standard_normal((B, U)))
    kernel = bf(np.random.standard_normal((I, 4 * U)) / np.sqrt(I))
    recurrent_kernel = bf(np.random.standard_normal((U, 4 * U)) / np.sqrt(U))
    recurrent_latent = bf(np.random.standard_normal((U, 4 * U)) / np.sqrt(U))
    g = bf(np.random.standard_normal((B, U)) * np.exp2(np.random.randint(-12, 1, (B, 1))) * G_SCALE / s)
    x = f64(inputs0) @ f64(kernel) + f64(h_tm1) @ f64(recurrent_kernel) + f64(z_tm1) @ f64(recurrent_latent) + f64(bias)
    return {"inputs": bf(f64(inputs0) * s),
            "h_tm1": h_tm1,
            "c_tm1": c_tm1,
            "z_tm1": z_tm1,
            "kernel": kernel,
            "recurrent_kernel": recurrent_kernel,
            "recurrent_latent": recurrent_latent,
            "bias": bias,
            "x": np.asarray(x, np.float32),
            "grad_out": g}


def reference(inputs, h_tm1, c_tm1, z_tm1, kernel, recurrent_kernel, recurrent_latent, bias, x, grad_out):
    x_i, x_f, x_c, x_o = np.split(f64(x), 4, axis=1)
    g = f64(grad_out)
    cp = f64(c_tm1)
    i = hard_sigmoid(x_i)
    f = hard_sigmoid(x_f)
    o = hard_sigmoid(x_o)
    tx = np.tanh(x_c)
    c = f * cp + i * tx
    tc = np.tanh(c)
    dc = g * o * (1.0 - tc * tc)
    dx_i = dc * tx * hard_sigmoid_grad(x_i)
    dx_f = dc * cp * hard_sigmoid_grad(x_f)
    dx_c = dc * i * (1.0 - tx * tx)
    dx_o = g * tc * hard_sigmoid_grad(x_o)
    dx = np.concatenate([dx_i, dx_f, dx_c, dx_o], axis=1)
    return mxq(f64(inputs), 0, "e4m3").T @ mxq(dx, 0, "e5m2")

@@ -1,0 +1,205 @@
+from contextlib import ExitStack
+
+import concourse.mybir as mybir
+
+F32 = mybir.dt.float32
+BF16 = mybir.dt.bfloat16
+U32 = mybir.dt.uint32
+U8 = mybir.dt.uint8
+E4M3_X4 = mybir.dt.float8_e4m3fn_x4
+E5M2_X4 = mybir.dt.float8_e5m2_x4
+ALU = mybir.AluOpType
+ACT = mybir.ActivationFunctionType
+
+TOKENS, FEATURES, UNITS = 1024, 1024, 512
+GATES = 4
+GATE_I, GATE_F, GATE_C, GATE_O = 0, 1, 2, 3
+P = 128
+PACK = 4
+K_PASS = P * PACK
+PASSES = TOKENS // K_PASS
+M_TILE = 128
+M_TILES = FEATURES // M_TILE
+N_TILE = 512
+U_CHUNK = N_TILE // GATES
+CHUNKS = UNITS // U_CHUNK
+U_LOAD = 2 * U_CHUNK
+HS_SLOPE, HS_EDGE = 0.2, 2.5
+
+FLOPS = 2 * TOKENS * FEATURES * GATES * UNITS
+BYTES = 2 * TOKENS * (FEATURES + 2 * UNITS) + 4 * TOKENS * GATES * UNITS + 4 * FEATURES * GATES * UNITS
+
+
+def tile_vlstmcell_v_kernel(
+    tc, inputs, h_tm1, c_tm1, z_tm1, kernel, recurrent_kernel, recurrent_latent, bias, x, grad_out, out
+):
+    nc = tc.nc
+    with ExitStack() as stack:
+        keep = stack.enter_context(tc.tile_pool(name="keep", bufs=1))
+        stage_in = stack.enter_context(tc.tile_pool(name="stage_in", bufs=2))
+        work = stack.enter_context(tc.tile_pool(name="work", bufs=2))
+        stage_dx = stack.enter_context(tc.tile_pool(name="stage_dx", bufs=2))
+        stage_out = stack.enter_context(tc.tile_pool(name="stage_out", bufs=4))
+        psum = stack.enter_context(tc.psum_pool(name="psum", bufs=M_TILES))
+
+        def token_rows(ap, c):
+            return ap[c * K_PASS : (c + 1) * K_PASS, :].rearrange("(p j) w -> p j w", j=PACK)
+
+        x_sb = {}
+        cell_sb = {}
+        grad_sb = {}
+        raw_in = {}
+
+        def load_x(c, half, gate):
+            x_sb[c, half, gate] = keep.tile([P, PACK, U_LOAD], F32, name="x_%d_%d_%d" % (c, half, gate))
+            first = gate * UNITS + half * U_LOAD
+            nc.sync.dma_start(out=x_sb[c, half, gate][:], in_=token_rows(x, c)[:, :, first : first + U_LOAD])
+
+        for c in range(PASSES):
+            load_x(c, 0, GATE_C)
+            load_x(c, 0, GATE_I)
+            raw_in[c] = stage_in.tile([P, PACK, FEATURES], BF16, name="raw_in")
+            nc.sync.dma_start(out=raw_in[c][:], in_=token_rows(inputs, c))
+            cell_sb[c] = keep.tile([P, PACK, UNITS], BF16, name="cell_%d" % c)
+            nc.sync.dma_start(out=cell_sb[c][:], in_=token_rows(c_tm1, c))
+            load_x(c, 0, GATE_F)
+            grad_sb[c] = keep.tile([P, PACK, UNITS], BF16, name="grad_%d" % c)
+            nc.sync.dma_start(out=grad_sb[c][:], in_=token_rows(grad_out, c))
+            load_x(c, 0, GATE_O)
+            for gate in (GATE_C, GATE_I, GATE_F, GATE_O):
+                load_x(c, 1, gate)
+
+        in_codes = keep.tile([P, PASSES, FEATURES], U32, align_bytes=64)
+        in_scales = keep.tile([P, PASSES, FEATURES], U8, align_bytes=64)
+        for c in range(PASSES):
+            grouped_in = stage_in.tile([P, FEATURES, PACK], BF16, align_bytes=64)
+            nc.vector.tensor_copy(
+                out=grouped_in[:].rearrange("p (w i) j -> p w j i", i=4),
+                in_=raw_in[c][:].rearrange("p j (w i) -> p w j i", i=4),
+            )
+            nc.vector.quantize_mx(
+                out=in_codes[:, c, :].bitcast(E4M3_X4),
+                scales=in_scales[:, c, :],
+                in_=grouped_in[:].rearrange("p w j -> p (w j)"),
+            )
+
+        dx_codes = keep.tile([P, PASSES, CHUNKS, N_TILE], U32, align_bytes=64)
+        dx_scales = keep.tile([P, PASSES, CHUNKS, N_TILE], U8, align_bytes=64)
+
+        def gradient_chunk(c, q):
+            shape = [P, PACK, U_CHUNK]
+            half, first = divmod(q * U_CHUNK, U_LOAD)
+            x_i, x_f, x_c, x_o = [x_sb[c, half, gate][:, :, first : first + U_CHUNK] for gate in range(GATES)]
+            cell = cell_sb[c][:, :, q * U_CHUNK : (q + 1) * U_CHUNK]
+            grad = grad_sb[c][:, :, q * U_CHUNK : (q + 1) * U_CHUNK]
+
+            tanh_x = work.tile(shape, F32)
+            nc.scalar.activation(out=tanh_x[:], in_=x_c, func=ACT.Tanh)
+            ramp_i = work.tile(shape, F32)
+            nc.scalar.activation(out=ramp_i[:], in_=x_i, func=ACT.Relu, bias=0.5, scale=HS_SLOPE)
+            ramp_f = work.tile(shape, F32)
+            nc.scalar.activation(out=ramp_f[:], in_=x_f, func=ACT.Relu, bias=0.5, scale=HS_SLOPE)
+            ramp_o = work.tile(shape, F32)
+            nc.scalar.activation(out=ramp_o[:], in_=x_o, func=ACT.Relu, bias=0.5, scale=HS_SLOPE)
+            abs_i = work.tile(shape, F32)
+            nc.scalar.activation(out=abs_i[:], in_=x_i, func=ACT.Abs)
+            abs_f = work.tile(shape, F32)
+            nc.scalar.activation(out=abs_f[:], in_=x_f, func=ACT.Abs)
+            abs_o = work.tile(shape, F32)
+            nc.scalar.activation(out=abs_o[:], in_=x_o, func=ACT.Abs)
+            tanh_x_sq = work.tile(shape, F32)
+            nc.scalar.activation(out=tanh_x_sq[:], in_=tanh_x[:], func=ACT.Square)
+
+            i_tanh_x = work.tile(shape, F32)
+            nc.vector.scalar_tensor_tensor(
+                out=i_tanh_x[:], in0=ramp_i[:], scalar=1.0, in1=tanh_x[:], op0=ALU.min, op1=ALU.mult
+            )
+            f_cell = work.tile(shape, F32)
+            nc.vector.scalar_tensor_tensor(
+                out=f_cell[:], in0=ramp_f[:], scalar=1.0, in1=cell, op0=ALU.min, op1=ALU.mult
+            )
+            new_cell = work.tile(shape, F32)
+            nc.vector.tensor_tensor(out=new_cell[:], in0=i_tanh_x[:], in1=f_cell[:], op=ALU.add)
+            tanh_c = work.tile(shape, F32)
+            nc.scalar.activation(out=tanh_c[:], in_=new_cell[:], func=ACT.Tanh)
+            tanh_c_sq = work.tile(shape, F32)
+            nc.scalar.activation(out=tanh_c_sq[:], in_=tanh_c[:], func=ACT.Square)
+
+            o_grad = work.tile(shape, F32)
+            nc.vector.scalar_tensor_tensor(
+                out=o_grad[:], in0=ramp_o[:], scalar=1.0, in1=grad, op0=ALU.min, op1=ALU.mult
+            )
+            open_o_grad = work.tile(shape, BF16)
+            nc.vector.scalar_tensor_tensor(
+                out=open_o_grad[:], in0=abs_o[:], scalar=HS_EDGE, in1=grad, op0=ALU.is_lt, op1=ALU.mult
+            )
+            open_i_tanh_x = work.tile(shape, F32)
+            nc.vector.scalar_tensor_tensor(
+                out=open_i_tanh_x[:], in0=abs_i[:], scalar=HS_EDGE, in1=tanh_x[:], op0=ALU.is_lt, op1=ALU.mult
+            )
+            open_f_cell = work.tile(shape, BF16)
+            nc.vector.scalar_tensor_tensor(
+                out=open_f_cell[:], in0=abs_f[:], scalar=HS_EDGE, in1=cell, op0=ALU.is_lt, op1=ALU.mult
+            )
+
+            minus_dc = work.tile(shape, F32)
+            nc.vector.scalar_tensor_tensor(
+                out=minus_dc[:], in0=tanh_c_sq[:], scalar=1.0, in1=o_grad[:], op0=ALU.subtract, op1=ALU.mult
+            )
+            minus_dc_i = work.tile(shape, F32)
+            nc.vector.scalar_tensor_tensor(
+                out=minus_dc_i[:], in0=ramp_i[:], scalar=1.0, in1=minus_dc[:], op0=ALU.min, op1=ALU.mult
+            )
+
+            grouped_dx = stage_dx.tile([P, GATES, U_CHUNK, PACK], BF16, align_bytes=64)
+
+            def last_product(gate, in0, scalar, op0, in1):
+                nc.vector.scalar_tensor_tensor(
+                    out=grouped_dx[:, gate, :, :],
+                    in0=in0[:].rearrange("p j u -> p u j"),
+                    scalar=scalar,
+                    in1=in1[:].rearrange("p j u -> p u j"),
+                    op0=op0,
+                    op1=ALU.mult,
+                )
+
+            last_product(GATE_O, tanh_c, HS_SLOPE, ALU.mult, open_o_grad)
+            last_product(GATE_I, minus_dc, -HS_SLOPE, ALU.mult, open_i_tanh_x)
+            last_product(GATE_F, minus_dc, -HS_SLOPE, ALU.mult, open_f_cell)
+            last_product(GATE_C, tanh_x_sq, 1.0, ALU.subtract, minus_dc_i)
+            nc.vector.quantize_mx(
+                out=dx_codes[:, c, q, :].bitcast(E5M2_X4),
+                scales=dx_scales[:, c, q, :],
+                in_=grouped_dx[:].rearrange("p g u j -> p (g u j)"),
+            )
+
+        def multiply_chunk(q):
+            sums = [psum.tile([M_TILE, N_TILE], F32, name="sums") for m in range(M_TILES)]
+            for c in range(PASSES):
+                for m in range(M_TILES):
+                    features = slice(m * M_TILE, (m + 1) * M_TILE)
+                    nc.tensor.matmul_mx(
+                        out=sums[m][:],
+                        lhsT=in_codes[:, c, features].bitcast(E4M3_X4),
+                        lhsT_scale=in_scales[:, c, features],
+                        rhs=dx_codes[:, c, q, :].bitcast(E5M2_X4),
+                        rhs_scale=dx_scales[:, c, q, :],
+                        start=(c == 0),
+                        stop=(c == PASSES - 1),
+                    )
+            for m in range(M_TILES):
+                result = stage_out.tile([M_TILE, GATES, U_CHUNK], F32)
+                nc.scalar.copy(out=result[:].rearrange("p g u -> p (g u)"), in_=sums[m][:])
+                nc.sync.dma_start(
+                    out=out[m * M_TILE : (m + 1) * M_TILE, :].rearrange(
+                        "i (g q u) -> i g q u", g=GATES, q=CHUNKS
+                    )[:, :, q, :],
+                    in_=result[:],
+                )
+
+        for c in range(PASSES - 1):
+            for q in range(CHUNKS):
+                gradient_chunk(c, q)
+        for q in range(CHUNKS):
+            gradient_chunk(PASSES - 1, q)
+            multiply_chunk(q)

@@ -22,8 +22,9 @@ M_TILE = 128
 M_TILES = FEATURES // M_TILE
 N_TILE = 512
 U_CHUNK = N_TILE // GATES
-CHUNKS = UNITS // U_CHUNK
-U_LOAD = 2 * U_CHUNK
+ROUNDS = UNITS // U_CHUNK
+CHUNKS = ROUNDS * PASSES
+F_PIECE = 512
 HS_SLOPE, HS_EDGE = 0.2, 2.5
 
 FLOPS = 2 * TOKENS * FEATURES * GATES * UNITS
@@ -39,8 +40,9 @@ def tile_vlstmcell_v_kernel(
         stage_in = stack.enter_context(tc.tile_pool(name="stage_in", bufs=2))
         work = stack.enter_context(tc.tile_pool(name="work", bufs=2))
         stage_dx = stack.enter_context(tc.tile_pool(name="stage_dx", bufs=2))
-        stage_out = stack.enter_context(tc.tile_pool(name="stage_out", bufs=4))
+        stage_out = stack.enter_context(tc.tile_pool(name="stage_out", bufs=M_TILES))
         psum = stack.enter_context(tc.psum_pool(name="psum", bufs=M_TILES))
+        stack.enter_context(tc.manual_schedule())
 
         def token_rows(ap, c):
             return ap[c * K_PASS : (c + 1) * K_PASS, :].rearrange("(p j) w -> p j w", j=PACK)
@@ -50,156 +52,230 @@ def tile_vlstmcell_v_kernel(
         grad_sb = {}
         raw_in = {}
 
-        def load_x(c, half, gate):
-            x_sb[c, half, gate] = keep.tile([P, PACK, U_LOAD], F32, name="x_%d_%d_%d" % (c, half, gate))
-            first = gate * UNITS + half * U_LOAD
-            nc.sync.dma_start(out=x_sb[c, half, gate][:], in_=token_rows(x, c)[:, :, first : first + U_LOAD])
+        def load_x(r, c, gate):
+            x_sb[r, c, gate] = keep.tile([P, PACK, U_CHUNK], F32, name="x_%d_%d_%d" % (r, c, gate))
+            first = gate * UNITS + r * U_CHUNK
+            nc.sync.dma_start(out=x_sb[r, c, gate][:], in_=token_rows(x, c)[:, :, first : first + U_CHUNK])
+
+        def load_inputs(c, piece):
+            raw_in[c, piece] = keep.tile([P, PACK, F_PIECE], BF16, name="raw_in_%d_%d" % (c, piece))
+            nc.sync.dma_start(
+                out=raw_in[c, piece][:], in_=token_rows(inputs, c)[:, :, piece * F_PIECE : (piece + 1) * F_PIECE]
+            )
 
         for c in range(PASSES):
-            load_x(c, 0, GATE_C)
-            load_x(c, 0, GATE_I)
-            raw_in[c] = stage_in.tile([P, PACK, FEATURES], BF16, name="raw_in")
-            nc.sync.dma_start(out=raw_in[c][:], in_=token_rows(inputs, c))
+            load_inputs(c, 0)
+            load_x(0, c, GATE_C)
+            load_x(0, c, GATE_I)
+            load_inputs(c, 1)
             cell_sb[c] = keep.tile([P, PACK, UNITS], BF16, name="cell_%d" % c)
             nc.sync.dma_start(out=cell_sb[c][:], in_=token_rows(c_tm1, c))
-            load_x(c, 0, GATE_F)
+            load_x(0, c, GATE_F)
             grad_sb[c] = keep.tile([P, PACK, UNITS], BF16, name="grad_%d" % c)
             nc.sync.dma_start(out=grad_sb[c][:], in_=token_rows(grad_out, c))
-            load_x(c, 0, GATE_O)
-            for gate in (GATE_C, GATE_I, GATE_F, GATE_O):
-                load_x(c, 1, gate)
+            load_x(0, c, GATE_O)
+        for r in range(1, ROUNDS):
+            for c in range(PASSES):
+                for gate in (GATE_C, GATE_I, GATE_F, GATE_O):
+                    load_x(r, c, gate)
 
         in_codes = keep.tile([P, PASSES, FEATURES], U32, align_bytes=64)
         in_scales = keep.tile([P, PASSES, FEATURES], U8, align_bytes=64)
-        for c in range(PASSES):
-            grouped_in = stage_in.tile([P, FEATURES, PACK], BF16, align_bytes=64)
+        grouped_in = {}
+
+        def regroup_inputs(c, piece):
+            if c >= PASSES:
+                return
+            grouped_in[c, piece] = stage_in.tile([P, F_PIECE, PACK], BF16, align_bytes=64, name="grouped_in")
             nc.vector.tensor_copy(
-                out=grouped_in[:].rearrange("p (w i) j -> p w j i", i=4),
-                in_=raw_in[c][:].rearrange("p j (w i) -> p w j i", i=4),
+                out=grouped_in[c, piece][:].rearrange("p (w i) j -> p w j i", i=4),
+                in_=raw_in[c, piece][:].rearrange("p j (w i) -> p w j i", i=4),
             )
+
+        def quantise_inputs(c, piece):
+            if c >= PASSES:
+                return
+            features = slice(piece * F_PIECE, (piece + 1) * F_PIECE)
             nc.vector.quantize_mx(
-                out=in_codes[:, c, :].bitcast(E4M3_X4),
-                scales=in_scales[:, c, :],
-                in_=grouped_in[:].rearrange("p w j -> p (w j)"),
+                out=in_codes[:, c, features].bitcast(E4M3_X4),
+                scales=in_scales[:, c, features],
+                in_=grouped_in[c, piece][:].rearrange("p w j -> p (w j)"),
             )
 
-        dx_codes = keep.tile([P, PASSES, CHUNKS, N_TILE], U32, align_bytes=64)
-        dx_scales = keep.tile([P, PASSES, CHUNKS, N_TILE], U8, align_bytes=64)
+        dx_codes = keep.tile([P, PASSES, ROUNDS, N_TILE], U32, align_bytes=64)
+        dx_scales = keep.tile([P, PASSES, ROUNDS, N_TILE], U8, align_bytes=64)
 
-        def gradient_chunk(c, q):
-            shape = [P, PACK, U_CHUNK]
-            half, first = divmod(q * U_CHUNK, U_LOAD)
-            x_i, x_f, x_c, x_o = [x_sb[c, half, gate][:, :, first : first + U_CHUNK] for gate in range(GATES)]
-            cell = cell_sb[c][:, :, q * U_CHUNK : (q + 1) * U_CHUNK]
-            grad = grad_sb[c][:, :, q * U_CHUNK : (q + 1) * U_CHUNK]
+        planes = {}
 
-            tanh_x = work.tile(shape, F32)
-            nc.scalar.activation(out=tanh_x[:], in_=x_c, func=ACT.Tanh)
-            ramp_i = work.tile(shape, F32)
-            nc.scalar.activation(out=ramp_i[:], in_=x_i, func=ACT.Relu, bias=0.5, scale=HS_SLOPE)
-            ramp_f = work.tile(shape, F32)
-            nc.scalar.activation(out=ramp_f[:], in_=x_f, func=ACT.Relu, bias=0.5, scale=HS_SLOPE)
-            ramp_o = work.tile(shape, F32)
-            nc.scalar.activation(out=ramp_o[:], in_=x_o, func=ACT.Relu, bias=0.5, scale=HS_SLOPE)
-            abs_i = work.tile(shape, F32)
-            nc.scalar.activation(out=abs_i[:], in_=x_i, func=ACT.Abs)
-            abs_f = work.tile(shape, F32)
-            nc.scalar.activation(out=abs_f[:], in_=x_f, func=ACT.Abs)
-            abs_o = work.tile(shape, F32)
-            nc.scalar.activation(out=abs_o[:], in_=x_o, func=ACT.Abs)
-            tanh_x_sq = work.tile(shape, F32)
-            nc.scalar.activation(out=tanh_x_sq[:], in_=tanh_x[:], func=ACT.Square)
+        def no_chunk(k):
+            return k < 0 or k >= CHUNKS
 
-            i_tanh_x = work.tile(shape, F32)
-            nc.vector.scalar_tensor_tensor(
-                out=i_tanh_x[:], in0=ramp_i[:], scalar=1.0, in1=tanh_x[:], op0=ALU.min, op1=ALU.mult
-            )
-            f_cell = work.tile(shape, F32)
-            nc.vector.scalar_tensor_tensor(
-                out=f_cell[:], in0=ramp_f[:], scalar=1.0, in1=cell, op0=ALU.min, op1=ALU.mult
-            )
-            new_cell = work.tile(shape, F32)
-            nc.vector.tensor_tensor(out=new_cell[:], in0=i_tanh_x[:], in1=f_cell[:], op=ALU.add)
-            tanh_c = work.tile(shape, F32)
-            nc.scalar.activation(out=tanh_c[:], in_=new_cell[:], func=ACT.Tanh)
-            tanh_c_sq = work.tile(shape, F32)
-            nc.scalar.activation(out=tanh_c_sq[:], in_=tanh_c[:], func=ACT.Square)
+        def new_plane(name, k, dtype=F32):
+            planes[name, k] = work.tile([P, PACK, U_CHUNK], dtype, name=name)
+            return planes[name, k][:]
 
-            o_grad = work.tile(shape, F32)
-            nc.vector.scalar_tensor_tensor(
-                out=o_grad[:], in0=ramp_o[:], scalar=1.0, in1=grad, op0=ALU.min, op1=ALU.mult
-            )
-            open_o_grad = work.tile(shape, BF16)
-            nc.vector.scalar_tensor_tensor(
-                out=open_o_grad[:], in0=abs_o[:], scalar=HS_EDGE, in1=grad, op0=ALU.is_lt, op1=ALU.mult
-            )
-            open_i_tanh_x = work.tile(shape, F32)
-            nc.vector.scalar_tensor_tensor(
-                out=open_i_tanh_x[:], in0=abs_i[:], scalar=HS_EDGE, in1=tanh_x[:], op0=ALU.is_lt, op1=ALU.mult
-            )
-            open_f_cell = work.tile(shape, BF16)
-            nc.vector.scalar_tensor_tensor(
-                out=open_f_cell[:], in0=abs_f[:], scalar=HS_EDGE, in1=cell, op0=ALU.is_lt, op1=ALU.mult
-            )
+        def x_of(gate, k):
+            return x_sb[k // PASSES, k % PASSES, gate][:]
 
-            minus_dc = work.tile(shape, F32)
-            nc.vector.scalar_tensor_tensor(
-                out=minus_dc[:], in0=tanh_c_sq[:], scalar=1.0, in1=o_grad[:], op0=ALU.subtract, op1=ALU.mult
-            )
-            minus_dc_i = work.tile(shape, F32)
-            nc.vector.scalar_tensor_tensor(
-                out=minus_dc_i[:], in0=ramp_i[:], scalar=1.0, in1=minus_dc[:], op0=ALU.min, op1=ALU.mult
-            )
+        def units_of(by_pass, k):
+            r, c = divmod(k, PASSES)
+            return by_pass[c][:, :, r * U_CHUNK : (r + 1) * U_CHUNK]
 
-            grouped_dx = stage_dx.tile([P, GATES, U_CHUNK, PACK], BF16, align_bytes=64)
+        def function(name, k, func, in_, scale=1.0, bias=0.0):
+            nc.scalar.activation(out=new_plane(name, k), in_=in_, func=func, bias=bias, scale=scale)
 
-            def last_product(gate, in0, scalar, op0, in1):
-                nc.vector.scalar_tensor_tensor(
-                    out=grouped_dx[:, gate, :, :],
-                    in0=in0[:].rearrange("p j u -> p u j"),
-                    scalar=scalar,
-                    in1=in1[:].rearrange("p j u -> p u j"),
-                    op0=op0,
-                    op1=ALU.mult,
+        def product(out_ap, in0, scalar, op0, in1):
+            nc.vector.scalar_tensor_tensor(out=out_ap, in0=in0, scalar=scalar, in1=in1, op0=op0, op1=ALU.mult)
+
+        def tanh_x(k):
+            if not no_chunk(k):
+                function("tanh_x", k, ACT.Tanh, x_of(GATE_C, k))
+
+        def ramp_and_size(name, gate, k):
+            if not no_chunk(k):
+                function("ramp_" + name, k, ACT.Relu, x_of(gate, k), scale=HS_SLOPE, bias=0.5)
+                function("abs_" + name, k, ACT.Abs, x_of(gate, k))
+
+        def tanh_x_sq(k):
+            if not no_chunk(k):
+                function("tanh_x_sq", k, ACT.Square, planes["tanh_x", k][:])
+
+        def tanh_c(k):
+            if not no_chunk(k):
+                function("tanh_c", k, ACT.Tanh, planes["new_cell", k][:])
+
+        def tanh_c_sq(k):
+            if not no_chunk(k):
+                function("tanh_c_sq", k, ACT.Square, planes["tanh_c", k][:])
+
+        def i_tanh_x(k):
+            if not no_chunk(k):
+                product(new_plane("i_tanh_x", k), planes["ramp_i", k][:], 1.0, ALU.min, planes["tanh_x", k][:])
+
+        def f_cell(k):
+            if not no_chunk(k):
+                product(new_plane("f_cell", k), planes["ramp_f", k][:], 1.0, ALU.min, units_of(cell_sb, k))
+
+        def new_cell(k):
+            if not no_chunk(k):
+                nc.vector.tensor_tensor(
+                    out=new_plane("new_cell", k), in0=planes["i_tanh_x", k][:], in1=planes["f_cell", k][:], op=ALU.add
                 )
 
-            last_product(GATE_O, tanh_c, HS_SLOPE, ALU.mult, open_o_grad)
-            last_product(GATE_I, minus_dc, -HS_SLOPE, ALU.mult, open_i_tanh_x)
-            last_product(GATE_F, minus_dc, -HS_SLOPE, ALU.mult, open_f_cell)
-            last_product(GATE_C, tanh_x_sq, 1.0, ALU.subtract, minus_dc_i)
-            nc.vector.quantize_mx(
-                out=dx_codes[:, c, q, :].bitcast(E5M2_X4),
-                scales=dx_scales[:, c, q, :],
-                in_=grouped_dx[:].rearrange("p g u j -> p (g u j)"),
+        def o_grad(k):
+            if not no_chunk(k):
+                product(new_plane("o_grad", k), planes["ramp_o", k][:], 1.0, ALU.min, units_of(grad_sb, k))
+
+        def open_o_grad(k):
+            if not no_chunk(k):
+                product(new_plane("open_o_grad", k, BF16), planes["abs_o", k][:], HS_EDGE, ALU.is_lt, units_of(grad_sb, k))
+
+        def open_i_tanh_x(k):
+            if not no_chunk(k):
+                product(new_plane("open_i_tanh_x", k), planes["abs_i", k][:], HS_EDGE, ALU.is_lt, planes["tanh_x", k][:])
+
+        def open_f_cell(k):
+            if not no_chunk(k):
+                product(new_plane("open_f_cell", k, BF16), planes["abs_f", k][:], HS_EDGE, ALU.is_lt, units_of(cell_sb, k))
+
+        def minus_dc(k):
+            if not no_chunk(k):
+                product(new_plane("minus_dc", k), planes["tanh_c_sq", k][:], 1.0, ALU.subtract, planes["o_grad", k][:])
+
+        def minus_dc_i(k):
+            if not no_chunk(k):
+                product(new_plane("minus_dc_i", k), planes["ramp_i", k][:], 1.0, ALU.min, planes["minus_dc", k][:])
+
+        grouped_dx = {}
+
+        def dx(gate, k, in0, scalar, op0, in1):
+            if no_chunk(k):
+                return
+            if k not in grouped_dx:
+                grouped_dx[k] = stage_dx.tile([P, GATES, U_CHUNK, PACK], BF16, align_bytes=64, name="grouped_dx")
+            product(
+                grouped_dx[k][:, gate, :, :],
+                planes[in0, k][:].rearrange("p j u -> p u j"),
+                scalar,
+                op0,
+                planes[in1, k][:].rearrange("p j u -> p u j"),
             )
 
-        def multiply_chunk(q):
-            sums = [psum.tile([M_TILE, N_TILE], F32, name="sums") for m in range(M_TILES)]
-            for c in range(PASSES):
-                for m in range(M_TILES):
-                    features = slice(m * M_TILE, (m + 1) * M_TILE)
-                    nc.tensor.matmul_mx(
-                        out=sums[m][:],
-                        lhsT=in_codes[:, c, features].bitcast(E4M3_X4),
-                        lhsT_scale=in_scales[:, c, features],
-                        rhs=dx_codes[:, c, q, :].bitcast(E5M2_X4),
-                        rhs_scale=dx_scales[:, c, q, :],
-                        start=(c == 0),
-                        stop=(c == PASSES - 1),
-                    )
+        def quantise_dx(k):
+            if no_chunk(k):
+                return
+            r, c = divmod(k, PASSES)
+            nc.vector.quantize_mx(
+                out=dx_codes[:, c, r, :].bitcast(E5M2_X4),
+                scales=dx_scales[:, c, r, :],
+                in_=grouped_dx[k][:].rearrange("p g u j -> p (g u j)"),
+            )
+
+        sums = {}
+
+        def multiply(k):
+            if no_chunk(k):
+                return
+            r, c = divmod(k, PASSES)
             for m in range(M_TILES):
+                if c == 0:
+                    sums[r, m] = psum.tile([M_TILE, N_TILE], F32, name="sums")
+                features = slice(m * M_TILE, (m + 1) * M_TILE)
+                nc.tensor.matmul_mx(
+                    out=sums[r, m][:],
+                    lhsT=in_codes[:, c, features].bitcast(E4M3_X4),
+                    lhsT_scale=in_scales[:, c, features],
+                    rhs=dx_codes[:, c, r, :].bitcast(E5M2_X4),
+                    rhs_scale=dx_scales[:, c, r, :],
+                    start=(c == 0),
+                    stop=(c == PASSES - 1),
+                )
+
+        def empty_banks(r, part, copy):
+            for m in range(part, M_TILES, PASSES):
                 result = stage_out.tile([M_TILE, GATES, U_CHUNK], F32)
-                nc.scalar.copy(out=result[:].rearrange("p g u -> p (g u)"), in_=sums[m][:])
+                copy(out=result[:].rearrange("p g u -> p (g u)"), in_=sums[r, m][:])
                 nc.sync.dma_start(
                     out=out[m * M_TILE : (m + 1) * M_TILE, :].rearrange(
-                        "i (g q u) -> i g q u", g=GATES, q=CHUNKS
-                    )[:, :, q, :],
+                        "i (g r u) -> i g r u", g=GATES, r=ROUNDS
+                    )[:, :, r, :],
                     in_=result[:],
                 )
 
-        for c in range(PASSES - 1):
-            for q in range(CHUNKS):
-                gradient_chunk(c, q)
-        for q in range(CHUNKS):
-            gradient_chunk(PASSES - 1, q)
-            multiply_chunk(q)
+        tanh_x(0)
+        ramp_and_size("i", GATE_I, 0)
+        ramp_and_size("f", GATE_F, 0)
+        ramp_and_size("o", GATE_O, 0)
+        tanh_x_sq(0)
+        for t in range(CHUNKS + 1):
+            regroup_inputs(t, 0)
+            i_tanh_x(t)
+            minus_dc(t - 1)
+            regroup_inputs(t, 1)
+            f_cell(t)
+            dx(GATE_O, t - 1, "tanh_c", HS_SLOPE, ALU.mult, "open_o_grad")
+            quantise_inputs(t, 0)
+            new_cell(t)
+            minus_dc_i(t - 1)
+            open_i_tanh_x(t)
+            dx(GATE_I, t - 1, "minus_dc", -HS_SLOPE, ALU.mult, "open_i_tanh_x")
+            open_f_cell(t)
+            dx(GATE_C, t - 1, "tanh_x_sq", 1.0, ALU.subtract, "minus_dc_i")
+            quantise_inputs(t, 1)
+            o_grad(t)
+            dx(GATE_F, t - 1, "minus_dc", -HS_SLOPE, ALU.mult, "open_f_cell")
+            open_o_grad(t)
+            quantise_dx(t - 1)
+
+            multiply(t - 1)
+
+            tanh_c(t)
+            tanh_x(t + 1)
+            tanh_c_sq(t)
+            ramp_and_size("i", GATE_I, t + 1)
+            ramp_and_size("f", GATE_F, t + 1)
+            ramp_and_size("o", GATE_O, t + 1)
+            tanh_x_sq(t + 1)
+            if t >= PASSES:
+                empty_banks((t - PASSES) // PASSES, (t - PASSES) % PASSES, nc.scalar.copy)
+        empty_banks(ROUNDS - 1, PASSES - 1, nc.vector.tensor_copy)

@@ -1,6 +1,7 @@
 from contextlib import ExitStack
 
 import concourse.mybir as mybir
+from concourse.masks import make_identity
 
 F32 = mybir.dt.float32
 BF16 = mybir.dt.bfloat16
@@ -21,6 +22,7 @@ PASSES = TOKENS // K_PASS
 M_TILE = 128
 M_TILES = FEATURES // M_TILE
 N_TILE = 512
+BANKS = 8
 U_CHUNK = N_TILE // GATES
 ROUNDS = UNITS // U_CHUNK
 CHUNKS = ROUNDS * PASSES
@@ -39,23 +41,34 @@ def tile_vlstmcell_v_kernel(
         keep = stack.enter_context(tc.tile_pool(name="keep", bufs=1))
         stage_in = stack.enter_context(tc.tile_pool(name="stage_in", bufs=2))
         work = stack.enter_context(tc.tile_pool(name="work", bufs=2))
+        work_long = stack.enter_context(tc.tile_pool(name="work_long", bufs=3))
         stage_dx = stack.enter_context(tc.tile_pool(name="stage_dx", bufs=2))
         stage_out = stack.enter_context(tc.tile_pool(name="stage_out", bufs=M_TILES))
-        psum = stack.enter_context(tc.psum_pool(name="psum", bufs=M_TILES))
+        psum = stack.enter_context(tc.psum_pool(name="psum", bufs=BANKS))
         stack.enter_context(tc.manual_schedule())
 
         def token_rows(ap, c):
             return ap[c * K_PASS : (c + 1) * K_PASS, :].rearrange("(p j) w -> p j w", j=PACK)
 
-        x_sb = {}
-        cell_sb = {}
-        grad_sb = {}
+        def no_chunk(k):
+            return k < 0 or k >= CHUNKS
+
+        loaded = {}
         raw_in = {}
 
-        def load_x(r, c, gate):
-            x_sb[r, c, gate] = keep.tile([P, PACK, U_CHUNK], F32, name="x_%d_%d_%d" % (r, c, gate))
-            first = gate * UNITS + r * U_CHUNK
-            nc.sync.dma_start(out=x_sb[r, c, gate][:], in_=token_rows(x, c)[:, :, first : first + U_CHUNK])
+        def load(name, k, source, first_column, dtype):
+            r, c = divmod(k, PASSES)
+            first = first_column + r * U_CHUNK
+            loaded[name, k] = keep.tile([P, PACK, U_CHUNK], dtype, name="%s_%d" % (name, k))
+            nc.sync.dma_start(out=loaded[name, k][:], in_=token_rows(source, c)[:, :, first : first + U_CHUNK])
+
+        def load_chunk(k):
+            load("x_c", k, x, GATE_C * UNITS, F32)
+            load("x_i", k, x, GATE_I * UNITS, F32)
+            load("cell", k, c_tm1, 0, BF16)
+            load("x_f", k, x, GATE_F * UNITS, F32)
+            load("grad", k, grad_out, 0, BF16)
+            load("x_o", k, x, GATE_O * UNITS, F32)
 
         def load_inputs(c, piece):
             raw_in[c, piece] = keep.tile([P, PACK, F_PIECE], BF16, name="raw_in_%d_%d" % (c, piece))
@@ -63,21 +76,17 @@ def tile_vlstmcell_v_kernel(
                 out=raw_in[c, piece][:], in_=token_rows(inputs, c)[:, :, piece * F_PIECE : (piece + 1) * F_PIECE]
             )
 
-        for c in range(PASSES):
-            load_inputs(c, 0)
-            load_x(0, c, GATE_C)
-            load_x(0, c, GATE_I)
-            load_inputs(c, 1)
-            cell_sb[c] = keep.tile([P, PACK, UNITS], BF16, name="cell_%d" % c)
-            nc.sync.dma_start(out=cell_sb[c][:], in_=token_rows(c_tm1, c))
-            load_x(0, c, GATE_F)
-            grad_sb[c] = keep.tile([P, PACK, UNITS], BF16, name="grad_%d" % c)
-            nc.sync.dma_start(out=grad_sb[c][:], in_=token_rows(grad_out, c))
-            load_x(0, c, GATE_O)
-        for r in range(1, ROUNDS):
-            for c in range(PASSES):
-                for gate in (GATE_C, GATE_I, GATE_F, GATE_O):
-                    load_x(r, c, gate)
+        load_inputs(0, 0)
+        load_chunk(0)
+        load_inputs(0, 1)
+        load_inputs(1, 0)
+        load_chunk(1)
+        load_inputs(1, 1)
+        for k in range(2, CHUNKS):
+            load_chunk(k)
+
+        identity = keep.tile([P, P], F32)
+        make_identity(nc, identity[:])
 
         in_codes = keep.tile([P, PASSES, FEATURES], U32, align_bytes=64)
         in_scales = keep.tile([P, PASSES, FEATURES], U8, align_bytes=64)
@@ -107,84 +116,82 @@ def tile_vlstmcell_v_kernel(
 
         planes = {}
 
-        def no_chunk(k):
-            return k < 0 or k >= CHUNKS
-
-        def new_plane(name, k, dtype=F32):
-            planes[name, k] = work.tile([P, PACK, U_CHUNK], dtype, name=name)
+        def new_plane(name, k, dtype=F32, pool=work):
+            planes[name, k] = pool.tile([P, PACK, U_CHUNK], dtype, name=name)
             return planes[name, k][:]
 
-        def x_of(gate, k):
-            return x_sb[k // PASSES, k % PASSES, gate][:]
+        def function(name, k, func, in_, scale=1.0, bias=0.0, pool=work):
+            if not no_chunk(k):
+                nc.scalar.activation(out=new_plane(name, k, pool=pool), in_=in_(k), func=func, bias=bias, scale=scale)
 
-        def units_of(by_pass, k):
-            r, c = divmod(k, PASSES)
-            return by_pass[c][:, :, r * U_CHUNK : (r + 1) * U_CHUNK]
+        def product(name, k, in0, scalar, op0, in1, dtype=F32):
+            if not no_chunk(k):
+                nc.vector.scalar_tensor_tensor(
+                    out=new_plane(name, k, dtype), in0=in0(k), scalar=scalar, in1=in1(k), op0=op0, op1=ALU.mult
+                )
 
-        def function(name, k, func, in_, scale=1.0, bias=0.0):
-            nc.scalar.activation(out=new_plane(name, k), in_=in_, func=func, bias=bias, scale=scale)
+        def from_hbm(name):
+            return lambda k: loaded[name, k][:]
 
-        def product(out_ap, in0, scalar, op0, in1):
-            nc.vector.scalar_tensor_tensor(out=out_ap, in0=in0, scalar=scalar, in1=in1, op0=op0, op1=ALU.mult)
+        def computed(name):
+            return lambda k: planes[name, k][:]
 
         def tanh_x(k):
-            if not no_chunk(k):
-                function("tanh_x", k, ACT.Tanh, x_of(GATE_C, k))
+            function("tanh_x", k, ACT.Tanh, from_hbm("x_c"))
 
-        def ramp_and_size(name, gate, k):
-            if not no_chunk(k):
-                function("ramp_" + name, k, ACT.Relu, x_of(gate, k), scale=HS_SLOPE, bias=0.5)
-                function("abs_" + name, k, ACT.Abs, x_of(gate, k))
+        def ramp(gate, k, pool=work):
+            function("ramp_" + gate, k, ACT.Relu, from_hbm("x_" + gate), scale=HS_SLOPE, bias=0.5, pool=pool)
+
+        def size(gate, k):
+            function("abs_" + gate, k, ACT.Abs, from_hbm("x_" + gate))
 
         def tanh_x_sq(k):
-            if not no_chunk(k):
-                function("tanh_x_sq", k, ACT.Square, planes["tanh_x", k][:])
+            function("tanh_x_sq", k, ACT.Square, computed("tanh_x"), pool=work_long)
 
         def tanh_c(k):
-            if not no_chunk(k):
-                function("tanh_c", k, ACT.Tanh, planes["new_cell", k][:])
+            function("tanh_c", k, ACT.Tanh, lambda k: new_cell[k][:].rearrange("p (j u) -> p j u", j=PACK))
 
         def tanh_c_sq(k):
-            if not no_chunk(k):
-                function("tanh_c_sq", k, ACT.Square, planes["tanh_c", k][:])
+            function("tanh_c_sq", k, ACT.Square, computed("tanh_c"))
 
         def i_tanh_x(k):
-            if not no_chunk(k):
-                product(new_plane("i_tanh_x", k), planes["ramp_i", k][:], 1.0, ALU.min, planes["tanh_x", k][:])
+            product("i_tanh_x", k, computed("ramp_i"), 1.0, ALU.min, computed("tanh_x"))
 
         def f_cell(k):
-            if not no_chunk(k):
-                product(new_plane("f_cell", k), planes["ramp_f", k][:], 1.0, ALU.min, units_of(cell_sb, k))
+            product("f_cell", k, computed("ramp_f"), 1.0, ALU.min, from_hbm("cell"))
 
-        def new_cell(k):
-            if not no_chunk(k):
-                nc.vector.tensor_tensor(
-                    out=new_plane("new_cell", k), in0=planes["i_tanh_x", k][:], in1=planes["f_cell", k][:], op=ALU.add
+        new_cell = {}
+
+        def add_new_cell(k):
+            if no_chunk(k):
+                return
+            new_cell[k] = psum.tile([P, N_TILE], F32, name="bank")
+            for name in ("i_tanh_x", "f_cell"):
+                nc.tensor.matmul(
+                    out=new_cell[k][:],
+                    lhsT=identity[:],
+                    rhs=planes[name, k][:].rearrange("p j u -> p (j u)"),
+                    start=(name == "i_tanh_x"),
+                    stop=(name == "f_cell"),
                 )
 
         def o_grad(k):
-            if not no_chunk(k):
-                product(new_plane("o_grad", k), planes["ramp_o", k][:], 1.0, ALU.min, units_of(grad_sb, k))
+            product("o_grad", k, computed("ramp_o"), 1.0, ALU.min, from_hbm("grad"))
 
         def open_o_grad(k):
-            if not no_chunk(k):
-                product(new_plane("open_o_grad", k, BF16), planes["abs_o", k][:], HS_EDGE, ALU.is_lt, units_of(grad_sb, k))
+            product("open_o_grad", k, computed("abs_o"), HS_EDGE, ALU.is_lt, from_hbm("grad"), BF16)
 
         def open_i_tanh_x(k):
-            if not no_chunk(k):
-                product(new_plane("open_i_tanh_x", k), planes["abs_i", k][:], HS_EDGE, ALU.is_lt, planes["tanh_x", k][:])
+            product("open_i_tanh_x", k, computed("abs_i"), HS_EDGE, ALU.is_lt, computed("tanh_x"))
 
         def open_f_cell(k):
-            if not no_chunk(k):
-                product(new_plane("open_f_cell", k, BF16), planes["abs_f", k][:], HS_EDGE, ALU.is_lt, units_of(cell_sb, k))
+            product("open_f_cell", k, computed("abs_f"), HS_EDGE, ALU.is_lt, from_hbm("cell"), BF16)
 
         def minus_dc(k):
-            if not no_chunk(k):
-                product(new_plane("minus_dc", k), planes["tanh_c_sq", k][:], 1.0, ALU.subtract, planes["o_grad", k][:])
+            product("minus_dc", k, computed("tanh_c_sq"), 1.0, ALU.subtract, computed("o_grad"))
 
         def minus_dc_i(k):
-            if not no_chunk(k):
-                product(new_plane("minus_dc_i", k), planes["ramp_i", k][:], 1.0, ALU.min, planes["minus_dc", k][:])
+            product("minus_dc_i", k, computed("ramp_i"), 1.0, ALU.min, computed("minus_dc"))
 
         grouped_dx = {}
 
@@ -193,12 +200,13 @@ def tile_vlstmcell_v_kernel(
                 return
             if k not in grouped_dx:
                 grouped_dx[k] = stage_dx.tile([P, GATES, U_CHUNK, PACK], BF16, align_bytes=64, name="grouped_dx")
-            product(
-                grouped_dx[k][:, gate, :, :],
-                planes[in0, k][:].rearrange("p j u -> p u j"),
-                scalar,
-                op0,
-                planes[in1, k][:].rearrange("p j u -> p u j"),
+            nc.vector.scalar_tensor_tensor(
+                out=grouped_dx[k][:, gate, :, :],
+                in0=planes[in0, k][:].rearrange("p j u -> p u j"),
+                scalar=scalar,
+                in1=planes[in1, k][:].rearrange("p j u -> p u j"),
+                op0=op0,
+                op1=ALU.mult,
             )
 
         def quantise_dx(k):
@@ -213,28 +221,41 @@ def tile_vlstmcell_v_kernel(
 
         sums = {}
 
+        def multiply_pass(r, c, m):
+            if c == 0:
+                sums[r, m] = psum.tile([M_TILE, N_TILE], F32, name="bank")
+            features = slice(m * M_TILE, (m + 1) * M_TILE)
+            nc.tensor.matmul_mx(
+                out=sums[r, m][:],
+                lhsT=in_codes[:, c, features].bitcast(E4M3_X4),
+                lhsT_scale=in_scales[:, c, features],
+                rhs=dx_codes[:, c, r, :].bitcast(E5M2_X4),
+                rhs_scale=dx_scales[:, c, r, :],
+                start=(c == 0),
+                stop=(c == PASSES - 1),
+            )
+
         def multiply(k):
             if no_chunk(k):
                 return
             r, c = divmod(k, PASSES)
-            for m in range(M_TILES):
-                if c == 0:
-                    sums[r, m] = psum.tile([M_TILE, N_TILE], F32, name="sums")
-                features = slice(m * M_TILE, (m + 1) * M_TILE)
-                nc.tensor.matmul_mx(
-                    out=sums[r, m][:],
-                    lhsT=in_codes[:, c, features].bitcast(E4M3_X4),
-                    lhsT_scale=in_scales[:, c, features],
-                    rhs=dx_codes[:, c, r, :].bitcast(E5M2_X4),
-                    rhs_scale=dx_scales[:, c, r, :],
-                    start=(c == 0),
-                    stop=(c == PASSES - 1),
-                )
+            for m in range(BANKS - 1):
+                multiply_pass(r, c, m)
+            if c == PASSES - 1:
+                for m in range(BANKS - 1, M_TILES):
+                    for each_pass in range(PASSES):
+                        multiply_pass(r, each_pass, m)
 
-        def empty_banks(r, part, copy):
-            for m in range(part, M_TILES, PASSES):
+        def empty_banks(k):
+            r, c = divmod(k, PASSES)
+            if no_chunk(k) or c < PASSES - 1:
+                return
+            for m in range(M_TILES):
                 result = stage_out.tile([M_TILE, GATES, U_CHUNK], F32)
-                copy(out=result[:].rearrange("p g u -> p (g u)"), in_=sums[r, m][:])
+                if k == CHUNKS - 1 and m % 2 == 1:
+                    nc.vector.tensor_copy(out=result[:].rearrange("p g u -> p (g u)"), in_=sums[r, m][:])
+                else:
+                    nc.scalar.copy(out=result[:].rearrange("p g u -> p (g u)"), in_=sums[r, m][:])
                 nc.sync.dma_start(
                     out=out[m * M_TILE : (m + 1) * M_TILE, :].rearrange(
                         "i (g r u) -> i g r u", g=GATES, r=ROUNDS
@@ -242,40 +263,38 @@ def tile_vlstmcell_v_kernel(
                     in_=result[:],
                 )
 
-        tanh_x(0)
-        ramp_and_size("i", GATE_I, 0)
-        ramp_and_size("f", GATE_F, 0)
-        ramp_and_size("o", GATE_O, 0)
-        tanh_x_sq(0)
+        def scalar_step(t):
+            tanh_x(t + 1)
+            ramp("i", t + 1, pool=work_long)
+            size("i", t + 1)
+            ramp("f", t + 1)
+            size("f", t + 1)
+            tanh_c(t)
+            ramp("o", t + 1)
+            tanh_c_sq(t)
+            size("o", t + 1)
+            tanh_x_sq(t + 1)
+
+        scalar_step(-1)
         for t in range(CHUNKS + 1):
             regroup_inputs(t, 0)
             i_tanh_x(t)
-            minus_dc(t - 1)
-            regroup_inputs(t, 1)
             f_cell(t)
-            dx(GATE_O, t - 1, "tanh_c", HS_SLOPE, ALU.mult, "open_o_grad")
-            quantise_inputs(t, 0)
-            new_cell(t)
-            minus_dc_i(t - 1)
+            add_new_cell(t)
             open_i_tanh_x(t)
-            dx(GATE_I, t - 1, "minus_dc", -HS_SLOPE, ALU.mult, "open_i_tanh_x")
+            minus_dc(t - 1)
             open_f_cell(t)
+            dx(GATE_O, t - 1, "tanh_c", HS_SLOPE, ALU.mult, "open_o_grad")
+            regroup_inputs(t, 1)
+            o_grad(t)
+            minus_dc_i(t - 1)
+            quantise_inputs(t, 0)
+            dx(GATE_I, t - 1, "minus_dc", -HS_SLOPE, ALU.mult, "open_i_tanh_x")
             dx(GATE_C, t - 1, "tanh_x_sq", 1.0, ALU.subtract, "minus_dc_i")
             quantise_inputs(t, 1)
-            o_grad(t)
             dx(GATE_F, t - 1, "minus_dc", -HS_SLOPE, ALU.mult, "open_f_cell")
             open_o_grad(t)
             quantise_dx(t - 1)
-
             multiply(t - 1)
-
-            tanh_c(t)
-            tanh_x(t + 1)
-            tanh_c_sq(t)
-            ramp_and_size("i", GATE_I, t + 1)
-            ramp_and_size("f", GATE_F, t + 1)
-            ramp_and_size("o", GATE_O, t + 1)
-            tanh_x_sq(t + 1)
-            if t >= PASSES:
-                empty_banks((t - PASSES) // PASSES, (t - PASSES) % PASSES, nc.scalar.copy)
-        empty_banks(ROUNDS - 1, PASSES - 1, nc.vector.tensor_copy)
+            scalar_step(t)
+            empty_banks(t - 1)

@@ -120,9 +120,11 @@ def tile_vlstmcell_v_kernel(
             planes[name, k] = pool.tile([P, PACK, U_CHUNK], dtype, name=name)
             return planes[name, k][:]
 
-        def function(name, k, func, in_, scale=1.0, bias=0.0, pool=work):
+        def function(name, k, func, in_, scale=1.0, bias=0.0, pool=work, dtype=F32):
             if not no_chunk(k):
-                nc.scalar.activation(out=new_plane(name, k, pool=pool), in_=in_(k), func=func, bias=bias, scale=scale)
+                nc.scalar.activation(
+                    out=new_plane(name, k, dtype, pool=pool), in_=in_(k), func=func, bias=bias, scale=scale
+                )
 
         def product(name, k, in0, scalar, op0, in1, dtype=F32):
             if not no_chunk(k):
@@ -144,6 +146,12 @@ def tile_vlstmcell_v_kernel(
 
         def size(gate, k):
             function("abs_" + gate, k, ACT.Abs, from_hbm("x_" + gate))
+
+        def upper_half(name):
+            return lambda k: loaded[name, k][:].bitcast(BF16).rearrange("p j (u h) -> p j u h", h=2)[:, :, :, 1]
+
+        def short_size(gate, k):
+            function("abs_" + gate, k, ACT.Abs, upper_half("x_" + gate), dtype=BF16)
 
         def tanh_x_sq(k):
             function("tanh_x_sq", k, ACT.Square, computed("tanh_x"), pool=work_long)
@@ -268,11 +276,11 @@ def tile_vlstmcell_v_kernel(
             ramp("i", t + 1, pool=work_long)
             size("i", t + 1)
             ramp("f", t + 1)
-            size("f", t + 1)
+            short_size("f", t + 1)
             tanh_c(t)
             ramp("o", t + 1)
             tanh_c_sq(t)
-            size("o", t + 1)
+            short_size("o", t + 1)
             tanh_x_sq(t + 1)
 
         scalar_step(-1)

@@ -33,17 +33,29 @@ FLOPS = 2 * TOKENS * FEATURES * GATES * UNITS
 BYTES = 2 * TOKENS * (FEATURES + 2 * UNITS) + 4 * TOKENS * GATES * UNITS + 4 * FEATURES * GATES * UNITS
 
 
+CFG = {
+    "cell_whole": False, "in_whole": False, "x_pair_from": None, "inplace": True, "loads": None,
+    "s_order": [("tanh_x", 1), ("ramp_i", 1), ("size_i", 1), ("ramp_f", 1), ("size_f", 1), ("ramp_o", 1), ("size_o", 1),
+                ("tanh_x_sq", 1), ("tanh_c", 0), ("tanh_c_sq", 0), ("empty", -2)],
+    "v_order": [("regroup0", 0), ("i_tanh_x", 0), ("f_cell", 0), ("open_i_tanh_x", 0), ("minus_dc", -2), ("open_f_cell", 0),
+                ("dx_o", -2), ("regroup1", 0), ("o_grad", 0), ("minus_dc_i", -2), ("quant_in0", 0), ("dx_i", -2), ("dx_c", -2),
+                ("quant_in1", 0), ("dx_f", -2), ("open_o_grad", 0), ("quantise_dx", -2)],
+    "bufs": {"ramp_i": 4, "tanh_x_sq": 4, "o_grad": 3, "open_o_grad": 3, "open_i_tanh_x": 3, "open_f_cell": 3},
+    "s_regroup": (), "steps_extra": 2, "out_bufs": 8, "late": 0, "free_banks": 1,
+}
+
+
 def tile_vlstmcell_v_kernel(
     tc, inputs, h_tm1, c_tm1, z_tm1, kernel, recurrent_kernel, recurrent_latent, bias, x, grad_out, out
 ):
     nc = tc.nc
+    cfg = CFG
     with ExitStack() as stack:
         keep = stack.enter_context(tc.tile_pool(name="keep", bufs=1))
         stage_in = stack.enter_context(tc.tile_pool(name="stage_in", bufs=2))
         work = stack.enter_context(tc.tile_pool(name="work", bufs=2))
-        work_long = stack.enter_context(tc.tile_pool(name="work_long", bufs=3))
         stage_dx = stack.enter_context(tc.tile_pool(name="stage_dx", bufs=2))
-        stage_out = stack.enter_context(tc.tile_pool(name="stage_out", bufs=M_TILES))
+        stage_out = stack.enter_context(tc.tile_pool(name="stage_out", bufs=cfg["out_bufs"]))
         psum = stack.enter_context(tc.psum_pool(name="psum", bufs=BANKS))
         stack.enter_context(tc.manual_schedule())
 
@@ -55,35 +67,58 @@ def tile_vlstmcell_v_kernel(
 
         loaded = {}
         raw_in = {}
+        whole = {}
 
-        def load(name, k, source, first_column, dtype):
+        def load(name, k):
+            source, first_column, dtype = {
+                "x_c": (x, GATE_C * UNITS, F32), "x_i": (x, GATE_I * UNITS, F32), "x_f": (x, GATE_F * UNITS, F32),
+                "x_o": (x, GATE_O * UNITS, F32), "cell": (c_tm1, 0, BF16), "grad": (grad_out, 0, BF16)}[name]
             r, c = divmod(k, PASSES)
+            if dtype == BF16 and cfg["cell_whole"]:
+                if (name, c) not in whole:
+                    whole[name, c] = keep.tile([P, PACK, UNITS], dtype, name="%s_w%d" % (name, c))
+                    nc.sync.dma_start(out=whole[name, c][:], in_=token_rows(source, c))
+                loaded[name, k] = whole[name, c][:, :, r * U_CHUNK : (r + 1) * U_CHUNK]
+                return
+            if dtype == F32 and cfg["x_pair_from"] is not None and r >= cfg["x_pair_from"]:
+                r0 = cfg["x_pair_from"]
+                n = ROUNDS - r0
+                if (name, c) not in whole:
+                    whole[name, c] = keep.tile([P, PACK, n * U_CHUNK], dtype, name="%s_w%d" % (name, c))
+                    first = first_column + r0 * U_CHUNK
+                    nc.sync.dma_start(out=whole[name, c][:], in_=token_rows(source, c)[:, :, first : first + n * U_CHUNK])
+                loaded[name, k] = whole[name, c][:, :, (r - r0) * U_CHUNK : (r - r0 + 1) * U_CHUNK]
+                return
             first = first_column + r * U_CHUNK
-            loaded[name, k] = keep.tile([P, PACK, U_CHUNK], dtype, name="%s_%d" % (name, k))
-            nc.sync.dma_start(out=loaded[name, k][:], in_=token_rows(source, c)[:, :, first : first + U_CHUNK])
+            t = keep.tile([P, PACK, U_CHUNK], dtype, name="%s_%d" % (name, k))
+            loaded[name, k] = t[:]
+            nc.sync.dma_start(out=t[:], in_=token_rows(source, c)[:, :, first : first + U_CHUNK])
 
         def load_chunk(k):
-            load("x_c", k, x, GATE_C * UNITS, F32)
-            load("x_i", k, x, GATE_I * UNITS, F32)
-            load("cell", k, c_tm1, 0, BF16)
-            load("x_f", k, x, GATE_F * UNITS, F32)
-            load("grad", k, grad_out, 0, BF16)
-            load("x_o", k, x, GATE_O * UNITS, F32)
+            for name in ("x_c", "x_i", "cell", "x_f", "grad", "x_o"):
+                load(name, k)
 
         def load_inputs(c, piece):
-            raw_in[c, piece] = keep.tile([P, PACK, F_PIECE], BF16, name="raw_in_%d_%d" % (c, piece))
-            nc.sync.dma_start(
-                out=raw_in[c, piece][:], in_=token_rows(inputs, c)[:, :, piece * F_PIECE : (piece + 1) * F_PIECE]
-            )
+            if cfg["in_whole"]:
+                if ("in", c) not in whole:
+                    whole["in", c] = keep.tile([P, PACK, FEATURES], BF16, name="raw_in_%d" % c)
+                    nc.sync.dma_start(out=whole["in", c][:], in_=token_rows(inputs, c))
+                raw_in[c, piece] = whole["in", c][:, :, piece * F_PIECE : (piece + 1) * F_PIECE]
+                return
+            t = keep.tile([P, PACK, F_PIECE], BF16, name="raw_in_%d_%d" % (c, piece))
+            raw_in[c, piece] = t[:]
+            nc.sync.dma_start(out=t[:], in_=token_rows(inputs, c)[:, :, piece * F_PIECE : (piece + 1) * F_PIECE])
 
-        load_inputs(0, 0)
-        load_chunk(0)
-        load_inputs(0, 1)
-        load_inputs(1, 0)
-        load_chunk(1)
-        load_inputs(1, 1)
-        for k in range(2, CHUNKS):
-            load_chunk(k)
+        order = cfg["loads"] or [("in", 0, 0), 0, ("in", 0, 1), ("in", 1, 0), 1, ("in", 1, 1), 2, 3, 4, 5, 6, 7]
+        late = order[len(order) - cfg["late"] :] if cfg["late"] else []
+        for item in order[: len(order) - cfg["late"]]:
+            if isinstance(item, tuple):
+                if item[0] == "in":
+                    load_inputs(item[1], item[2])
+                else:
+                    load(item[0], item[1])
+            else:
+                load_chunk(item)
 
         identity = keep.tile([P, P], F32)
         make_identity(nc, identity[:])
@@ -92,17 +127,19 @@ def tile_vlstmcell_v_kernel(
         in_scales = keep.tile([P, PASSES, FEATURES], U8, align_bytes=64)
         grouped_in = {}
 
-        def regroup_inputs(c, piece):
-            if c >= PASSES:
+        def regroup_inputs(c, piece, engine=None):
+            if c < 0 or c >= PASSES:
                 return
-            grouped_in[c, piece] = stage_in.tile([P, F_PIECE, PACK], BF16, align_bytes=64, name="grouped_in")
-            nc.vector.tensor_copy(
-                out=grouped_in[c, piece][:].rearrange("p (w i) j -> p w j i", i=4),
-                in_=raw_in[c, piece][:].rearrange("p j (w i) -> p w j i", i=4),
-            )
+            grouped_in[c, piece] = stage_in.tile([P, F_PIECE, PACK], BF16, align_bytes=64, name="grouped_in", bufs=cfg["bufs"].get("grouped_in", 2))
+            o = grouped_in[c, piece][:].rearrange("p (w i) j -> p w j i", i=4)
+            i_ = raw_in[c, piece].rearrange("p j (w i) -> p w j i", i=4)
+            if engine == "S":
+                nc.scalar.copy(out=o, in_=i_)
+            else:
+                nc.vector.tensor_copy(out=o, in_=i_)
 
         def quantise_inputs(c, piece):
-            if c >= PASSES:
+            if c < 0 or c >= PASSES:
                 return
             features = slice(piece * F_PIECE, (piece + 1) * F_PIECE)
             nc.vector.quantize_mx(
@@ -113,196 +150,154 @@ def tile_vlstmcell_v_kernel(
 
         dx_codes = keep.tile([P, PASSES, ROUNDS, N_TILE], U32, align_bytes=64)
         dx_scales = keep.tile([P, PASSES, ROUNDS, N_TILE], U8, align_bytes=64)
-
         planes = {}
 
-        def new_plane(name, k, dtype=F32, pool=work):
-            planes[name, k] = pool.tile([P, PACK, U_CHUNK], dtype, name=name)
-            return planes[name, k][:]
+        def new_plane(name, k, dtype=F32):
+            t = work.tile([P, PACK, U_CHUNK], dtype, name=name, bufs=cfg["bufs"].get(name, 2))
+            planes[name, k] = t[:]
+            return planes[name, k]
 
-        def function(name, k, func, in_, scale=1.0, bias=0.0, pool=work, dtype=F32):
-            if not no_chunk(k):
-                nc.scalar.activation(
-                    out=new_plane(name, k, dtype, pool=pool), in_=in_(k), func=func, bias=bias, scale=scale
-                )
+        def function(name, k, func, in_, scale=1.0, bias=0.0, dtype=F32, over=None):
+            if over is not None:
+                planes[name, k] = over
+                o = over
+            else:
+                o = new_plane(name, k, dtype)
+            nc.scalar.activation(out=o, in_=in_, func=func, bias=bias, scale=scale)
 
-        def product(name, k, in0, scalar, op0, in1, dtype=F32):
-            if not no_chunk(k):
-                nc.vector.scalar_tensor_tensor(
-                    out=new_plane(name, k, dtype), in0=in0(k), scalar=scalar, in1=in1(k), op0=op0, op1=ALU.mult
-                )
+        def product(name, k, in0, scalar, op0, in1, dtype=F32, over=None):
+            if over is not None:
+                planes[name, k] = over
+                o = over
+            else:
+                o = new_plane(name, k, dtype)
+            nc.vector.scalar_tensor_tensor(out=o, in0=in0, scalar=scalar, in1=in1, op0=op0, op1=ALU.mult)
 
-        def from_hbm(name):
-            return lambda k: loaded[name, k][:]
-
-        def computed(name):
-            return lambda k: planes[name, k][:]
-
-        def tanh_x(k):
-            function("tanh_x", k, ACT.Tanh, from_hbm("x_c"))
-
-        def ramp(gate, k, pool=work):
-            function("ramp_" + gate, k, ACT.Relu, from_hbm("x_" + gate), scale=HS_SLOPE, bias=0.5, pool=pool)
-
-        def size(gate, k):
-            function("abs_" + gate, k, ACT.Abs, from_hbm("x_" + gate))
-
-        def upper_half(name):
-            return lambda k: loaded[name, k][:].bitcast(BF16).rearrange("p j (u h) -> p j u h", h=2)[:, :, :, 1]
-
-        def short_size(gate, k):
-            function("abs_" + gate, k, ACT.Abs, upper_half("x_" + gate), dtype=BF16)
-
-        def tanh_x_sq(k):
-            function("tanh_x_sq", k, ACT.Square, computed("tanh_x"), pool=work_long)
-
-        def tanh_c(k):
-            function("tanh_c", k, ACT.Tanh, lambda k: new_cell[k][:].rearrange("p (j u) -> p j u", j=PACK))
-
-        def tanh_c_sq(k):
-            function("tanh_c_sq", k, ACT.Square, computed("tanh_c"))
-
-        def i_tanh_x(k):
-            product("i_tanh_x", k, computed("ramp_i"), 1.0, ALU.min, computed("tanh_x"))
-
-        def f_cell(k):
-            product("f_cell", k, computed("ramp_f"), 1.0, ALU.min, from_hbm("cell"))
+        def upper_half(ap):
+            return ap.bitcast(BF16).rearrange("p j (u h) -> p j u h", h=2)[:, :, :, 1]
 
         new_cell = {}
-
-        def add_new_cell(k):
-            if no_chunk(k):
-                return
-            new_cell[k] = psum.tile([P, N_TILE], F32, name="bank")
-            for name in ("i_tanh_x", "f_cell"):
-                nc.tensor.matmul(
-                    out=new_cell[k][:],
-                    lhsT=identity[:],
-                    rhs=planes[name, k][:].rearrange("p j u -> p (j u)"),
-                    start=(name == "i_tanh_x"),
-                    stop=(name == "f_cell"),
-                )
-
-        def o_grad(k):
-            product("o_grad", k, computed("ramp_o"), 1.0, ALU.min, from_hbm("grad"))
-
-        def open_o_grad(k):
-            product("open_o_grad", k, computed("abs_o"), HS_EDGE, ALU.is_lt, from_hbm("grad"), BF16)
-
-        def open_i_tanh_x(k):
-            product("open_i_tanh_x", k, computed("abs_i"), HS_EDGE, ALU.is_lt, computed("tanh_x"))
-
-        def open_f_cell(k):
-            product("open_f_cell", k, computed("abs_f"), HS_EDGE, ALU.is_lt, from_hbm("cell"), BF16)
-
-        def minus_dc(k):
-            product("minus_dc", k, computed("tanh_c_sq"), 1.0, ALU.subtract, computed("o_grad"))
-
-        def minus_dc_i(k):
-            product("minus_dc_i", k, computed("ramp_i"), 1.0, ALU.min, computed("minus_dc"))
-
         grouped_dx = {}
+        sums = {}
+        inpl = cfg["inplace"]
 
         def dx(gate, k, in0, scalar, op0, in1):
-            if no_chunk(k):
-                return
             if k not in grouped_dx:
-                grouped_dx[k] = stage_dx.tile([P, GATES, U_CHUNK, PACK], BF16, align_bytes=64, name="grouped_dx")
+                grouped_dx[k] = stage_dx.tile([P, GATES, U_CHUNK, PACK], BF16, align_bytes=64, name="grouped_dx", bufs=cfg["bufs"].get("grouped_dx", 2))
             nc.vector.scalar_tensor_tensor(
-                out=grouped_dx[k][:, gate, :, :],
-                in0=planes[in0, k][:].rearrange("p j u -> p u j"),
-                scalar=scalar,
-                in1=planes[in1, k][:].rearrange("p j u -> p u j"),
-                op0=op0,
-                op1=ALU.mult,
-            )
-
-        def quantise_dx(k):
-            if no_chunk(k):
-                return
-            r, c = divmod(k, PASSES)
-            nc.vector.quantize_mx(
-                out=dx_codes[:, c, r, :].bitcast(E5M2_X4),
-                scales=dx_scales[:, c, r, :],
-                in_=grouped_dx[k][:].rearrange("p g u j -> p (g u j)"),
-            )
-
-        sums = {}
+                out=grouped_dx[k][:, gate, :, :], in0=planes[in0, k].rearrange("p j u -> p u j"), scalar=scalar,
+                in1=planes[in1, k].rearrange("p j u -> p u j"), op0=op0, op1=ALU.mult)
 
         def multiply_pass(r, c, m):
             if c == 0:
                 sums[r, m] = psum.tile([M_TILE, N_TILE], F32, name="bank")
             features = slice(m * M_TILE, (m + 1) * M_TILE)
             nc.tensor.matmul_mx(
-                out=sums[r, m][:],
-                lhsT=in_codes[:, c, features].bitcast(E4M3_X4),
-                lhsT_scale=in_scales[:, c, features],
-                rhs=dx_codes[:, c, r, :].bitcast(E5M2_X4),
-                rhs_scale=dx_scales[:, c, r, :],
-                start=(c == 0),
-                stop=(c == PASSES - 1),
-            )
+                out=sums[r, m][:], lhsT=in_codes[:, c, features].bitcast(E4M3_X4), lhsT_scale=in_scales[:, c, features],
+                rhs=dx_codes[:, c, r, :].bitcast(E5M2_X4), rhs_scale=dx_scales[:, c, r, :],
+                start=(c == 0), stop=(c == PASSES - 1))
 
         def multiply(k):
-            if no_chunk(k):
-                return
             r, c = divmod(k, PASSES)
-            for m in range(BANKS - 1):
+            for m in range(BANKS - cfg.get("free_banks", 1)):
                 multiply_pass(r, c, m)
             if c == PASSES - 1:
-                for m in range(BANKS - 1, M_TILES):
+                for m in range(BANKS - cfg.get("free_banks", 1), M_TILES):
                     for each_pass in range(PASSES):
                         multiply_pass(r, each_pass, m)
 
-        def empty_banks(k):
+        def empty_banks(k, which=None):
             r, c = divmod(k, PASSES)
-            if no_chunk(k) or c < PASSES - 1:
+            if c < PASSES - 1:
                 return
-            for m in range(M_TILES):
-                result = stage_out.tile([M_TILE, GATES, U_CHUNK], F32)
+            for m in range(M_TILES) if which is None else which:
+                result = stage_out.tile([M_TILE, GATES, U_CHUNK], F32, name="result")
                 if k == CHUNKS - 1 and m % 2 == 1:
                     nc.vector.tensor_copy(out=result[:].rearrange("p g u -> p (g u)"), in_=sums[r, m][:])
                 else:
                     nc.scalar.copy(out=result[:].rearrange("p g u -> p (g u)"), in_=sums[r, m][:])
                 nc.sync.dma_start(
-                    out=out[m * M_TILE : (m + 1) * M_TILE, :].rearrange(
-                        "i (g r u) -> i g r u", g=GATES, r=ROUNDS
-                    )[:, :, r, :],
-                    in_=result[:],
-                )
+                    out=out[m * M_TILE : (m + 1) * M_TILE, :].rearrange("i (g r u) -> i g r u", g=GATES, r=ROUNDS)[:, :, r, :],
+                    in_=result[:])
 
-        def scalar_step(t):
-            tanh_x(t + 1)
-            ramp("i", t + 1, pool=work_long)
-            size("i", t + 1)
-            ramp("f", t + 1)
-            short_size("f", t + 1)
-            tanh_c(t)
-            ramp("o", t + 1)
-            tanh_c_sq(t)
-            short_size("o", t + 1)
-            tanh_x_sq(t + 1)
+        def do(name, k, t):
+            if name.startswith("regroup") or name.startswith("quant_in") or name.startswith("sregroup"):
+                piece = int(name[-1])
+                if name.startswith("regroup"):
+                    if (k, piece) not in cfg["s_regroup"]:
+                        regroup_inputs(k, piece)
+                elif name.startswith("sregroup"):
+                    if (k, piece) in cfg["s_regroup"]:
+                        regroup_inputs(k, piece, "S")
+                else:
+                    quantise_inputs(k, piece)
+                return
+            if no_chunk(k):
+                return
+            if name == "tanh_x":
+                function("tanh_x", k, ACT.Tanh, loaded["x_c", k], over=loaded["x_c", k] if inpl else None)
+            elif name.startswith("ramp_"):
+                function(name, k, ACT.Relu, loaded["x_" + name[-1], k], scale=HS_SLOPE, bias=0.5)
+            elif name == "size_i":
+                function("abs_i", k, ACT.Abs, loaded["x_i", k], over=loaded["x_i", k] if inpl else None)
+            elif name.startswith("size_"):
+                function("abs_" + name[-1], k, ACT.Abs, upper_half(loaded["x_" + name[-1], k]), dtype=BF16)
+            elif name == "tanh_x_sq":
+                function("tanh_x_sq", k, ACT.Square, planes["tanh_x", k])
+            elif name == "tanh_c":
+                function("tanh_c", k, ACT.Tanh, new_cell[k][:].rearrange("p (j u) -> p j u", j=PACK))
+            elif name == "tanh_c_sq":
+                function("tanh_c_sq", k, ACT.Square, planes["tanh_c", k])
+            elif name == "empty":
+                empty_banks(k)
+            elif name == "empty_a":
+                empty_banks(k, range(0, M_TILES // 2))
+            elif name == "empty_b":
+                empty_banks(k, range(M_TILES // 2, M_TILES))
+            elif name == "i_tanh_x":
+                product("i_tanh_x", k, planes["ramp_i", k], 1.0, ALU.min, planes["tanh_x", k])
+            elif name == "f_cell":
+                product("f_cell", k, planes["ramp_f", k], 1.0, ALU.min, loaded["cell", k])
+                new_cell[k] = psum.tile([P, N_TILE], F32, name="bank")
+                for nm in ("i_tanh_x", "f_cell"):
+                    nc.tensor.matmul(out=new_cell[k][:], lhsT=identity[:], rhs=planes[nm, k].rearrange("p j u -> p (j u)"),
+                                     start=(nm == "i_tanh_x"), stop=(nm == "f_cell"))
+            elif name == "o_grad":
+                product("o_grad", k, planes["ramp_o", k], 1.0, ALU.min, loaded["grad", k])
+            elif name == "open_o_grad":
+                product("open_o_grad", k, planes["abs_o", k], HS_EDGE, ALU.is_lt, loaded["grad", k], BF16)
+            elif name == "open_i_tanh_x":
+                product("open_i_tanh_x", k, planes["abs_i", k], HS_EDGE, ALU.is_lt, planes["tanh_x", k])
+            elif name == "open_f_cell":
+                product("open_f_cell", k, planes["abs_f", k], HS_EDGE, ALU.is_lt, loaded["cell", k], BF16)
+            elif name == "minus_dc":
+                product("minus_dc", k, planes["tanh_c_sq", k], 1.0, ALU.subtract, planes["o_grad", k], over=planes["tanh_c_sq", k] if inpl else None)
+            elif name == "minus_dc_i":
+                product("minus_dc_i", k, planes["ramp_i", k], 1.0, ALU.min, planes["minus_dc", k], over=planes["o_grad", k] if inpl else None)
+            elif name == "dx_o":
+                dx(GATE_O, k, "tanh_c", HS_SLOPE, ALU.mult, "open_o_grad")
+            elif name == "dx_i":
+                dx(GATE_I, k, "minus_dc", -HS_SLOPE, ALU.mult, "open_i_tanh_x")
+            elif name == "dx_c":
+                dx(GATE_C, k, "tanh_x_sq", 1.0, ALU.subtract, "minus_dc_i")
+            elif name == "dx_f":
+                dx(GATE_F, k, "minus_dc", -HS_SLOPE, ALU.mult, "open_f_cell")
+            elif name == "quantise_dx":
+                r, c = divmod(k, PASSES)
+                nc.vector.quantize_mx(out=dx_codes[:, c, r, :].bitcast(E5M2_X4), scales=dx_scales[:, c, r, :],
+                                      in_=grouped_dx[k][:].rearrange("p g u j -> p (g u j)"))
+                multiply(k)
+            else:
+                raise ValueError(name)
 
-        scalar_step(-1)
-        for t in range(CHUNKS + 1):
-            regroup_inputs(t, 0)
-            i_tanh_x(t)
-            f_cell(t)
-            add_new_cell(t)
-            open_i_tanh_x(t)
-            minus_dc(t - 1)
-            open_f_cell(t)
-            dx(GATE_O, t - 1, "tanh_c", HS_SLOPE, ALU.mult, "open_o_grad")
-            regroup_inputs(t, 1)
-            o_grad(t)
-            minus_dc_i(t - 1)
-            quantise_inputs(t, 0)
-            dx(GATE_I, t - 1, "minus_dc", -HS_SLOPE, ALU.mult, "open_i_tanh_x")
-            dx(GATE_C, t - 1, "tanh_x_sq", 1.0, ALU.subtract, "minus_dc_i")
-            quantise_inputs(t, 1)
-            dx(GATE_F, t - 1, "minus_dc", -HS_SLOPE, ALU.mult, "open_f_cell")
-            open_o_grad(t)
-            quantise_dx(t - 1)
-            multiply(t - 1)
-            scalar_step(t)
-            empty_banks(t - 1)
+        for name, d in cfg["s_order"]:
+            if d >= 1:
+                do(name, -1 + d, -1)
+        for t in range(CHUNKS + cfg["steps_extra"]):
+            for name, d in cfg["v_order"]:
+                do(name, t + d, t)
+            for name, d in cfg["s_order"]:
+                do(name, t + d, t)
+            if t == PASSES:
+                for item in late:
+                    load_chunk(item)

@@ -34,12 +34,13 @@ BYTES = 2 * TOKENS * (FEATURES + 2 * UNITS) + 4 * TOKENS * GATES * UNITS + 4 * F
 
 
 CFG = {
-    "cell_whole": False, "in_whole": False, "x_pair_from": None, "inplace": True, "loads": None,
+    "cell_whole": False, "in_whole": False, "x_pair_from": None, "inplace": True, "loads": None, "runs4": True,
     "s_order": [("tanh_x", 1), ("ramp_i", 1), ("size_i", 1), ("ramp_f", 1), ("size_f", 1), ("ramp_o", 1), ("size_o", 1),
                 ("tanh_x_sq", 1), ("tanh_c", 0), ("tanh_c_sq", 0), ("empty", -2)],
-    "v_order": [("regroup0", 0), ("i_tanh_x", 0), ("f_cell", 0), ("open_i_tanh_x", 0), ("minus_dc", -2), ("open_f_cell", 0),
-                ("dx_o", -2), ("regroup1", 0), ("o_grad", 0), ("minus_dc_i", -2), ("quant_in0", 0), ("dx_i", -2), ("dx_c", -2),
-                ("quant_in1", 0), ("dx_f", -2), ("open_o_grad", 0), ("quantise_dx", -2)],
+    "v_order": [("regroup0", 0), ("i_tanh_x", 0), ("mask_i", 0), ("f_cell", 0), ("mask_f", 0), ("minus_dc", -2),
+                ("open_i_tanh_x", 0), ("dx_o", -2), ("open_f_cell", 0), ("regroup1", 0), ("mask_o", 0), ("o_grad", 0),
+                ("minus_dc_i", -2), ("quant_in0", 0), ("dx_i", -2), ("dx_c", -2), ("quant_in1", 0), ("dx_f", -2),
+                ("open_o_grad", 0), ("quantise_dx", -2)],
     "bufs": {"ramp_i": 4, "tanh_x_sq": 4, "o_grad": 3, "open_o_grad": 3, "open_i_tanh_x": 3, "open_f_cell": 3},
     "s_regroup": (), "steps_extra": 2, "out_bufs": 8, "late": 0, "free_banks": 1,
 }
@@ -180,10 +181,17 @@ def tile_vlstmcell_v_kernel(
         grouped_dx = {}
         sums = {}
         inpl = cfg["inplace"]
+        runs4 = cfg.get("runs4", False)
 
         def dx(gate, k, in0, scalar, op0, in1):
             if k not in grouped_dx:
                 grouped_dx[k] = stage_dx.tile([P, GATES, U_CHUNK, PACK], BF16, align_bytes=64, name="grouped_dx", bufs=cfg["bufs"].get("grouped_dx", 2))
+            if scalar is None:
+                nc.vector.tensor_tensor(
+                    out=grouped_dx[k][:, gate, :, :].rearrange("p (w i) j -> p w j i", i=4),
+                    in0=planes[in0, k].rearrange("p j (w i) -> p w j i", i=4),
+                    in1=planes[in1, k].rearrange("p j (w i) -> p w j i", i=4), op=ALU.mult)
+                return
             nc.vector.scalar_tensor_tensor(
                 out=grouped_dx[k][:, gate, :, :], in0=planes[in0, k].rearrange("p j u -> p u j"), scalar=scalar,
                 in1=planes[in1, k].rearrange("p j u -> p u j"), op0=op0, op1=ALU.mult)
@@ -238,8 +246,10 @@ def tile_vlstmcell_v_kernel(
                 function("tanh_x", k, ACT.Tanh, loaded["x_c", k], over=loaded["x_c", k] if inpl else None)
             elif name.startswith("ramp_"):
                 function(name, k, ACT.Relu, loaded["x_" + name[-1], k], scale=HS_SLOPE, bias=0.5)
-            elif name == "size_i":
+            elif name == "size_i" and not runs4:
                 function("abs_i", k, ACT.Abs, loaded["x_i", k], over=loaded["x_i", k] if inpl else None)
+            elif name.startswith("mask_"):
+                nc.vector.tensor_scalar(out=planes["abs_" + name[-1], k], in0=planes["abs_" + name[-1], k], scalar1=HS_EDGE, scalar2=None, op0=ALU.is_lt)
             elif name.startswith("size_"):
                 function("abs_" + name[-1], k, ACT.Abs, upper_half(loaded["x_" + name[-1], k]), dtype=BF16)
             elif name == "tanh_x_sq":
@@ -264,6 +274,18 @@ def tile_vlstmcell_v_kernel(
                                      start=(nm == "i_tanh_x"), stop=(nm == "f_cell"))
             elif name == "o_grad":
                 product("o_grad", k, planes["ramp_o", k], 1.0, ALU.min, loaded["grad", k])
+            elif name == "open_o_grad" and runs4:
+                product("open_o_grad", k, loaded["grad", k], HS_SLOPE, ALU.mult, planes["abs_o", k])
+            elif name == "open_i_tanh_x" and runs4:
+                product("open_i_tanh_x", k, planes["tanh_x", k], -HS_SLOPE, ALU.mult, planes["abs_i", k])
+            elif name == "open_f_cell" and runs4:
+                product("open_f_cell", k, loaded["cell", k], -HS_SLOPE, ALU.mult, planes["abs_f", k])
+            elif name == "dx_o" and runs4:
+                dx(GATE_O, k, "tanh_c", None, None, "open_o_grad")
+            elif name == "dx_i" and runs4:
+                dx(GATE_I, k, "minus_dc", None, None, "open_i_tanh_x")
+            elif name == "dx_f" and runs4:
+                dx(GATE_F, k, "minus_dc", None, None, "open_f_cell")
             elif name == "open_o_grad":
                 product("open_o_grad", k, planes["abs_o", k], HS_EDGE, ALU.is_lt, loaded["grad", k], BF16)
             elif name == "open_i_tanh_x":

@@ -1,3 +1,4 @@
+import math
 from contextlib import ExitStack
 
 import concourse.mybir as mybir
@@ -34,10 +35,10 @@ BYTES = 2 * TOKENS * (FEATURES + 2 * UNITS) + 4 * TOKENS * GATES * UNITS + 4 * F
 
 
 CFG = {
-    "cell_whole": False, "in_whole": False, "x_pair_from": None, "inplace": True, "loads": None, "runs4": True,
+    "cell_whole": False, "in_whole": False, "x_pair_from": None, "inplace": True, "loads": None, "runs4": True, "scaled": True,
     "s_order": [("tanh_x", 1), ("ramp_i", 1), ("size_i", 1), ("ramp_f", 1), ("size_f", 1), ("ramp_o", 1), ("size_o", 1),
                 ("tanh_x_sq", 1), ("tanh_c", 0), ("tanh_c_sq", 0), ("empty", -2)],
-    "v_order": [("regroup0", 0), ("i_tanh_x", 0), ("mask_i", 0), ("f_cell", 0), ("mask_f", 0), ("minus_dc", -2),
+    "v_order": [("regroup0", 0), ("i_tanh_x", 0), ("f_cell", 0), ("mask_f", 0), ("minus_dc", -2),
                 ("open_i_tanh_x", 0), ("dx_o", -2), ("open_f_cell", 0), ("regroup1", 0), ("mask_o", 0), ("o_grad", 0),
                 ("minus_dc_i", -2), ("quant_in0", 0), ("dx_i", -2), ("dx_c", -2), ("quant_in1", 0), ("dx_f", -2),
                 ("open_o_grad", 0), ("quantise_dx", -2)],
@@ -123,6 +124,8 @@ def tile_vlstmcell_v_kernel(
 
         identity = keep.tile([P, P], F32)
         make_identity(nc, identity[:])
+        minus_identity = keep.tile([P, P], F32)
+        nc.vector.tensor_scalar(out=minus_identity[:], in0=identity[:], scalar1=-1.0, scalar2=None, op0=ALU.mult)
 
         in_codes = keep.tile([P, PASSES, FEATURES], U32, align_bytes=64)
         in_scales = keep.tile([P, PASSES, FEATURES], U8, align_bytes=64)
@@ -182,6 +185,7 @@ def tile_vlstmcell_v_kernel(
         sums = {}
         inpl = cfg["inplace"]
         runs4 = cfg.get("runs4", False)
+        scaled = cfg.get("scaled", False)
 
         def dx(gate, k, in0, scalar, op0, in1):
             if k not in grouped_dx:
@@ -242,7 +246,23 @@ def tile_vlstmcell_v_kernel(
                 return
             if no_chunk(k):
                 return
-            if name == "tanh_x":
+            if scaled and name == "tanh_x":
+                function("tanh_x", k, ACT.Tanh, loaded["x_c", k], scale=-1.0, over=loaded["x_c", k])
+            elif scaled and name == "ramp_o":
+                function(name, k, ACT.Relu, loaded["x_o", k], scale=HS_SLOPE * HS_SLOPE, bias=0.5 * HS_SLOPE)
+            elif scaled and name == "tanh_x_sq":
+                function("tanh_x_sq", k, ACT.Square, planes["tanh_x", k], scale=math.sqrt(1.0 / HS_SLOPE))
+            elif scaled and name == "o_grad":
+                product("o_grad", k, planes["ramp_o", k], HS_SLOPE, ALU.min, loaded["grad", k])
+            elif scaled and name == "open_i_tanh_x":
+                product("open_i_tanh_x", k, planes["abs_i", k], HS_EDGE, ALU.is_lt, planes["tanh_x", k])
+            elif scaled and name == "mask_f":
+                nc.vector.tensor_scalar(out=planes["abs_f", k], in0=planes["abs_f", k], scalar1=HS_EDGE, scalar2=-1.0, op0=ALU.is_lt, op1=ALU.mult)
+            elif scaled and name == "open_f_cell":
+                nc.vector.tensor_tensor(out=new_plane("open_f_cell", k, BF16), in0=planes["abs_f", k], in1=loaded["cell", k], op=ALU.mult)
+            elif scaled and name == "dx_c":
+                dx(GATE_C, k, "tanh_x_sq", 1.0 / HS_SLOPE, ALU.subtract, "minus_dc_i")
+            elif name == "tanh_x":
                 function("tanh_x", k, ACT.Tanh, loaded["x_c", k], over=loaded["x_c", k] if inpl else None)
             elif name.startswith("ramp_"):
                 function(name, k, ACT.Relu, loaded["x_" + name[-1], k], scale=HS_SLOPE, bias=0.5)
@@ -270,7 +290,7 @@ def tile_vlstmcell_v_kernel(
                 product("f_cell", k, planes["ramp_f", k], 1.0, ALU.min, loaded["cell", k])
                 new_cell[k] = psum.tile([P, N_TILE], F32, name="bank")
                 for nm in ("i_tanh_x", "f_cell"):
-                    nc.tensor.matmul(out=new_cell[k][:], lhsT=identity[:], rhs=planes[nm, k].rearrange("p j u -> p (j u)"),
+                    nc.tensor.matmul(out=new_cell[k][:], lhsT=minus_identity[:] if scaled and nm == "i_tanh_x" else identity[:], rhs=planes[nm, k].rearrange("p j u -> p (j u)"),
                                      start=(nm == "i_tanh_x"), stop=(nm == "f_cell"))
             elif name == "o_grad":
                 product("o_grad", k, planes["ramp_o", k], 1.0, ALU.min, loaded["grad", k])

@@ -35,7 +35,7 @@ BYTES = 2 * TOKENS * (FEATURES + 2 * UNITS) + 4 * TOKENS * GATES * UNITS + 4 * F
 
 
 CFG = {
-    "cell_whole": False, "in_whole": False, "x_pair_from": None, "inplace": True, "loads": None, "runs4": True, "scaled": True,
+    "cell_whole": False, "in_whole": False, "x_pair_from": None, "inplace": True, "loads": None, "runs4": True, "scaled": True, "run": 8,
     "s_order": [("tanh_x", 1), ("ramp_i", 1), ("size_i", 1), ("ramp_f", 1), ("size_f", 1), ("ramp_o", 1), ("size_o", 1),
                 ("tanh_x_sq", 1), ("tanh_c", 0), ("tanh_c_sq", 0), ("empty", -2)],
     "v_order": [("regroup0", 0), ("i_tanh_x", 0), ("f_cell", 0), ("mask_f", 0), ("minus_dc", -2),
@@ -92,6 +92,12 @@ def tile_vlstmcell_v_kernel(
                 loaded[name, k] = whole[name, c][:, :, (r - r0) * U_CHUNK : (r - r0 + 1) * U_CHUNK]
                 return
             first = first_column + r * U_CHUNK
+            if dtype == BF16 and cfg.get("tc02", False):
+                if ("cg", k) not in whole:
+                    whole["cg", k] = keep.tile([P, 2, PACK, U_CHUNK], BF16, name="cell_grad_%d" % k)
+                loaded[name, k] = whole["cg", k][:, 0 if name == "cell" else 1, :, :]
+                nc.sync.dma_start(out=loaded[name, k], in_=token_rows(source, c)[:, :, first : first + U_CHUNK])
+                return
             t = keep.tile([P, PACK, U_CHUNK], dtype, name="%s_%d" % (name, k))
             loaded[name, k] = t[:]
             nc.sync.dma_start(out=t[:], in_=token_rows(source, c)[:, :, first : first + U_CHUNK])
@@ -186,15 +192,16 @@ def tile_vlstmcell_v_kernel(
         inpl = cfg["inplace"]
         runs4 = cfg.get("runs4", False)
         scaled = cfg.get("scaled", False)
+        tc02 = cfg.get("tc02", False)
 
         def dx(gate, k, in0, scalar, op0, in1):
             if k not in grouped_dx:
                 grouped_dx[k] = stage_dx.tile([P, GATES, U_CHUNK, PACK], BF16, align_bytes=64, name="grouped_dx", bufs=cfg["bufs"].get("grouped_dx", 2))
             if scalar is None:
                 nc.vector.tensor_tensor(
-                    out=grouped_dx[k][:, gate, :, :].rearrange("p (w i) j -> p w j i", i=4),
-                    in0=planes[in0, k].rearrange("p j (w i) -> p w j i", i=4),
-                    in1=planes[in1, k].rearrange("p j (w i) -> p w j i", i=4), op=ALU.mult)
+                    out=grouped_dx[k][:, gate, :, :].rearrange("p (w i) j -> p w j i", i=cfg.get("run", 4)),
+                    in0=planes[in0, k].rearrange("p j (w i) -> p w j i", i=cfg.get("run", 4)),
+                    in1=planes[in1, k].rearrange("p j (w i) -> p w j i", i=cfg.get("run", 4)), op=ALU.mult)
                 return
             nc.vector.scalar_tensor_tensor(
                 out=grouped_dx[k][:, gate, :, :], in0=planes[in0, k].rearrange("p j u -> p u j"), scalar=scalar,
@@ -218,13 +225,17 @@ def tile_vlstmcell_v_kernel(
                     for each_pass in range(PASSES):
                         multiply_pass(r, each_pass, m)
 
-        def empty_banks(k, which=None):
+        def empty_banks(k, which=None, by_vector=False):
             r, c = divmod(k, PASSES)
             if c < PASSES - 1:
                 return
+            if k == CHUNKS - 1 and by_vector:
+                return
             for m in range(M_TILES) if which is None else which:
+                if k < CHUNKS - 1 and not by_vector and m in cfg.get("v_evac", ()):
+                    continue
                 result = stage_out.tile([M_TILE, GATES, U_CHUNK], F32, name="result")
-                if k == CHUNKS - 1 and m % 2 == 1:
+                if by_vector or (k == CHUNKS - 1 and m % 2 == 1):
                     nc.vector.tensor_copy(out=result[:].rearrange("p g u -> p (g u)"), in_=sums[r, m][:])
                 else:
                     nc.scalar.copy(out=result[:].rearrange("p g u -> p (g u)"), in_=sums[r, m][:])
@@ -246,7 +257,20 @@ def tile_vlstmcell_v_kernel(
                 return
             if no_chunk(k):
                 return
-            if scaled and name == "tanh_x":
+            if tc02 and name in ("size_f", "size_o"):
+                if ("abs_fo", k) not in planes:
+                    planes["abs_fo", k] = work.tile([P, 2, PACK, U_CHUNK], BF16, name="abs_fo", bufs=cfg["bufs"].get("abs_fo", 2))[:]
+                nc.scalar.activation(out=planes["abs_fo", k][:, 0 if name == "size_f" else 1, :, :], in_=upper_half(loaded["x_" + name[-1], k]), func=ACT.Abs)
+            elif name == "mask_fo":
+                nc.vector.tensor_scalar(out=planes["abs_fo", k], in0=planes["abs_fo", k], scalar1=HS_EDGE, scalar2=-1.0, op0=ALU.is_lt, op1=ALU.mult)
+            elif name == "open_fo":
+                planes["open_fo", k] = work.tile([P, 2, PACK, U_CHUNK], BF16, name="open_fo", bufs=cfg["bufs"].get("open_fo", 3))[:]
+                nc.vector.tensor_tensor(out=planes["open_fo", k], in0=planes["abs_fo", k], in1=whole["cg", k][:], op=ALU.mult)
+                planes["open_f_cell", k] = planes["open_fo", k][:, 0, :, :]
+                planes["open_o_grad", k] = planes["open_fo", k][:, 1, :, :]
+            elif name == "tanh_c02":
+                nc.scalar.activation(out=planes["tanh_c", k], in_=planes["tanh_c", k], func=ACT.Copy, scale=-HS_SLOPE)
+            elif scaled and name == "tanh_x":
                 function("tanh_x", k, ACT.Tanh, loaded["x_c", k], scale=-1.0, over=loaded["x_c", k])
             elif scaled and name == "ramp_o":
                 function(name, k, ACT.Relu, loaded["x_o", k], scale=HS_SLOPE * HS_SLOPE, bias=0.5 * HS_SLOPE)
@@ -280,6 +304,8 @@ def tile_vlstmcell_v_kernel(
                 function("tanh_c_sq", k, ACT.Square, planes["tanh_c", k])
             elif name == "empty":
                 empty_banks(k)
+            elif name == "vempty":
+                empty_banks(k, cfg.get("v_evac", ()), True)
             elif name == "empty_a":
                 empty_banks(k, range(0, M_TILES // 2))
             elif name == "empty_b":

@@ -35,14 +35,14 @@ BYTES = 2 * TOKENS * (FEATURES + 2 * UNITS) + 4 * TOKENS * GATES * UNITS + 4 * F
 
 
 CFG = {
-    "cell_whole": False, "in_whole": False, "x_pair_from": None, "inplace": True, "loads": None, "runs4": True, "scaled": True, "run": 8,
+    "tc02": True, "cell_whole": False, "in_whole": False, "x_pair_from": None, "inplace": True, "loads": None, "runs4": True, "scaled": True, "run": 8,
     "s_order": [("tanh_x", 1), ("ramp_i", 1), ("size_i", 1), ("ramp_f", 1), ("size_f", 1), ("ramp_o", 1), ("size_o", 1),
                 ("tanh_x_sq", 1), ("tanh_c", 0), ("tanh_c_sq", 0), ("empty", -2)],
-    "v_order": [("regroup0", 0), ("i_tanh_x", 0), ("f_cell", 0), ("mask_f", 0), ("minus_dc", -2),
-                ("open_i_tanh_x", 0), ("dx_o", -2), ("open_f_cell", 0), ("regroup1", 0), ("mask_o", 0), ("o_grad", 0),
-                ("minus_dc_i", -2), ("quant_in0", 0), ("dx_i", -2), ("dx_c", -2), ("quant_in1", 0), ("dx_f", -2),
-                ("open_o_grad", 0), ("quantise_dx", -2)],
-    "bufs": {"ramp_i": 4, "tanh_x_sq": 4, "o_grad": 3, "open_o_grad": 3, "open_i_tanh_x": 3, "open_f_cell": 3},
+    "v_order": [("regroup0", 0), ("i_tanh_x", 0), ("f_cell", 0), ("minus_dc", -2),
+                ("open_i_tanh_x", 0), ("dx_o", -2), ("mask_fo", 0), ("regroup1", 0), ("o_grad", 0),
+                ("minus_dc_i", -2), ("quant_in0", 0), ("dx_i", -2), ("open_fo", 0), ("dx_c", -2), ("quant_in1", 0), ("dx_f", -2),
+                ("quantise_dx", -2)],
+    "bufs": {"ramp_i": 4, "tanh_x_sq": 4, "o_grad": 3, "open_i_tanh_x": 3},
     "s_regroup": (), "steps_extra": 2, "out_bufs": 8, "late": 0, "free_banks": 1,
 }
 
@@ -327,7 +327,7 @@ def tile_vlstmcell_v_kernel(
             elif name == "open_f_cell" and runs4:
                 product("open_f_cell", k, loaded["cell", k], -HS_SLOPE, ALU.mult, planes["abs_f", k])
             elif name == "dx_o" and runs4:
-                dx(GATE_O, k, "tanh_c", None, None, "open_o_grad")
+                dx(GATE_O, k, "tanh_c", -HS_SLOPE, ALU.mult, "open_o_grad")
             elif name == "dx_i" and runs4:
                 dx(GATE_I, k, "minus_dc", None, None, "open_i_tanh_x")
             elif name == "dx_f" and runs4:

@@ -14,358 +14,360 @@ ALU = mybir.AluOpType
 ACT = mybir.ActivationFunctionType
 
 TOKENS, FEATURES, UNITS = 1024, 1024, 512
-GATES = 4
-GATE_I, GATE_F, GATE_C, GATE_O = 0, 1, 2, 3
+GATES = "ifco"
 P = 128
 PACK = 4
 K_PASS = P * PACK
 PASSES = TOKENS // K_PASS
+CHUNKS = PASSES * PACK
 M_TILE = 128
 M_TILES = FEATURES // M_TILE
-N_TILE = 512
 BANKS = 8
-U_CHUNK = N_TILE // GATES
-ROUNDS = UNITS // U_CHUNK
-CHUNKS = ROUNDS * PASSES
 F_PIECE = 512
+PIECES = PASSES * FEATURES // F_PIECE
+HALF = UNITS // 2
+QUARTER = UNITS // 4
+RUN = 8
 HS_SLOPE, HS_EDGE = 0.2, 2.5
 
-FLOPS = 2 * TOKENS * FEATURES * GATES * UNITS
-BYTES = 2 * TOKENS * (FEATURES + 2 * UNITS) + 4 * TOKENS * GATES * UNITS + 4 * FEATURES * GATES * UNITS
-
-
-CFG = {
-    "tc02": True, "cell_whole": False, "in_whole": False, "x_pair_from": None, "inplace": True, "loads": None, "runs4": True, "scaled": True, "run": 8,
-    "s_order": [("tanh_x", 1), ("ramp_i", 1), ("size_i", 1), ("ramp_f", 1), ("size_f", 1), ("ramp_o", 1), ("size_o", 1),
-                ("tanh_x_sq", 1), ("tanh_c", 0), ("tanh_c_sq", 0), ("empty", -2)],
-    "v_order": [("regroup0", 0), ("i_tanh_x", 0), ("f_cell", 0), ("minus_dc", -2),
-                ("open_i_tanh_x", 0), ("dx_o", -2), ("mask_fo", 0), ("regroup1", 0), ("o_grad", 0),
-                ("minus_dc_i", -2), ("quant_in0", 0), ("dx_i", -2), ("open_fo", 0), ("dx_c", -2), ("quant_in1", 0), ("dx_f", -2),
-                ("quantise_dx", -2)],
-    "bufs": {"ramp_i": 4, "tanh_x_sq": 4, "o_grad": 3, "open_i_tanh_x": 3},
-    "s_regroup": (), "steps_extra": 2, "out_bufs": 8, "late": 0, "free_banks": 1,
-}
+FLOPS = 2 * TOKENS * FEATURES * len(GATES) * UNITS
+BYTES = 2 * TOKENS * (FEATURES + 2 * UNITS) + 4 * TOKENS * len(GATES) * UNITS + 4 * FEATURES * len(GATES) * UNITS
 
 
 def tile_vlstmcell_v_kernel(
     tc, inputs, h_tm1, c_tm1, z_tm1, kernel, recurrent_kernel, recurrent_latent, bias, x, grad_out, out
 ):
     nc = tc.nc
-    cfg = CFG
     with ExitStack() as stack:
         keep = stack.enter_context(tc.tile_pool(name="keep", bufs=1))
-        stage_in = stack.enter_context(tc.tile_pool(name="stage_in", bufs=2))
         work = stack.enter_context(tc.tile_pool(name="work", bufs=2))
-        stage_dx = stack.enter_context(tc.tile_pool(name="stage_dx", bufs=2))
-        stage_out = stack.enter_context(tc.tile_pool(name="stage_out", bufs=cfg["out_bufs"]))
         psum = stack.enter_context(tc.psum_pool(name="psum", bufs=BANKS))
         stack.enter_context(tc.manual_schedule())
 
         def token_rows(ap, c):
             return ap[c * K_PASS : (c + 1) * K_PASS, :].rearrange("(p j) w -> p j w", j=PACK)
 
-        def no_chunk(k):
-            return k < 0 or k >= CHUNKS
+        def full_plane(name, dtype):
+            return [keep.tile([P, PACK, UNITS], dtype, name="%s_%d" % (name, c)) for c in range(PASSES)]
 
-        loaded = {}
+        x_of = {g: full_plane("x_" + g, F32) for g in GATES}
+        cell = full_plane("cell", BF16)
+        grad = full_plane("grad", BF16)
+        ramp_i = full_plane("ramp_i", F32)
+        tanh_c = full_plane("tanh_c", F32)
+        open_o = full_plane("open_o", BF16)
+
         raw_in = {}
-        whole = {}
 
-        def load(name, k):
-            source, first_column, dtype = {
-                "x_c": (x, GATE_C * UNITS, F32), "x_i": (x, GATE_I * UNITS, F32), "x_f": (x, GATE_F * UNITS, F32),
-                "x_o": (x, GATE_O * UNITS, F32), "cell": (c_tm1, 0, BF16), "grad": (grad_out, 0, BF16)}[name]
-            r, c = divmod(k, PASSES)
-            if dtype == BF16 and cfg["cell_whole"]:
-                if (name, c) not in whole:
-                    whole[name, c] = keep.tile([P, PACK, UNITS], dtype, name="%s_w%d" % (name, c))
-                    nc.sync.dma_start(out=whole[name, c][:], in_=token_rows(source, c))
-                loaded[name, k] = whole[name, c][:, :, r * U_CHUNK : (r + 1) * U_CHUNK]
-                return
-            if dtype == F32 and cfg["x_pair_from"] is not None and r >= cfg["x_pair_from"]:
-                r0 = cfg["x_pair_from"]
-                n = ROUNDS - r0
-                if (name, c) not in whole:
-                    whole[name, c] = keep.tile([P, PACK, n * U_CHUNK], dtype, name="%s_w%d" % (name, c))
-                    first = first_column + r0 * U_CHUNK
-                    nc.sync.dma_start(out=whole[name, c][:], in_=token_rows(source, c)[:, :, first : first + n * U_CHUNK])
-                loaded[name, k] = whole[name, c][:, :, (r - r0) * U_CHUNK : (r - r0 + 1) * U_CHUNK]
-                return
-            first = first_column + r * U_CHUNK
-            if dtype == BF16 and cfg.get("tc02", False):
-                if ("cg", k) not in whole:
-                    whole["cg", k] = keep.tile([P, 2, PACK, U_CHUNK], BF16, name="cell_grad_%d" % k)
-                loaded[name, k] = whole["cg", k][:, 0 if name == "cell" else 1, :, :]
-                nc.sync.dma_start(out=loaded[name, k], in_=token_rows(source, c)[:, :, first : first + U_CHUNK])
-                return
-            t = keep.tile([P, PACK, U_CHUNK], dtype, name="%s_%d" % (name, k))
-            loaded[name, k] = t[:]
-            nc.sync.dma_start(out=t[:], in_=token_rows(source, c)[:, :, first : first + U_CHUNK])
+        def load_inputs(piece):
+            c, half = divmod(piece, FEATURES // F_PIECE)
+            if half == 0:
+                raw_in[c] = work.tile([P, PACK, FEATURES], BF16, name="raw_in", bufs=1)
+            features = slice(half * F_PIECE, (half + 1) * F_PIECE)
+            nc.sync.dma_start(out=raw_in[c][:, :, features], in_=token_rows(inputs, c)[:, :, features])
+
+        def load_gate(g, k):
+            c, j = divmod(k, PACK)
+            first = GATES.index(g) * UNITS
+            nc.sync.dma_start(out=x_of[g][c][:, j, :], in_=token_rows(x, c)[:, j, first : first + UNITS])
 
         def load_chunk(k):
-            for name in ("x_c", "x_i", "cell", "x_f", "grad", "x_o"):
-                load(name, k)
+            c, j = divmod(k, PACK)
+            load_gate("c", k)
+            load_gate("i", k)
+            nc.sync.dma_start(out=cell[c][:, j, :], in_=token_rows(c_tm1, c)[:, j, :])
+            load_gate("f", k)
+            nc.sync.dma_start(out=grad[c][:, j, :], in_=token_rows(grad_out, c)[:, j, :])
+            load_gate("o", k)
 
-        def load_inputs(c, piece):
-            if cfg["in_whole"]:
-                if ("in", c) not in whole:
-                    whole["in", c] = keep.tile([P, PACK, FEATURES], BF16, name="raw_in_%d" % c)
-                    nc.sync.dma_start(out=whole["in", c][:], in_=token_rows(inputs, c))
-                raw_in[c, piece] = whole["in", c][:, :, piece * F_PIECE : (piece + 1) * F_PIECE]
-                return
-            t = keep.tile([P, PACK, F_PIECE], BF16, name="raw_in_%d_%d" % (c, piece))
-            raw_in[c, piece] = t[:]
-            nc.sync.dma_start(out=t[:], in_=token_rows(inputs, c)[:, :, piece * F_PIECE : (piece + 1) * F_PIECE])
-
-        order = cfg["loads"] or [("in", 0, 0), 0, ("in", 0, 1), ("in", 1, 0), 1, ("in", 1, 1), 2, 3, 4, 5, 6, 7]
-        late = order[len(order) - cfg["late"] :] if cfg["late"] else []
-        for item in order[: len(order) - cfg["late"]]:
-            if isinstance(item, tuple):
-                if item[0] == "in":
-                    load_inputs(item[1], item[2])
-                else:
-                    load(item[0], item[1])
-            else:
-                load_chunk(item)
+        for k in range(CHUNKS):
+            if k < PIECES:
+                load_inputs(k)
+            load_chunk(k)
 
         identity = keep.tile([P, P], F32)
         make_identity(nc, identity[:])
         minus_identity = keep.tile([P, P], F32)
         nc.vector.tensor_scalar(out=minus_identity[:], in0=identity[:], scalar1=-1.0, scalar2=None, op0=ALU.mult)
+        minus_slope = keep.tile([P, P], F32)
+        nc.vector.tensor_scalar(out=minus_slope[:], in0=identity[:], scalar1=-HS_SLOPE, scalar2=None, op0=ALU.mult)
 
         in_codes = keep.tile([P, PASSES, FEATURES], U32, align_bytes=64)
         in_scales = keep.tile([P, PASSES, FEATURES], U8, align_bytes=64)
+        dx_codes = keep.tile([P, len(GATES), PASSES, UNITS], U32, align_bytes=64)
+        dx_scales = keep.tile([P, len(GATES), PASSES, UNITS], U8, align_bytes=64)
         grouped_in = {}
 
-        def regroup_inputs(c, piece, engine=None):
-            if c < 0 or c >= PASSES:
-                return
-            grouped_in[c, piece] = stage_in.tile([P, F_PIECE, PACK], BF16, align_bytes=64, name="grouped_in", bufs=cfg["bufs"].get("grouped_in", 2))
-            o = grouped_in[c, piece][:].rearrange("p (w i) j -> p w j i", i=4)
-            i_ = raw_in[c, piece].rearrange("p j (w i) -> p w j i", i=4)
-            if engine == "S":
-                nc.scalar.copy(out=o, in_=i_)
-            else:
-                nc.vector.tensor_copy(out=o, in_=i_)
+        def regroup_inputs(piece):
+            c, half = divmod(piece, FEATURES // F_PIECE)
+            grouped_in[piece] = work.tile([P, F_PIECE, PACK], BF16, align_bytes=64, name="grouped_in", bufs=1)
+            nc.vector.tensor_copy(
+                out=grouped_in[piece][:].rearrange("p (w i) j -> p w j i", i=4),
+                in_=raw_in[c][:, :, half * F_PIECE : (half + 1) * F_PIECE].rearrange("p j (w i) -> p w j i", i=4),
+            )
 
-        def quantise_inputs(c, piece):
-            if c < 0 or c >= PASSES:
-                return
-            features = slice(piece * F_PIECE, (piece + 1) * F_PIECE)
+        def quantise_inputs(piece):
+            c, half = divmod(piece, FEATURES // F_PIECE)
+            features = slice(half * F_PIECE, (half + 1) * F_PIECE)
             nc.vector.quantize_mx(
                 out=in_codes[:, c, features].bitcast(E4M3_X4),
                 scales=in_scales[:, c, features],
-                in_=grouped_in[c, piece][:].rearrange("p w j -> p (w j)"),
+                in_=grouped_in[piece][:].rearrange("p w j -> p (w j)"),
             )
 
-        dx_codes = keep.tile([P, PASSES, ROUNDS, N_TILE], U32, align_bytes=64)
-        dx_scales = keep.tile([P, PASSES, ROUNDS, N_TILE], U8, align_bytes=64)
-        planes = {}
-
-        def new_plane(name, k, dtype=F32):
-            t = work.tile([P, PACK, U_CHUNK], dtype, name=name, bufs=cfg["bufs"].get(name, 2))
-            planes[name, k] = t[:]
-            return planes[name, k]
-
-        def function(name, k, func, in_, scale=1.0, bias=0.0, dtype=F32, over=None):
-            if over is not None:
-                planes[name, k] = over
-                o = over
-            else:
-                o = new_plane(name, k, dtype)
-            nc.scalar.activation(out=o, in_=in_, func=func, bias=bias, scale=scale)
-
-        def product(name, k, in0, scalar, op0, in1, dtype=F32, over=None):
-            if over is not None:
-                planes[name, k] = over
-                o = over
-            else:
-                o = new_plane(name, k, dtype)
-            nc.vector.scalar_tensor_tensor(out=o, in0=in0, scalar=scalar, in1=in1, op0=op0, op1=ALU.mult)
-
-        def upper_half(ap):
-            return ap.bitcast(BF16).rearrange("p j (u h) -> p j u h", h=2)[:, :, :, 1]
-
+        plane = {}
         new_cell = {}
-        grouped_dx = {}
-        sums = {}
-        inpl = cfg["inplace"]
-        runs4 = cfg.get("runs4", False)
-        scaled = cfg.get("scaled", False)
-        tc02 = cfg.get("tc02", False)
 
-        def dx(gate, k, in0, scalar, op0, in1):
-            if k not in grouped_dx:
-                grouped_dx[k] = stage_dx.tile([P, GATES, U_CHUNK, PACK], BF16, align_bytes=64, name="grouped_dx", bufs=cfg["bufs"].get("grouped_dx", 2))
-            if scalar is None:
-                nc.vector.tensor_tensor(
-                    out=grouped_dx[k][:, gate, :, :].rearrange("p (w i) j -> p w j i", i=cfg.get("run", 4)),
-                    in0=planes[in0, k].rearrange("p j (w i) -> p w j i", i=cfg.get("run", 4)),
-                    in1=planes[in1, k].rearrange("p j (w i) -> p w j i", i=cfg.get("run", 4)), op=ALU.mult)
-                return
+        def new(name, k, bufs, dtype=F32):
+            plane[name, k] = work.tile([P, UNITS], dtype, name=name, bufs=bufs)
+            return plane[name, k][:]
+
+        def stt(target, in0, scalar, op0, in1):
+            nc.vector.scalar_tensor_tensor(out=target, in0=in0, scalar=scalar, in1=in1, op0=op0, op1=ALU.mult)
+
+        def gates_first(k):
+            c, j = divmod(k, PACK)
+            x_c = x_of["c"][c][:, j, :]
+            nc.scalar.activation(out=x_c, in_=x_c, func=ACT.Tanh, scale=-1.0)
+            nc.scalar.activation(out=ramp_i[c][:, j, :], in_=x_of["i"][c][:, j, :], func=ACT.Relu, scale=HS_SLOPE, bias=0.5)
+            nc.scalar.activation(out=new("ramp_f", k, 3), in_=x_of["f"][c][:, j, :], func=ACT.Relu, scale=HS_SLOPE, bias=0.5)
+
+        def gates_last(k):
+            c, j = divmod(k, PACK)
+            x_o = x_of["o"][c][:, j, :]
+            upper = x_o.bitcast(BF16).rearrange("p (u h) -> p u h", h=2)[:, :, 1]
+            nc.scalar.activation(out=new("abs_o", k, 2, BF16), in_=upper, func=ACT.Abs)
+            nc.scalar.activation(out=new("ramp_o", k, 4), in_=x_o, func=ACT.Relu, scale=HS_SLOPE * HS_SLOPE, bias=0.5 * HS_SLOPE)
+
+        def tanh_of_cell(k):
+            c, j = divmod(k, PACK)
+            nc.scalar.activation(out=tanh_c[c][:, j, :], in_=new_cell[k][:], func=ACT.Tanh)
+            nc.scalar.activation(out=x_of["o"][c][:, j, :], in_=tanh_c[c][:, j, :], func=ACT.Square)
+
+        def cell_products(k):
+            c, j = divmod(k, PACK)
+            i_tanh_x = new("i_tanh_x", k, 2)
+            stt(i_tanh_x, ramp_i[c][:, j, :], 1.0, ALU.min, x_of["c"][c][:, j, :])
+            f_cell = plane["ramp_f", k][:]
+            stt(f_cell, f_cell, 1.0, ALU.min, cell[c][:, j, :])
+            new_cell[k] = psum.tile([P, UNITS], F32, name="bank")
+            nc.tensor.matmul(out=new_cell[k][:], lhsT=minus_identity[:], rhs=i_tanh_x, start=True, stop=False)
+            nc.tensor.matmul(out=new_cell[k][:], lhsT=identity[:], rhs=f_cell, start=False, stop=True)
+
+        def minus_dc(k):
+            c, j = divmod(k, PACK)
+            dc = x_of["o"][c][:, j, :]
+            stt(dc, dc, 1.0, ALU.subtract, plane["ramp_o", k][:])
+
+        def grad_products(k):
+            c, j = divmod(k, PACK)
+            mask = plane["abs_o", k][:]
+            nc.vector.tensor_scalar(out=mask, in0=mask, scalar1=HS_EDGE, scalar2=-1.0, op0=ALU.is_lt, op1=ALU.mult)
+            o_grad = plane["ramp_o", k][:]
+            stt(o_grad, o_grad, HS_SLOPE, ALU.min, grad[c][:, j, :])
+            nc.vector.tensor_tensor(out=open_o[c][:, j, :], in0=grad[c][:, j, :], in1=mask, op=ALU.mult)
+
+        grouped = {}
+        size = {}
+        scaled_tanh_c = {}
+
+        def runs(ap):
+            return ap.rearrange("p j (w i) -> p w j i", i=RUN)
+
+        def target(g, c, units):
+            if (g, c) not in grouped:
+                grouped[g, c] = work.tile([P, UNITS, PACK], BF16, align_bytes=64, name="grouped_dx", bufs=3)
+            return grouped[g, c][:, units, :]
+
+        def dx_product(g, c, units, in0, in1):
+            nc.vector.tensor_tensor(
+                out=target(g, c, units).rearrange("p (w i) j -> p w j i", i=RUN), in0=runs(in0), in1=runs(in1), op=ALU.mult
+            )
+
+        def halves():
+            return (slice(0, HALF), slice(HALF, UNITS))
+
+        def quarter(n):
+            return slice(n * QUARTER, (n + 1) * QUARTER)
+
+        def abs_of(g, c):
+            size[g, c] = work.tile([P, PACK, UNITS], BF16, name="abs_" + g, bufs=2)
+            upper = x_of[g][c][:].bitcast(BF16).rearrange("p j (u h) -> p j u h", h=2)
+            for units in halves():
+                nc.scalar.activation(out=size[g, c][:, :, units], in_=upper[:, :, units, 1], func=ACT.Abs)
+
+        def scale_tanh_c(c, n):
+            scaled_tanh_c[c, n] = psum.tile([P, PACK, QUARTER], F32, name="bank")
+            nc.tensor.matmul(
+                out=scaled_tanh_c[c, n][:].rearrange("p j u -> p (j u)"), lhsT=minus_slope[:], rhs=tanh_c[c][:, :, quarter(n)],
+                start=True, stop=True,
+            )
+
+        def dx_o(c, n):
+            dx_product("o", c, quarter(n), scaled_tanh_c[c, n][:], open_o[c][:, :, quarter(n)])
+
+        def mask_f(c, units):
+            mask = size["f", c][:, :, units]
+            nc.vector.tensor_scalar(out=mask, in0=mask, scalar1=HS_EDGE, scalar2=-1.0, op0=ALU.is_lt, op1=ALU.mult)
+
+        def open_f(c, units):
+            mask = size["f", c][:, :, units]
+            nc.vector.tensor_tensor(out=mask, in0=mask, in1=cell[c][:, :, units], op=ALU.mult)
+
+        def dx_f(c, units):
+            dx_product("f", c, units, x_of["o"][c][:, :, units], size["f", c][:, :, units])
+
+        def open_i(c, units):
+            stt(x_of["i"][c][:, :, units], size["i", c][:, :, units], HS_EDGE, ALU.is_lt, x_of["c"][c][:, :, units])
+
+        def dx_i(c, units):
+            dx_product("i", c, units, x_of["o"][c][:, :, units], x_of["i"][c][:, :, units])
+
+        def square_tanh_x(c, units):
+            plane_c = x_of["c"][c][:, :, units]
+            nc.scalar.activation(out=plane_c, in_=plane_c, func=ACT.Square, scale=math.sqrt(1.0 / HS_SLOPE))
+
+        def minus_dc_i(c, units):
+            plane_i = ramp_i[c][:, :, units]
+            stt(plane_i, plane_i, 1.0, ALU.min, x_of["o"][c][:, :, units])
+
+        def dx_c(c, units):
             nc.vector.scalar_tensor_tensor(
-                out=grouped_dx[k][:, gate, :, :], in0=planes[in0, k].rearrange("p j u -> p u j"), scalar=scalar,
-                in1=planes[in1, k].rearrange("p j u -> p u j"), op0=op0, op1=ALU.mult)
+                out=target("c", c, units), in0=x_of["c"][c][:, :, units].rearrange("p j u -> p u j"), scalar=1.0 / HS_SLOPE,
+                in1=ramp_i[c][:, :, units].rearrange("p j u -> p u j"), op0=ALU.subtract, op1=ALU.mult,
+            )
 
-        def multiply_pass(r, c, m):
-            if c == 0:
-                sums[r, m] = psum.tile([M_TILE, N_TILE], F32, name="bank")
-            features = slice(m * M_TILE, (m + 1) * M_TILE)
-            nc.tensor.matmul_mx(
-                out=sums[r, m][:], lhsT=in_codes[:, c, features].bitcast(E4M3_X4), lhsT_scale=in_scales[:, c, features],
-                rhs=dx_codes[:, c, r, :].bitcast(E5M2_X4), rhs_scale=dx_scales[:, c, r, :],
-                start=(c == 0), stop=(c == PASSES - 1))
+        def quantise_dx(g, c, units=slice(0, UNITS)):
+            n = GATES.index(g)
+            nc.vector.quantize_mx(
+                out=dx_codes[:, n, c, units].bitcast(E5M2_X4), scales=dx_scales[:, n, c, units],
+                in_=grouped[g, c][:, units, :].rearrange("p u j -> p (u j)"),
+            )
 
-        def multiply(k):
-            r, c = divmod(k, PASSES)
-            for m in range(BANKS - cfg.get("free_banks", 1)):
-                multiply_pass(r, c, m)
-            if c == PASSES - 1:
-                for m in range(BANKS - cfg.get("free_banks", 1), M_TILES):
-                    for each_pass in range(PASSES):
-                        multiply_pass(r, each_pass, m)
+        sums = {}
 
-        def empty_banks(k, which=None, by_vector=False):
-            r, c = divmod(k, PASSES)
-            if c < PASSES - 1:
-                return
-            if k == CHUNKS - 1 and by_vector:
-                return
-            for m in range(M_TILES) if which is None else which:
-                if k < CHUNKS - 1 and not by_vector and m in cfg.get("v_evac", ()):
-                    continue
-                result = stage_out.tile([M_TILE, GATES, U_CHUNK], F32, name="result")
-                if by_vector or (k == CHUNKS - 1 and m % 2 == 1):
-                    nc.vector.tensor_copy(out=result[:].rearrange("p g u -> p (g u)"), in_=sums[r, m][:])
-                else:
-                    nc.scalar.copy(out=result[:].rearrange("p g u -> p (g u)"), in_=sums[r, m][:])
-                nc.sync.dma_start(
-                    out=out[m * M_TILE : (m + 1) * M_TILE, :].rearrange("i (g r u) -> i g r u", g=GATES, r=ROUNDS)[:, :, r, :],
-                    in_=result[:])
+        def multiply(g):
+            n = GATES.index(g)
+            for m in range(M_TILES):
+                sums[g, m] = psum.tile([M_TILE, UNITS], F32, name="bank")
+            for c in range(PASSES):
+                for m in range(M_TILES):
+                    features = slice(m * M_TILE, (m + 1) * M_TILE)
+                    nc.tensor.matmul_mx(
+                        out=sums[g, m][:], lhsT=in_codes[:, c, features].bitcast(E4M3_X4), lhsT_scale=in_scales[:, c, features],
+                        rhs=dx_codes[:, n, c, :].bitcast(E5M2_X4), rhs_scale=dx_scales[:, n, c, :],
+                        start=(c == 0), stop=(c == PASSES - 1),
+                    )
 
-        def do(name, k, t):
-            if name.startswith("regroup") or name.startswith("quant_in") or name.startswith("sregroup"):
-                piece = int(name[-1])
-                if name.startswith("regroup"):
-                    if (k, piece) not in cfg["s_regroup"]:
-                        regroup_inputs(k, piece)
-                elif name.startswith("sregroup"):
-                    if (k, piece) in cfg["s_regroup"]:
-                        regroup_inputs(k, piece, "S")
-                else:
-                    quantise_inputs(k, piece)
-                return
-            if no_chunk(k):
-                return
-            if tc02 and name in ("size_f", "size_o"):
-                if ("abs_fo", k) not in planes:
-                    planes["abs_fo", k] = work.tile([P, 2, PACK, U_CHUNK], BF16, name="abs_fo", bufs=cfg["bufs"].get("abs_fo", 2))[:]
-                nc.scalar.activation(out=planes["abs_fo", k][:, 0 if name == "size_f" else 1, :, :], in_=upper_half(loaded["x_" + name[-1], k]), func=ACT.Abs)
-            elif name == "mask_fo":
-                nc.vector.tensor_scalar(out=planes["abs_fo", k], in0=planes["abs_fo", k], scalar1=HS_EDGE, scalar2=-1.0, op0=ALU.is_lt, op1=ALU.mult)
-            elif name == "open_fo":
-                planes["open_fo", k] = work.tile([P, 2, PACK, U_CHUNK], BF16, name="open_fo", bufs=cfg["bufs"].get("open_fo", 3))[:]
-                nc.vector.tensor_tensor(out=planes["open_fo", k], in0=planes["abs_fo", k], in1=whole["cg", k][:], op=ALU.mult)
-                planes["open_f_cell", k] = planes["open_fo", k][:, 0, :, :]
-                planes["open_o_grad", k] = planes["open_fo", k][:, 1, :, :]
-            elif name == "tanh_c02":
-                nc.scalar.activation(out=planes["tanh_c", k], in_=planes["tanh_c", k], func=ACT.Copy, scale=-HS_SLOPE)
-            elif scaled and name == "tanh_x":
-                function("tanh_x", k, ACT.Tanh, loaded["x_c", k], scale=-1.0, over=loaded["x_c", k])
-            elif scaled and name == "ramp_o":
-                function(name, k, ACT.Relu, loaded["x_o", k], scale=HS_SLOPE * HS_SLOPE, bias=0.5 * HS_SLOPE)
-            elif scaled and name == "tanh_x_sq":
-                function("tanh_x_sq", k, ACT.Square, planes["tanh_x", k], scale=math.sqrt(1.0 / HS_SLOPE))
-            elif scaled and name == "o_grad":
-                product("o_grad", k, planes["ramp_o", k], HS_SLOPE, ALU.min, loaded["grad", k])
-            elif scaled and name == "open_i_tanh_x":
-                product("open_i_tanh_x", k, planes["abs_i", k], HS_EDGE, ALU.is_lt, planes["tanh_x", k])
-            elif scaled and name == "mask_f":
-                nc.vector.tensor_scalar(out=planes["abs_f", k], in0=planes["abs_f", k], scalar1=HS_EDGE, scalar2=-1.0, op0=ALU.is_lt, op1=ALU.mult)
-            elif scaled and name == "open_f_cell":
-                nc.vector.tensor_tensor(out=new_plane("open_f_cell", k, BF16), in0=planes["abs_f", k], in1=loaded["cell", k], op=ALU.mult)
-            elif scaled and name == "dx_c":
-                dx(GATE_C, k, "tanh_x_sq", 1.0 / HS_SLOPE, ALU.subtract, "minus_dc_i")
-            elif name == "tanh_x":
-                function("tanh_x", k, ACT.Tanh, loaded["x_c", k], over=loaded["x_c", k] if inpl else None)
-            elif name.startswith("ramp_"):
-                function(name, k, ACT.Relu, loaded["x_" + name[-1], k], scale=HS_SLOPE, bias=0.5)
-            elif name == "size_i" and not runs4:
-                function("abs_i", k, ACT.Abs, loaded["x_i", k], over=loaded["x_i", k] if inpl else None)
-            elif name.startswith("mask_"):
-                nc.vector.tensor_scalar(out=planes["abs_" + name[-1], k], in0=planes["abs_" + name[-1], k], scalar1=HS_EDGE, scalar2=None, op0=ALU.is_lt)
-            elif name.startswith("size_"):
-                function("abs_" + name[-1], k, ACT.Abs, upper_half(loaded["x_" + name[-1], k]), dtype=BF16)
-            elif name == "tanh_x_sq":
-                function("tanh_x_sq", k, ACT.Square, planes["tanh_x", k])
-            elif name == "tanh_c":
-                function("tanh_c", k, ACT.Tanh, new_cell[k][:].rearrange("p (j u) -> p j u", j=PACK))
-            elif name == "tanh_c_sq":
-                function("tanh_c_sq", k, ACT.Square, planes["tanh_c", k])
-            elif name == "empty":
-                empty_banks(k)
-            elif name == "vempty":
-                empty_banks(k, cfg.get("v_evac", ()), True)
-            elif name == "empty_a":
-                empty_banks(k, range(0, M_TILES // 2))
-            elif name == "empty_b":
-                empty_banks(k, range(M_TILES // 2, M_TILES))
-            elif name == "i_tanh_x":
-                product("i_tanh_x", k, planes["ramp_i", k], 1.0, ALU.min, planes["tanh_x", k])
-            elif name == "f_cell":
-                product("f_cell", k, planes["ramp_f", k], 1.0, ALU.min, loaded["cell", k])
-                new_cell[k] = psum.tile([P, N_TILE], F32, name="bank")
-                for nm in ("i_tanh_x", "f_cell"):
-                    nc.tensor.matmul(out=new_cell[k][:], lhsT=minus_identity[:] if scaled and nm == "i_tanh_x" else identity[:], rhs=planes[nm, k].rearrange("p j u -> p (j u)"),
-                                     start=(nm == "i_tanh_x"), stop=(nm == "f_cell"))
-            elif name == "o_grad":
-                product("o_grad", k, planes["ramp_o", k], 1.0, ALU.min, loaded["grad", k])
-            elif name == "open_o_grad" and runs4:
-                product("open_o_grad", k, loaded["grad", k], HS_SLOPE, ALU.mult, planes["abs_o", k])
-            elif name == "open_i_tanh_x" and runs4:
-                product("open_i_tanh_x", k, planes["tanh_x", k], -HS_SLOPE, ALU.mult, planes["abs_i", k])
-            elif name == "open_f_cell" and runs4:
-                product("open_f_cell", k, loaded["cell", k], -HS_SLOPE, ALU.mult, planes["abs_f", k])
-            elif name == "dx_o" and runs4:
-                dx(GATE_O, k, "tanh_c", -HS_SLOPE, ALU.mult, "open_o_grad")
-            elif name == "dx_i" and runs4:
-                dx(GATE_I, k, "minus_dc", None, None, "open_i_tanh_x")
-            elif name == "dx_f" and runs4:
-                dx(GATE_F, k, "minus_dc", None, None, "open_f_cell")
-            elif name == "open_o_grad":
-                product("open_o_grad", k, planes["abs_o", k], HS_EDGE, ALU.is_lt, loaded["grad", k], BF16)
-            elif name == "open_i_tanh_x":
-                product("open_i_tanh_x", k, planes["abs_i", k], HS_EDGE, ALU.is_lt, planes["tanh_x", k])
-            elif name == "open_f_cell":
-                product("open_f_cell", k, planes["abs_f", k], HS_EDGE, ALU.is_lt, loaded["cell", k], BF16)
-            elif name == "minus_dc":
-                product("minus_dc", k, planes["tanh_c_sq", k], 1.0, ALU.subtract, planes["o_grad", k], over=planes["tanh_c_sq", k] if inpl else None)
-            elif name == "minus_dc_i":
-                product("minus_dc_i", k, planes["ramp_i", k], 1.0, ALU.min, planes["minus_dc", k], over=planes["o_grad", k] if inpl else None)
-            elif name == "dx_o":
-                dx(GATE_O, k, "tanh_c", HS_SLOPE, ALU.mult, "open_o_grad")
-            elif name == "dx_i":
-                dx(GATE_I, k, "minus_dc", -HS_SLOPE, ALU.mult, "open_i_tanh_x")
-            elif name == "dx_c":
-                dx(GATE_C, k, "tanh_x_sq", 1.0, ALU.subtract, "minus_dc_i")
-            elif name == "dx_f":
-                dx(GATE_F, k, "minus_dc", -HS_SLOPE, ALU.mult, "open_f_cell")
-            elif name == "quantise_dx":
-                r, c = divmod(k, PASSES)
-                nc.vector.quantize_mx(out=dx_codes[:, c, r, :].bitcast(E5M2_X4), scales=dx_scales[:, c, r, :],
-                                      in_=grouped_dx[k][:].rearrange("p g u j -> p (g u j)"))
-                multiply(k)
+        def empty_bank(g, m, by_vector=False):
+            n = GATES.index(g)
+            result = work.tile([M_TILE, UNITS], F32, name="result", bufs=8)
+            if by_vector:
+                nc.vector.tensor_copy(out=result[:], in_=sums[g, m][:])
             else:
-                raise ValueError(name)
+                nc.scalar.copy(out=result[:], in_=sums[g, m][:])
+            nc.sync.dma_start(out=out[m * M_TILE : (m + 1) * M_TILE, n * UNITS : (n + 1) * UNITS], in_=result[:])
 
-        for name, d in cfg["s_order"]:
-            if d >= 1:
-                do(name, -1 + d, -1)
-        for t in range(CHUNKS + cfg["steps_extra"]):
-            for name, d in cfg["v_order"]:
-                do(name, t + d, t)
-            for name, d in cfg["s_order"]:
-                do(name, t + d, t)
-            if t == PASSES:
-                for item in late:
-                    load_chunk(item)
+        def empty_banks(g):
+            for m in range(M_TILES):
+                empty_bank(g, m)
+
+        first, second = halves()
+        gates_first(0)
+        gates_last(0)
+        regroup_inputs(0)
+        quantise_inputs(0)
+        for t in range(CHUNKS + 1):
+            if t < CHUNKS:
+                cell_products(t)
+            else:
+                for step in (mask_f, open_f):
+                    for units in halves():
+                        step(0, units)
+            if 1 <= t < PIECES:
+                quantise_inputs(t)
+                if t + 1 < PIECES:
+                    regroup_inputs(t + 1)
+            if t in (4, 5):
+                for n in (0, 1):
+                    if t == 5:
+                        dx_o(0, n)
+                for n in (0, 1):
+                    scale_tanh_c(0, 2 * (t - 4) + n)
+            if t == 6:
+                dx_o(0, 2)
+                dx_o(0, 3)
+            if t == 7:
+                for units in halves():
+                    minus_dc_i(0, units)
+            if t >= 1:
+                minus_dc(t - 1)
+            if t < CHUNKS:
+                grad_products(t)
+            if t == 0:
+                regroup_inputs(1)
+            if t == 6:
+                quantise_dx("o", 0)
+            if t + 1 < CHUNKS:
+                gates_first(t + 1)
+            if t == CHUNKS - 1:
+                abs_of("f", 0)
+            if t < CHUNKS:
+                tanh_of_cell(t)
+            if t + 1 < CHUNKS:
+                gates_last(t + 1)
+        abs_of("f", 1)
+
+        for n in range(4):
+            scale_tanh_c(1, n)
+        for units in halves():
+            dx_f(0, units)
+        for n in range(4):
+            dx_o(1, n)
+        quantise_dx("o", 1)
+        multiply("o")
+
+        mask_f(1, first)
+        quantise_dx("f", 0)
+        mask_f(1, second)
+        for step in (open_f, dx_f):
+            for units in halves():
+                step(1, units)
+        abs_of("i", 0)
+        empty_banks("o")
+        abs_of("i", 1)
+        open_i(0, first)
+        quantise_dx("f", 1)
+        open_i(0, second)
+        multiply("f")
+
+        for units in halves():
+            dx_i(0, units)
+        open_i(1, first)
+        quantise_dx("i", 0)
+        open_i(1, second)
+        for units in halves():
+            dx_i(1, units)
+        empty_banks("f")
+        for c in range(PASSES):
+            for units in halves():
+                square_tanh_x(c, units)
+        minus_dc_i(1, first)
+        quantise_dx("i", 1)
+        minus_dc_i(1, second)
+        multiply("i")
+
+        for units in halves():
+            dx_c(0, units)
+        dx_c(1, quarter(0))
+        quantise_dx("c", 0)
+        dx_c(1, quarter(1))
+        dx_c(1, quarter(2))
+        quantise_dx("c", 1, first)
+        dx_c(1, quarter(3))
+        quantise_dx("c", 1, quarter(2))
+        quantise_dx("c", 1, quarter(3))
+        empty_banks("i")
+        multiply("c")
+        for m in range(M_TILES):
+            empty_bank("c", m, by_vector=(m % 2 == 1))

@@ -23,8 +23,7 @@ CHUNKS = PASSES * PACK
 M_TILE = 128
 M_TILES = FEATURES // M_TILE
 BANKS = 8
-F_PIECE = 512
-PIECES = PASSES * FEATURES // F_PIECE
+IN_PIECES = [(0, 0, 256), (0, 256, 256), (0, 512, 512), (1, 0, 512), (1, 512, 512)]
 HALF = UNITS // 2
 QUARTER = UNITS // 4
 RUN = 8
@@ -60,30 +59,30 @@ def tile_vlstmcell_v_kernel(
         raw_in = {}
 
         def load_inputs(piece):
-            c, half = divmod(piece, FEATURES // F_PIECE)
-            if half == 0:
-                raw_in[c] = work.tile([P, PACK, FEATURES], BF16, name="raw_in", bufs=1)
-            features = slice(half * F_PIECE, (half + 1) * F_PIECE)
-            nc.sync.dma_start(out=raw_in[c][:, :, features], in_=token_rows(inputs, c)[:, :, features])
+            c, first, width = IN_PIECES[piece]
+            raw_in[piece] = work.tile([P, PACK, width], BF16, name="raw_in", bufs=3)
+            nc.sync.dma_start(out=raw_in[piece][:], in_=token_rows(inputs, c)[:, :, first : first + width])
 
         def load_gate(g, k):
             c, j = divmod(k, PACK)
             first = GATES.index(g) * UNITS
             nc.sync.dma_start(out=x_of[g][c][:, j, :], in_=token_rows(x, c)[:, j, first : first + UNITS])
 
-        def load_chunk(k):
+        def load_half(plane, source, k):
             c, j = divmod(k, PACK)
-            load_gate("c", k)
-            load_gate("i", k)
-            nc.sync.dma_start(out=cell[c][:, j, :], in_=token_rows(c_tm1, c)[:, j, :])
-            load_gate("f", k)
-            nc.sync.dma_start(out=grad[c][:, j, :], in_=token_rows(grad_out, c)[:, j, :])
-            load_gate("o", k)
+            nc.sync.dma_start(out=plane[c][:, j, :], in_=token_rows(source, c)[:, j, :])
 
         for k in range(CHUNKS):
-            if k < PIECES:
-                load_inputs(k)
-            load_chunk(k)
+            load_gate("c", k)
+            load_gate("i", k)
+            load_gate("f", k)
+            load_half(cell, c_tm1, k)
+            load_gate("o", k)
+            if k == 0:
+                load_inputs(0)
+            load_half(grad, grad_out, k)
+            for piece in {0: (1,), 1: (2,), 2: (3,), 3: (4,)}.get(k, ()):
+                load_inputs(piece)
 
         identity = keep.tile([P, P], F32)
         make_identity(nc, identity[:])
@@ -99,16 +98,16 @@ def tile_vlstmcell_v_kernel(
         grouped_in = {}
 
         def regroup_inputs(piece):
-            c, half = divmod(piece, FEATURES // F_PIECE)
-            grouped_in[piece] = work.tile([P, F_PIECE, PACK], BF16, align_bytes=64, name="grouped_in", bufs=1)
+            width = IN_PIECES[piece][2]
+            grouped_in[piece] = work.tile([P, width, PACK], BF16, align_bytes=64, name="grouped_in", bufs=2)
             nc.vector.tensor_copy(
                 out=grouped_in[piece][:].rearrange("p (w i) j -> p w j i", i=4),
-                in_=raw_in[c][:, :, half * F_PIECE : (half + 1) * F_PIECE].rearrange("p j (w i) -> p w j i", i=4),
+                in_=raw_in[piece][:].rearrange("p j (w i) -> p w j i", i=4),
             )
 
         def quantise_inputs(piece):
-            c, half = divmod(piece, FEATURES // F_PIECE)
-            features = slice(half * F_PIECE, (half + 1) * F_PIECE)
+            c, first, width = IN_PIECES[piece]
+            features = slice(first, first + width)
             nc.vector.quantize_mx(
                 out=in_codes[:, c, features].bitcast(E4M3_X4),
                 scales=in_scales[:, c, features],
@@ -125,17 +124,13 @@ def tile_vlstmcell_v_kernel(
         def stt(target, in0, scalar, op0, in1):
             nc.vector.scalar_tensor_tensor(out=target, in0=in0, scalar=scalar, in1=in1, op0=op0, op1=ALU.mult)
 
-        def gates_first(k):
+        def gates(k):
             c, j = divmod(k, PACK)
-            x_c = x_of["c"][c][:, j, :]
+            x_c, x_o = x_of["c"][c][:, j, :], x_of["o"][c][:, j, :]
+            upper = x_o.bitcast(BF16).rearrange("p (u h) -> p u h", h=2)[:, :, 1]
             nc.scalar.activation(out=x_c, in_=x_c, func=ACT.Tanh, scale=-1.0)
             nc.scalar.activation(out=ramp_i[c][:, j, :], in_=x_of["i"][c][:, j, :], func=ACT.Relu, scale=HS_SLOPE, bias=0.5)
             nc.scalar.activation(out=new("ramp_f", k, 3), in_=x_of["f"][c][:, j, :], func=ACT.Relu, scale=HS_SLOPE, bias=0.5)
-
-        def gates_last(k):
-            c, j = divmod(k, PACK)
-            x_o = x_of["o"][c][:, j, :]
-            upper = x_o.bitcast(BF16).rearrange("p (u h) -> p u h", h=2)[:, :, 1]
             nc.scalar.activation(out=new("abs_o", k, 2, BF16), in_=upper, func=ACT.Abs)
             nc.scalar.activation(out=new("ramp_o", k, 4), in_=x_o, func=ACT.Relu, scale=HS_SLOPE * HS_SLOPE, bias=0.5 * HS_SLOPE)
 
@@ -187,14 +182,18 @@ def tile_vlstmcell_v_kernel(
         def halves():
             return (slice(0, HALF), slice(HALF, UNITS))
 
+        def pairs():
+            return (slice(0, PACK // 2), slice(PACK // 2, PACK))
+
         def quarter(n):
             return slice(n * QUARTER, (n + 1) * QUARTER)
 
-        def abs_of(g, c):
-            size[g, c] = work.tile([P, PACK, UNITS], BF16, name="abs_" + g, bufs=2)
-            upper = x_of[g][c][:].bitcast(BF16).rearrange("p j (u h) -> p j u h", h=2)
-            for units in halves():
-                nc.scalar.activation(out=size[g, c][:, :, units], in_=upper[:, :, units, 1], func=ACT.Abs)
+        def abs_of(g, c, n):
+            if n == 0:
+                size[g, c] = work.tile([P, PACK, UNITS], BF16, name="abs_" + g, bufs=2)
+            for tokens in pairs()[n : n + 1]:
+                upper = x_of[g][c][:, tokens, :].bitcast(BF16).rearrange("p j (u h) -> p j u h", h=2)[:, :, :, 1]
+                nc.scalar.activation(out=size[g, c][:, tokens, :], in_=upper, func=ACT.Abs)
 
         def scale_tanh_c(c, n):
             scaled_tanh_c[c, n] = psum.tile([P, PACK, QUARTER], F32, name="bank")
@@ -206,30 +205,35 @@ def tile_vlstmcell_v_kernel(
         def dx_o(c, n):
             dx_product("o", c, quarter(n), scaled_tanh_c[c, n][:], open_o[c][:, :, quarter(n)])
 
-        def mask_f(c, units):
-            mask = size["f", c][:, :, units]
+        def mask_f(c):
+            mask = size["f", c][:]
             nc.vector.tensor_scalar(out=mask, in0=mask, scalar1=HS_EDGE, scalar2=-1.0, op0=ALU.is_lt, op1=ALU.mult)
 
-        def open_f(c, units):
-            mask = size["f", c][:, :, units]
-            nc.vector.tensor_tensor(out=mask, in0=mask, in1=cell[c][:, :, units], op=ALU.mult)
+        def open_f(c, tokens):
+            mask = size["f", c][:, tokens, :]
+            nc.vector.tensor_tensor(out=mask, in0=mask, in1=cell[c][:, tokens, :], op=ALU.mult)
 
         def dx_f(c, units):
             dx_product("f", c, units, x_of["o"][c][:, :, units], size["f", c][:, :, units])
 
-        def open_i(c, units):
-            stt(x_of["i"][c][:, :, units], size["i", c][:, :, units], HS_EDGE, ALU.is_lt, x_of["c"][c][:, :, units])
+        def open_i(c, tokens):
+            stt(x_of["i"][c][:, tokens, :], size["i", c][:, tokens, :], HS_EDGE, ALU.is_lt, x_of["c"][c][:, tokens, :])
 
         def dx_i(c, units):
             dx_product("i", c, units, x_of["o"][c][:, :, units], x_of["i"][c][:, :, units])
 
-        def square_tanh_x(c, units):
-            plane_c = x_of["c"][c][:, :, units]
+        def square_tanh_x(c, tokens):
+            plane_c = x_of["c"][c][:, tokens, :]
             nc.scalar.activation(out=plane_c, in_=plane_c, func=ACT.Square, scale=math.sqrt(1.0 / HS_SLOPE))
 
-        def minus_dc_i(c, units):
-            plane_i = ramp_i[c][:, :, units]
-            stt(plane_i, plane_i, 1.0, ALU.min, x_of["o"][c][:, :, units])
+        def minus_dc_i(c, tokens):
+            plane_i = ramp_i[c][:, tokens, :]
+            stt(plane_i, plane_i, 1.0, ALU.min, x_of["o"][c][:, tokens, :])
+
+        def minus_dc_i_chunk(k):
+            c, j = divmod(k, PACK)
+            plane_i = ramp_i[c][:, j, :]
+            stt(plane_i, plane_i, 1.0, ALU.min, x_of["o"][c][:, j, :])
 
         def dx_c(c, units):
             nc.vector.scalar_tensor_tensor(
@@ -273,94 +277,118 @@ def tile_vlstmcell_v_kernel(
                 empty_bank(g, m)
 
         first, second = halves()
-        gates_first(0)
-        gates_last(0)
-        regroup_inputs(0)
-        quantise_inputs(0)
-        for t in range(CHUNKS + 1):
-            if t < CHUNKS:
-                cell_products(t)
-            else:
-                for step in (mask_f, open_f):
-                    for units in halves():
-                        step(0, units)
-            if 1 <= t < PIECES:
-                quantise_inputs(t)
-                if t + 1 < PIECES:
-                    regroup_inputs(t + 1)
-            if t in (4, 5):
-                for n in (0, 1):
-                    if t == 5:
-                        dx_o(0, n)
-                for n in (0, 1):
-                    scale_tanh_c(0, 2 * (t - 4) + n)
+        early, late = pairs()
+
+        def fill(t):
+            if t == 0:
+                regroup_inputs(0)
+            if t == 1:
+                quantise_inputs(1)
+                regroup_inputs(2)
+            if t == 2:
+                quantise_inputs(2)
+            if t == 3:
+                regroup_inputs(3)
+                minus_dc_i_chunk(0)
+            if t == 4:
+                quantise_inputs(3)
+                minus_dc_i_chunk(1)
+                scale_tanh_c(0, 0)
+                scale_tanh_c(0, 1)
+            if t == 5:
+                regroup_inputs(4)
+                scale_tanh_c(0, 2)
+                scale_tanh_c(0, 3)
             if t == 6:
+                dx_o(0, 0)
+                dx_o(0, 1)
+                mask_f(0)
+            if t == 7:
                 dx_o(0, 2)
                 dx_o(0, 3)
-            if t == 7:
-                for units in halves():
-                    minus_dc_i(0, units)
-            if t >= 1:
-                minus_dc(t - 1)
+            if t == 8:
+                dx_f(0, first)
+                quantise_dx("o", 0)
+                open_i(0, early)
+            if t == 9:
+                pass
+
+        def after(t):
+            if t == 0:
+                quantise_inputs(0)
+                regroup_inputs(1)
+            if t == 4:
+                minus_dc_i_chunk(2)
+            if t == 5:
+                quantise_inputs(4)
+                minus_dc_i_chunk(3)
+            if t == 6:
+                open_f(0, early)
+                open_f(0, late)
+
+        def scalar_after(t):
+            if t in (3, 4):
+                abs_of("f", 0, t - 3)
+            if t in (5, 6):
+                abs_of("i", 0, t - 5)
+
+        gates(0)
+        for t in range(CHUNKS + 2):
+            if t < CHUNKS:
+                cell_products(t)
+            fill(t)
+            if t >= 2:
+                minus_dc(t - 2)
             if t < CHUNKS:
                 grad_products(t)
-            if t == 0:
-                regroup_inputs(1)
-            if t == 6:
-                quantise_dx("o", 0)
+            after(t)
             if t + 1 < CHUNKS:
-                gates_first(t + 1)
-            if t == CHUNKS - 1:
-                abs_of("f", 0)
+                gates(t + 1)
             if t < CHUNKS:
                 tanh_of_cell(t)
-            if t + 1 < CHUNKS:
-                gates_last(t + 1)
-        abs_of("f", 1)
-
+            scalar_after(t)
+        for n in range(2):
+            abs_of("f", 1, n)
         for n in range(4):
             scale_tanh_c(1, n)
-        for units in halves():
-            dx_f(0, units)
-        for n in range(4):
+        dx_o(1, 0)
+        dx_f(0, second)
+        for n in (1, 2, 3):
             dx_o(1, n)
+        open_i(0, late)
         quantise_dx("o", 1)
-        multiply("o")
-
-        mask_f(1, first)
+        mask_f(1)
         quantise_dx("f", 0)
-        mask_f(1, second)
-        for step in (open_f, dx_f):
-            for units in halves():
-                step(1, units)
-        abs_of("i", 0)
-        empty_banks("o")
-        abs_of("i", 1)
-        open_i(0, first)
-        quantise_dx("f", 1)
-        open_i(0, second)
-        multiply("f")
-
+        dx_i(0, first)
+        for tokens in pairs():
+            open_f(1, tokens)
+        multiply("o")
         for units in halves():
-            dx_i(0, units)
-        open_i(1, first)
+            dx_f(1, units)
+        for n in range(2):
+            abs_of("i", 1, n)
+        empty_banks("o")
+        dx_i(0, second)
+        quantise_dx("f", 1)
+        open_i(1, early)
         quantise_dx("i", 0)
-        open_i(1, second)
+        open_i(1, late)
+        multiply("f")
         for units in halves():
             dx_i(1, units)
+        for tokens in pairs():
+            square_tanh_x(0, tokens)
         empty_banks("f")
-        for c in range(PASSES):
-            for units in halves():
-                square_tanh_x(c, units)
-        minus_dc_i(1, first)
+        for tokens in pairs():
+            square_tanh_x(1, tokens)
+        dx_c(0, first)
         quantise_dx("i", 1)
-        minus_dc_i(1, second)
+        dx_c(0, second)
         multiply("i")
-
-        for units in halves():
-            dx_c(0, units)
-        dx_c(1, quarter(0))
+        minus_dc_i(1, early)
         quantise_dx("c", 0)
+        minus_dc_i(1, late)
+        dx_c(1, quarter(0))
         dx_c(1, quarter(1))
         dx_c(1, quarter(2))
         quantise_dx("c", 1, first)

@@ -72,17 +72,23 @@ def tile_vlstmcell_v_kernel(
             c, j = divmod(k, PACK)
             nc.sync.dma_start(out=plane[c][:, j, :], in_=token_rows(source, c)[:, j, :])
 
+        cell_at = {k: k % 4 + 1 for k in range(8)}
+        pieces_at = {100: (0,), 0: (1,), 1: (2,), 3: (3,), 5: (4,)}
         for k in range(CHUNKS):
-            load_gate("c", k)
-            load_gate("i", k)
-            load_gate("f", k)
-            load_half(cell, c_tm1, k)
-            load_gate("o", k)
-            if k == 0:
-                load_inputs(0)
-            load_half(grad, grad_out, k)
-            for piece in {0: (1,), 1: (2,), 2: (3,), 3: (4,)}.get(k, ()):
-                load_inputs(piece)
+            c, j = divmod(k, PACK)
+            for name in ["c","i","f","cell","q","o","grad","p"]:
+                if name in GATES:
+                    load_gate(name, k)
+                elif name == "p":
+                    for piece in pieces_at.get(k, ()):
+                        load_inputs(piece)
+                elif name == "q":
+                    for piece in pieces_at.get(k + 100, ()):
+                        load_inputs(piece)
+                elif k in cell_at:
+                    plane, source = (cell, c_tm1) if name == "cell" else (grad, grad_out)
+                    tokens = slice(j, cell_at[k])
+                    nc.sync.dma_start(out=plane[c][:, tokens, :], in_=token_rows(source, c)[:, tokens, :])
 
         identity = keep.tile([P, P], F32)
         make_identity(nc, identity[:])
@@ -124,13 +130,18 @@ def tile_vlstmcell_v_kernel(
         def stt(target, in0, scalar, op0, in1):
             nc.vector.scalar_tensor_tensor(out=target, in0=in0, scalar=scalar, in1=in1, op0=op0, op1=ALU.mult)
 
-        def gates(k):
+        def gates_a(k):
             c, j = divmod(k, PACK)
             x_c, x_o = x_of["c"][c][:, j, :], x_of["o"][c][:, j, :]
             upper = x_o.bitcast(BF16).rearrange("p (u h) -> p u h", h=2)[:, :, 1]
             nc.scalar.activation(out=x_c, in_=x_c, func=ACT.Tanh, scale=-1.0)
             nc.scalar.activation(out=ramp_i[c][:, j, :], in_=x_of["i"][c][:, j, :], func=ACT.Relu, scale=HS_SLOPE, bias=0.5)
             nc.scalar.activation(out=new("ramp_f", k, 3), in_=x_of["f"][c][:, j, :], func=ACT.Relu, scale=HS_SLOPE, bias=0.5)
+
+        def gates_b(k):
+            c, j = divmod(k, PACK)
+            x_o = x_of["o"][c][:, j, :]
+            upper = x_o.bitcast(BF16).rearrange("p (u h) -> p u h", h=2)[:, :, 1]
             nc.scalar.activation(out=new("abs_o", k, 2, BF16), in_=upper, func=ACT.Abs)
             nc.scalar.activation(out=new("ramp_o", k, 4), in_=x_o, func=ACT.Relu, scale=HS_SLOPE * HS_SLOPE, bias=0.5 * HS_SLOPE)
 
@@ -226,6 +237,10 @@ def tile_vlstmcell_v_kernel(
             plane_c = x_of["c"][c][:, tokens, :]
             nc.scalar.activation(out=plane_c, in_=plane_c, func=ACT.Square, scale=math.sqrt(1.0 / HS_SLOPE))
 
+        def slope_of_tanh_x(c, tokens):
+            plane_c = x_of["c"][c][:, tokens, :]
+            nc.scalar.activation(out=plane_c, in_=plane_c, func=ACT.Copy, bias=-1.0 / HS_SLOPE)
+
         def minus_dc_i(c, tokens):
             plane_i = ramp_i[c][:, tokens, :]
             stt(plane_i, plane_i, 1.0, ALU.min, x_of["o"][c][:, tokens, :])
@@ -236,10 +251,7 @@ def tile_vlstmcell_v_kernel(
             stt(plane_i, plane_i, 1.0, ALU.min, x_of["o"][c][:, j, :])
 
         def dx_c(c, units):
-            nc.vector.scalar_tensor_tensor(
-                out=target("c", c, units), in0=x_of["c"][c][:, :, units].rearrange("p j u -> p u j"), scalar=1.0 / HS_SLOPE,
-                in1=ramp_i[c][:, :, units].rearrange("p j u -> p u j"), op0=ALU.subtract, op1=ALU.mult,
-            )
+            dx_product("c", c, units, x_of["c"][c][:, :, units], ramp_i[c][:, :, units])
 
         def quantise_dx(g, c, units=slice(0, UNITS)):
             n = GATES.index(g)
@@ -284,11 +296,9 @@ def tile_vlstmcell_v_kernel(
                 regroup_inputs(0)
             if t == 1:
                 quantise_inputs(1)
-                regroup_inputs(2)
             if t == 2:
                 quantise_inputs(2)
             if t == 3:
-                regroup_inputs(3)
                 minus_dc_i_chunk(0)
             if t == 4:
                 quantise_inputs(3)
@@ -311,12 +321,16 @@ def tile_vlstmcell_v_kernel(
                 quantise_dx("o", 0)
                 open_i(0, early)
             if t == 9:
-                pass
+                open_i(0, late)
 
         def after(t):
             if t == 0:
                 quantise_inputs(0)
                 regroup_inputs(1)
+            if t == 1:
+                regroup_inputs(2)
+            if t == 3:
+                regroup_inputs(3)
             if t == 4:
                 minus_dc_i_chunk(2)
             if t == 5:
@@ -332,7 +346,8 @@ def tile_vlstmcell_v_kernel(
             if t in (5, 6):
                 abs_of("i", 0, t - 5)
 
-        gates(0)
+        gates_a(0)
+        gates_b(0)
         for t in range(CHUNKS + 2):
             if t < CHUNKS:
                 cell_products(t)
@@ -343,9 +358,11 @@ def tile_vlstmcell_v_kernel(
                 grad_products(t)
             after(t)
             if t + 1 < CHUNKS:
-                gates(t + 1)
+                gates_a(t + 1)
             if t < CHUNKS:
                 tanh_of_cell(t)
+            if t + 1 < CHUNKS:
+                gates_b(t + 1)
             scalar_after(t)
         for n in range(2):
             abs_of("f", 1, n)
@@ -355,32 +372,35 @@ def tile_vlstmcell_v_kernel(
         dx_f(0, second)
         for n in (1, 2, 3):
             dx_o(1, n)
-        open_i(0, late)
         quantise_dx("o", 1)
         mask_f(1)
         quantise_dx("f", 0)
-        dx_i(0, first)
         for tokens in pairs():
             open_f(1, tokens)
         multiply("o")
         for units in halves():
             dx_f(1, units)
+        dx_i(0, first)
         for n in range(2):
             abs_of("i", 1, n)
+        for tokens in pairs():
+            square_tanh_x(0, tokens)
+        for tokens in pairs():
+            slope_of_tanh_x(0, tokens)
         empty_banks("o")
-        dx_i(0, second)
         quantise_dx("f", 1)
+        dx_i(0, second)
         open_i(1, early)
         quantise_dx("i", 0)
         open_i(1, late)
         multiply("f")
         for units in halves():
             dx_i(1, units)
-        for tokens in pairs():
-            square_tanh_x(0, tokens)
         empty_banks("f")
         for tokens in pairs():
             square_tanh_x(1, tokens)
+        for tokens in pairs():
+            slope_of_tanh_x(1, tokens)
         dx_c(0, first)
         quantise_dx("i", 1)
         dx_c(0, second)

@@ -130,18 +130,13 @@ def tile_vlstmcell_v_kernel(
         def stt(target, in0, scalar, op0, in1):
             nc.vector.scalar_tensor_tensor(out=target, in0=in0, scalar=scalar, in1=in1, op0=op0, op1=ALU.mult)
 
-        def gates_a(k):
+        def gates(k):
             c, j = divmod(k, PACK)
             x_c, x_o = x_of["c"][c][:, j, :], x_of["o"][c][:, j, :]
             upper = x_o.bitcast(BF16).rearrange("p (u h) -> p u h", h=2)[:, :, 1]
             nc.scalar.activation(out=x_c, in_=x_c, func=ACT.Tanh, scale=-1.0)
             nc.scalar.activation(out=ramp_i[c][:, j, :], in_=x_of["i"][c][:, j, :], func=ACT.Relu, scale=HS_SLOPE, bias=0.5)
             nc.scalar.activation(out=new("ramp_f", k, 3), in_=x_of["f"][c][:, j, :], func=ACT.Relu, scale=HS_SLOPE, bias=0.5)
-
-        def gates_b(k):
-            c, j = divmod(k, PACK)
-            x_o = x_of["o"][c][:, j, :]
-            upper = x_o.bitcast(BF16).rearrange("p (u h) -> p u h", h=2)[:, :, 1]
             nc.scalar.activation(out=new("abs_o", k, 2, BF16), in_=upper, func=ACT.Abs)
             nc.scalar.activation(out=new("ramp_o", k, 4), in_=x_o, func=ACT.Relu, scale=HS_SLOPE * HS_SLOPE, bias=0.5 * HS_SLOPE)
 
@@ -346,8 +341,7 @@ def tile_vlstmcell_v_kernel(
             if t in (5, 6):
                 abs_of("i", 0, t - 5)
 
-        gates_a(0)
-        gates_b(0)
+        gates(0)
         for t in range(CHUNKS + 2):
             if t < CHUNKS:
                 cell_products(t)
@@ -358,11 +352,9 @@ def tile_vlstmcell_v_kernel(
                 grad_products(t)
             after(t)
             if t + 1 < CHUNKS:
-                gates_a(t + 1)
+                gates(t + 1)
             if t < CHUNKS:
                 tanh_of_cell(t)
-            if t + 1 < CHUNKS:
-                gates_b(t + 1)
             scalar_after(t)
         for n in range(2):
             abs_of("f", 1, n)

@@ -19,7 +19,8 @@ P = 128
 PACK = 4
 K_PASS = P * PACK
 PASSES = TOKENS // K_PASS
-CHUNKS = PASSES * PACK
+GROUPS = [(0, 0, 1), (0, 1, 2), (0, 2, 4), (1, 0, 2), (1, 2, 4)]
+LOADS = [("c", 0), ("i", 0), ("f", 0), ("cell", 0), 0, ("o", 0), ("grad", 0), 1, ("c", 1), ("i", 1), ("f", 1), ("cell", 1), ("o", 1), ("grad", 1), 2, ("c", 2), ("i", 2), ("f", 2), ("cell", 2), ("o", 2), ("grad", 2), 3, ("c", 3), ("i", 3), ("f", 3), ("cell", 3), ("o", 3), ("grad", 3), 4, ("c", 4), ("i", 4), ("f", 4), ("cell", 4), ("o", 4), ("grad", 4)]
 M_TILE = 128
 M_TILES = FEATURES // M_TILE
 BANKS = 8
@@ -55,6 +56,11 @@ def tile_vlstmcell_v_kernel(
         ramp_i = full_plane("ramp_i", F32)
         tanh_c = full_plane("tanh_c", F32)
         open_o = full_plane("open_o", BF16)
+        open_f = full_plane("open_f", BF16)
+
+        def part(planes, k):
+            c, first, end = GROUPS[k]
+            return planes[c][:, first:end, :]
 
         raw_in = {}
 
@@ -63,32 +69,21 @@ def tile_vlstmcell_v_kernel(
             raw_in[piece] = work.tile([P, PACK, width], BF16, name="raw_in", bufs=3)
             nc.sync.dma_start(out=raw_in[piece][:], in_=token_rows(inputs, c)[:, :, first : first + width])
 
-        def load_gate(g, k):
-            c, j = divmod(k, PACK)
-            first = GATES.index(g) * UNITS
-            nc.sync.dma_start(out=x_of[g][c][:, j, :], in_=token_rows(x, c)[:, j, first : first + UNITS])
+        def load(name, k):
+            c, first, end = GROUPS[k]
+            if name in GATES:
+                column = GATES.index(name) * UNITS
+                planes, source = x_of[name], token_rows(x, c)[:, first:end, column : column + UNITS]
+            else:
+                planes, tensor = (cell, c_tm1) if name == "cell" else (grad, grad_out)
+                source = token_rows(tensor, c)[:, first:end, :]
+            nc.sync.dma_start(out=part(planes, k), in_=source)
 
-        def load_half(plane, source, k):
-            c, j = divmod(k, PACK)
-            nc.sync.dma_start(out=plane[c][:, j, :], in_=token_rows(source, c)[:, j, :])
-
-        cell_at = {k: k % 4 + 1 for k in range(8)}
-        pieces_at = {100: (0,), 0: (1,), 1: (2,), 3: (3,), 5: (4,)}
-        for k in range(CHUNKS):
-            c, j = divmod(k, PACK)
-            for name in ["c","i","f","cell","q","o","grad","p"]:
-                if name in GATES:
-                    load_gate(name, k)
-                elif name == "p":
-                    for piece in pieces_at.get(k, ()):
-                        load_inputs(piece)
-                elif name == "q":
-                    for piece in pieces_at.get(k + 100, ()):
-                        load_inputs(piece)
-                elif k in cell_at:
-                    plane, source = (cell, c_tm1) if name == "cell" else (grad, grad_out)
-                    tokens = slice(j, cell_at[k])
-                    nc.sync.dma_start(out=plane[c][:, tokens, :], in_=token_rows(source, c)[:, tokens, :])
+        for item in LOADS:
+            if isinstance(item, int):
+                load_inputs(item)
+            else:
+                load(item[0], item[1])
 
         identity = keep.tile([P, P], F32)
         make_identity(nc, identity[:])
@@ -123,53 +118,79 @@ def tile_vlstmcell_v_kernel(
         plane = {}
         new_cell = {}
 
-        def new(name, k, bufs, dtype=F32):
-            plane[name, k] = work.tile([P, UNITS], dtype, name=name, bufs=bufs)
-            return plane[name, k][:]
+        def upper_half(ap):
+            return ap.bitcast(BF16).rearrange("p j (u h) -> p j u h", h=2)[:, :, :, 1]
 
         def stt(target, in0, scalar, op0, in1):
             nc.vector.scalar_tensor_tensor(out=target, in0=in0, scalar=scalar, in1=in1, op0=op0, op1=ALU.mult)
 
-        def gates(k):
-            c, j = divmod(k, PACK)
-            x_c, x_o = x_of["c"][c][:, j, :], x_of["o"][c][:, j, :]
-            upper = x_o.bitcast(BF16).rearrange("p (u h) -> p u h", h=2)[:, :, 1]
-            nc.scalar.activation(out=x_c, in_=x_c, func=ACT.Tanh, scale=-1.0)
-            nc.scalar.activation(out=ramp_i[c][:, j, :], in_=x_of["i"][c][:, j, :], func=ACT.Relu, scale=HS_SLOPE, bias=0.5)
-            nc.scalar.activation(out=new("ramp_f", k, 3), in_=x_of["f"][c][:, j, :], func=ACT.Relu, scale=HS_SLOPE, bias=0.5)
-            nc.scalar.activation(out=new("abs_o", k, 2, BF16), in_=upper, func=ACT.Abs)
-            nc.scalar.activation(out=new("ramp_o", k, 4), in_=x_o, func=ACT.Relu, scale=HS_SLOPE * HS_SLOPE, bias=0.5 * HS_SLOPE)
+        def activate(target, source, func, scale=1.0, bias=0.0):
+            nc.scalar.activation(out=target, in_=source, func=func, scale=scale, bias=bias)
+
+        def tanh_x(k):
+            activate(part(x_of["c"], k), part(x_of["c"], k), ACT.Tanh, scale=-1.0)
+
+        def s_ramp_i(k):
+            activate(part(ramp_i, k), part(x_of["i"], k), ACT.Relu, scale=HS_SLOPE, bias=0.5)
+
+        def s_abs_f(k):
+            activate(part(open_f, k), upper_half(part(x_of["f"], k)), ACT.Abs)
+
+        def s_ramp_f(k):
+            activate(part(x_of["f"], k), part(x_of["f"], k), ACT.Relu, scale=HS_SLOPE, bias=0.5)
+
+        def s_abs_o(k):
+            activate(part(open_o, k), upper_half(part(x_of["o"], k)), ACT.Abs)
+
+        def s_ramp_o(k):
+            activate(part(x_of["o"], k), part(x_of["o"], k), ACT.Relu, scale=HS_SLOPE * HS_SLOPE, bias=0.5 * HS_SLOPE)
+
+        def s_abs_i(k):
+            c, first, end = GROUPS[k]
+            plane["abs_i", k] = work.tile([P, end - first, UNITS], BF16, name="abs_i", bufs=2)
+            activate(plane["abs_i", k][:], upper_half(part(x_of["i"], k)), ACT.Abs)
 
         def tanh_of_cell(k):
-            c, j = divmod(k, PACK)
-            nc.scalar.activation(out=tanh_c[c][:, j, :], in_=new_cell[k][:], func=ACT.Tanh)
-            nc.scalar.activation(out=x_of["o"][c][:, j, :], in_=tanh_c[c][:, j, :], func=ACT.Square)
+            c, first, end = GROUPS[k]
+            for j in range(first, end):
+                activate(tanh_c[c][:, j, :], new_cell[c, j][:], ACT.Tanh)
 
-        def cell_products(k):
-            c, j = divmod(k, PACK)
-            i_tanh_x = new("i_tanh_x", k, 2)
-            stt(i_tanh_x, ramp_i[c][:, j, :], 1.0, ALU.min, x_of["c"][c][:, j, :])
-            f_cell = plane["ramp_f", k][:]
-            stt(f_cell, f_cell, 1.0, ALU.min, cell[c][:, j, :])
-            new_cell[k] = psum.tile([P, UNITS], F32, name="bank")
-            nc.tensor.matmul(out=new_cell[k][:], lhsT=minus_identity[:], rhs=i_tanh_x, start=True, stop=False)
-            nc.tensor.matmul(out=new_cell[k][:], lhsT=identity[:], rhs=f_cell, start=False, stop=True)
+        def square_of_tanh(k):
+            activate(part(x_of["f"], k), part(tanh_c, k), ACT.Square)
+
+        def input_product(k):
+            c, first, end = GROUPS[k]
+            i_tanh_x = work.tile([P, end - first, UNITS], F32, name="i_tanh_x", bufs=2)
+            stt(i_tanh_x[:], part(ramp_i, k), 1.0, ALU.min, part(x_of["c"], k))
+            for j in range(first, end):
+                new_cell[c, j] = psum.tile([P, UNITS], F32, name="bank")
+                nc.tensor.matmul(out=new_cell[c, j][:], lhsT=minus_identity[:], rhs=i_tanh_x[:, j - first, :], start=True, stop=False)
+
+        def forget_product(k):
+            c, first, end = GROUPS[k]
+            stt(part(x_of["f"], k), part(x_of["f"], k), 1.0, ALU.min, part(cell, k))
+            for j in range(first, end):
+                nc.tensor.matmul(out=new_cell[c, j][:], lhsT=identity[:], rhs=x_of["f"][c][:, j, :], start=False, stop=True)
+
+        def open_i(k):
+            stt(part(x_of["i"], k), plane["abs_i", k][:], HS_EDGE, ALU.is_lt, part(x_of["c"], k))
+
+        def mask(planes, k):
+            nc.vector.tensor_scalar(out=part(planes, k), in0=part(planes, k), scalar1=HS_EDGE, scalar2=-1.0, op0=ALU.is_lt, op1=ALU.mult)
+
+        def o_grad(k):
+            stt(part(x_of["o"], k), part(x_of["o"], k), HS_SLOPE, ALU.min, part(grad, k))
+
+        def opened(planes, factor, k):
+            nc.vector.tensor_tensor(out=part(planes, k), in0=part(planes, k), in1=part(factor, k), op=ALU.mult)
 
         def minus_dc(k):
-            c, j = divmod(k, PACK)
-            dc = x_of["o"][c][:, j, :]
-            stt(dc, dc, 1.0, ALU.subtract, plane["ramp_o", k][:])
+            stt(part(x_of["f"], k), part(x_of["f"], k), 1.0, ALU.subtract, part(x_of["o"], k))
 
-        def grad_products(k):
-            c, j = divmod(k, PACK)
-            mask = plane["abs_o", k][:]
-            nc.vector.tensor_scalar(out=mask, in0=mask, scalar1=HS_EDGE, scalar2=-1.0, op0=ALU.is_lt, op1=ALU.mult)
-            o_grad = plane["ramp_o", k][:]
-            stt(o_grad, o_grad, HS_SLOPE, ALU.min, grad[c][:, j, :])
-            nc.vector.tensor_tensor(out=open_o[c][:, j, :], in0=grad[c][:, j, :], in1=mask, op=ALU.mult)
+        def minus_dc_i(k):
+            stt(part(ramp_i, k), part(ramp_i, k), 1.0, ALU.min, part(x_of["f"], k))
 
         grouped = {}
-        size = {}
         scaled_tanh_c = {}
 
         def runs(ap):
@@ -194,13 +215,6 @@ def tile_vlstmcell_v_kernel(
         def quarter(n):
             return slice(n * QUARTER, (n + 1) * QUARTER)
 
-        def abs_of(g, c, n):
-            if n == 0:
-                size[g, c] = work.tile([P, PACK, UNITS], BF16, name="abs_" + g, bufs=2)
-            for tokens in pairs()[n : n + 1]:
-                upper = x_of[g][c][:, tokens, :].bitcast(BF16).rearrange("p j (u h) -> p j u h", h=2)[:, :, :, 1]
-                nc.scalar.activation(out=size[g, c][:, tokens, :], in_=upper, func=ACT.Abs)
-
         def scale_tanh_c(c, n):
             scaled_tanh_c[c, n] = psum.tile([P, PACK, QUARTER], F32, name="bank")
             nc.tensor.matmul(
@@ -211,39 +225,22 @@ def tile_vlstmcell_v_kernel(
         def dx_o(c, n):
             dx_product("o", c, quarter(n), scaled_tanh_c[c, n][:], open_o[c][:, :, quarter(n)])
 
-        def mask_f(c):
-            mask = size["f", c][:]
-            nc.vector.tensor_scalar(out=mask, in0=mask, scalar1=HS_EDGE, scalar2=-1.0, op0=ALU.is_lt, op1=ALU.mult)
-
-        def open_f(c, tokens):
-            mask = size["f", c][:, tokens, :]
-            nc.vector.tensor_tensor(out=mask, in0=mask, in1=cell[c][:, tokens, :], op=ALU.mult)
-
         def dx_f(c, units):
-            dx_product("f", c, units, x_of["o"][c][:, :, units], size["f", c][:, :, units])
-
-        def open_i(c, tokens):
-            stt(x_of["i"][c][:, tokens, :], size["i", c][:, tokens, :], HS_EDGE, ALU.is_lt, x_of["c"][c][:, tokens, :])
+            dx_product("f", c, units, x_of["f"][c][:, :, units], open_f[c][:, :, units])
 
         def dx_i(c, units):
-            dx_product("i", c, units, x_of["o"][c][:, :, units], x_of["i"][c][:, :, units])
+            dx_product("i", c, units, x_of["f"][c][:, :, units], x_of["i"][c][:, :, units])
 
-        def square_tanh_x(c, tokens):
+        def square_tanh_x(c, tokens=slice(0, PACK)):
             plane_c = x_of["c"][c][:, tokens, :]
             nc.scalar.activation(out=plane_c, in_=plane_c, func=ACT.Square, scale=math.sqrt(1.0 / HS_SLOPE))
 
-        def slope_of_tanh_x(c, tokens):
+        def slope_of_tanh_x(c, tokens=slice(0, PACK)):
             plane_c = x_of["c"][c][:, tokens, :]
-            nc.scalar.activation(out=plane_c, in_=plane_c, func=ACT.Copy, bias=-1.0 / HS_SLOPE)
-
-        def minus_dc_i(c, tokens):
-            plane_i = ramp_i[c][:, tokens, :]
-            stt(plane_i, plane_i, 1.0, ALU.min, x_of["o"][c][:, tokens, :])
-
-        def minus_dc_i_chunk(k):
-            c, j = divmod(k, PACK)
-            plane_i = ramp_i[c][:, j, :]
-            stt(plane_i, plane_i, 1.0, ALU.min, x_of["o"][c][:, j, :])
+            if (0, 1)[c]:
+                nc.vector.tensor_scalar(out=plane_c, in0=plane_c, scalar1=-1.0 / HS_SLOPE, scalar2=None, op0=ALU.add)
+            else:
+                nc.scalar.activation(out=plane_c, in_=plane_c, func=ACT.Copy, bias=-1.0 / HS_SLOPE)
 
         def dx_c(c, units):
             dx_product("c", c, units, x_of["c"][c][:, :, units], ramp_i[c][:, :, units])
@@ -257,12 +254,14 @@ def tile_vlstmcell_v_kernel(
 
         sums = {}
 
-        def multiply(g):
+        def multiply(g, by_pass=False):
             n = GATES.index(g)
-            for m in range(M_TILES):
-                sums[g, m] = psum.tile([M_TILE, UNITS], F32, name="bank")
-            for c in range(PASSES):
-                for m in range(M_TILES):
+            order = [(m, c) for m in range(M_TILES) for c in range(PASSES)]
+            if by_pass:
+                order = [(m, c) for c in range(PASSES) for m in range(M_TILES)]
+            for m, c in order:
+                    if c == 0:
+                        sums[g, m] = psum.tile([M_TILE, UNITS], F32, name="bank")
                     features = slice(m * M_TILE, (m + 1) * M_TILE)
                     nc.tensor.matmul_mx(
                         out=sums[g, m][:], lhsT=in_codes[:, c, features].bitcast(E4M3_X4), lhsT_scale=in_scales[:, c, features],
@@ -285,129 +284,136 @@ def tile_vlstmcell_v_kernel(
 
         first, second = halves()
         early, late = pairs()
+        def scalar_front(k):
+            tanh_x(k)
+            s_ramp_i(k)
+            s_abs_f(k)
+            s_ramp_f(k)
+            s_abs_o(k)
+            s_ramp_o(k)
+            s_abs_i(k)
 
-        def fill(t):
-            if t == 0:
-                regroup_inputs(0)
-            if t == 1:
-                quantise_inputs(1)
-            if t == 2:
-                quantise_inputs(2)
-            if t == 3:
-                minus_dc_i_chunk(0)
-            if t == 4:
-                quantise_inputs(3)
-                minus_dc_i_chunk(1)
-                scale_tanh_c(0, 0)
-                scale_tanh_c(0, 1)
-            if t == 5:
-                regroup_inputs(4)
-                scale_tanh_c(0, 2)
-                scale_tanh_c(0, 3)
-            if t == 6:
-                dx_o(0, 0)
-                dx_o(0, 1)
-                mask_f(0)
-            if t == 7:
-                dx_o(0, 2)
-                dx_o(0, 3)
-            if t == 8:
-                dx_f(0, first)
-                quantise_dx("o", 0)
-                open_i(0, early)
-            if t == 9:
-                open_i(0, late)
+        def masks(k):
+            mask(open_f, k)
+            mask(open_o, k)
 
-        def after(t):
-            if t == 0:
-                quantise_inputs(0)
-                regroup_inputs(1)
-            if t == 1:
-                regroup_inputs(2)
-            if t == 3:
-                regroup_inputs(3)
-            if t == 4:
-                minus_dc_i_chunk(2)
-            if t == 5:
-                quantise_inputs(4)
-                minus_dc_i_chunk(3)
-            if t == 6:
-                open_f(0, early)
-                open_f(0, late)
+        def opens(k):
+            opened(open_f, cell, k)
+            opened(open_o, grad, k)
 
-        def scalar_after(t):
-            if t in (3, 4):
-                abs_of("f", 0, t - 3)
-            if t in (5, 6):
-                abs_of("i", 0, t - 5)
+        def scalar_cell(k):
+            tanh_of_cell(k)
+            square_of_tanh(k)
 
-        gates(0)
-        for t in range(CHUNKS + 2):
-            if t < CHUNKS:
-                cell_products(t)
-            fill(t)
-            if t >= 2:
-                minus_dc(t - 2)
-            if t < CHUNKS:
-                grad_products(t)
-            after(t)
-            if t + 1 < CHUNKS:
-                gates(t + 1)
-            if t < CHUNKS:
-                tanh_of_cell(t)
-            scalar_after(t)
-        for n in range(2):
-            abs_of("f", 1, n)
+        scalar_front(0)
+        scalar_front(1)
+        input_product(0)
+        forget_product(0)
+        regroup_inputs(0)
+        masks(0)
+        regroup_inputs(1)
+        o_grad(0)
+        opens(0)
+        quantise_inputs(0)
+        open_i(0)
+        quantise_inputs(1)
+        scalar_cell(0)
+        scalar_front(2)
+        input_product(1)
+        forget_product(1)
+        masks(1)
+        o_grad(1)
+        opens(1)
+        open_i(1)
+        scalar_cell(1)
+        scalar_front(3)
+        regroup_inputs(2)
+        minus_dc(0)
+        quantise_inputs(2)
+        minus_dc_i(0)
+        input_product(2)
+        forget_product(2)
+        masks(2)
+        regroup_inputs(3)
+        o_grad(2)
+        opens(2)
+        quantise_inputs(3)
+        minus_dc(1)
+        open_i(2)
+        minus_dc_i(1)
+        scalar_cell(2)
+        scalar_front(4)
+        input_product(3)
+        forget_product(3)
+        masks(3)
+        regroup_inputs(4)
+        o_grad(3)
+        opens(3)
+        quantise_inputs(4)
+        scale_tanh_c(0, 0)
+        scale_tanh_c(0, 1)
+        open_i(3)
+        minus_dc(2)
+        scalar_cell(3)
+        dx_f(0, first)
+        minus_dc_i(2)
+        input_product(4)
+        dx_f(0, second)
+        forget_product(4)
+        quantise_dx("f", 0)
+        scale_tanh_c(0, 2)
+        scale_tanh_c(0, 3)
+        mask(open_f, 4)
+        o_grad(4)
+        opened(open_f, cell, 4)
+        open_i(4)
+        scalar_cell(4)
+        square_tanh_x(0)
+        slope_of_tanh_x(0)
+        square_tanh_x(1)
+        mask(open_o, 4)
+        dx_o(0, 0)
+        minus_dc(3)
+        dx_o(0, 1)
+        dx_o(0, 2)
+        minus_dc(4)
         for n in range(4):
             scale_tanh_c(1, n)
+        opened(open_o, grad, 4)
+        dx_f(1, first)
+        dx_f(1, second)
+        dx_o(0, 3)
+        quantise_dx("f", 1)
+        multiply("f")
+        empty_banks("f")
         dx_o(1, 0)
-        dx_f(0, second)
+        quantise_dx("o", 0)
         for n in (1, 2, 3):
             dx_o(1, n)
         quantise_dx("o", 1)
-        mask_f(1)
-        quantise_dx("f", 0)
-        for tokens in pairs():
-            open_f(1, tokens)
         multiply("o")
-        for units in halves():
-            dx_f(1, units)
-        dx_i(0, first)
-        for n in range(2):
-            abs_of("i", 1, n)
-        for tokens in pairs():
-            square_tanh_x(0, tokens)
-        for tokens in pairs():
-            slope_of_tanh_x(0, tokens)
         empty_banks("o")
-        quantise_dx("f", 1)
+        dx_i(0, first)
         dx_i(0, second)
-        open_i(1, early)
+        dx_i(1, first)
         quantise_dx("i", 0)
-        open_i(1, late)
-        multiply("f")
-        for units in halves():
-            dx_i(1, units)
-        empty_banks("f")
-        for tokens in pairs():
-            square_tanh_x(1, tokens)
-        for tokens in pairs():
-            slope_of_tanh_x(1, tokens)
-        dx_c(0, first)
+        dx_i(1, second)
+        minus_dc_i(3)
         quantise_dx("i", 1)
-        dx_c(0, second)
         multiply("i")
-        minus_dc_i(1, early)
-        quantise_dx("c", 0)
-        minus_dc_i(1, late)
+        empty_banks("i")
+        dx_c(0, first)
+        slope_of_tanh_x(1)
+        minus_dc_i(4)
+        dx_c(0, second)
         dx_c(1, quarter(0))
+        quantise_dx("c", 0)
         dx_c(1, quarter(1))
         dx_c(1, quarter(2))
         quantise_dx("c", 1, first)
         dx_c(1, quarter(3))
         quantise_dx("c", 1, quarter(2))
         quantise_dx("c", 1, quarter(3))
-        empty_banks("i")
-        multiply("c")
+        multiply("c", by_pass=True)
         for m in range(M_TILES):
             empty_bank("c", m, by_vector=(m % 2 == 1))

@@ -98,10 +98,10 @@ def tile_vlstmcell_v_kernel(
         dx_scales = keep.tile([P, len(GATES), PASSES, UNITS], U8, align_bytes=64)
         grouped_in = {}
 
-        def regroup_inputs(piece):
+        def regroup_inputs(piece, by_scalar=False):
             width = IN_PIECES[piece][2]
             grouped_in[piece] = work.tile([P, width, PACK], BF16, align_bytes=64, name="grouped_in", bufs=2)
-            nc.vector.tensor_copy(
+            (nc.scalar.copy if by_scalar else nc.vector.tensor_copy)(
                 out=grouped_in[piece][:].rearrange("p (w i) j -> p w j i", i=4),
                 in_=raw_in[piece][:].rearrange("p j (w i) -> p w j i", i=4),
             )
@@ -237,7 +237,7 @@ def tile_vlstmcell_v_kernel(
 
         def slope_of_tanh_x(c, tokens=slice(0, PACK)):
             plane_c = x_of["c"][c][:, tokens, :]
-            if (0, 1)[c]:
+            if (0, 0)[c]:
                 nc.vector.tensor_scalar(out=plane_c, in0=plane_c, scalar1=-1.0 / HS_SLOPE, scalar2=None, op0=ALU.add)
             else:
                 nc.scalar.activation(out=plane_c, in_=plane_c, func=ACT.Copy, bias=-1.0 / HS_SLOPE)
@@ -287,11 +287,14 @@ def tile_vlstmcell_v_kernel(
         def scalar_front(k):
             tanh_x(k)
             s_ramp_i(k)
+            if k == 0:
+                s_abs_i(k)
             s_abs_f(k)
             s_ramp_f(k)
             s_abs_o(k)
             s_ramp_o(k)
-            s_abs_i(k)
+            if k > 0:
+                s_abs_i(k)
 
         def masks(k):
             mask(open_f, k)
@@ -308,14 +311,14 @@ def tile_vlstmcell_v_kernel(
         scalar_front(0)
         scalar_front(1)
         input_product(0)
-        forget_product(0)
+        open_i(0)
         regroup_inputs(0)
+        forget_product(0)
         masks(0)
         regroup_inputs(1)
         o_grad(0)
         opens(0)
         quantise_inputs(0)
-        open_i(0)
         quantise_inputs(1)
         scalar_cell(0)
         scalar_front(2)
@@ -355,11 +358,11 @@ def tile_vlstmcell_v_kernel(
         open_i(3)
         minus_dc(2)
         scalar_cell(3)
-        dx_f(0, first)
-        minus_dc_i(2)
         input_product(4)
+        dx_f(0, first)
         dx_f(0, second)
         forget_product(4)
+        minus_dc_i(2)
         quantise_dx("f", 0)
         scale_tanh_c(0, 2)
         scale_tanh_c(0, 3)
@@ -371,6 +374,7 @@ def tile_vlstmcell_v_kernel(
         square_tanh_x(0)
         slope_of_tanh_x(0)
         square_tanh_x(1)
+        slope_of_tanh_x(1)
         mask(open_o, 4)
         dx_o(0, 0)
         minus_dc(3)
@@ -390,6 +394,7 @@ def tile_vlstmcell_v_kernel(
         quantise_dx("o", 0)
         for n in (1, 2, 3):
             dx_o(1, n)
+        minus_dc_i(3)
         quantise_dx("o", 1)
         multiply("o")
         empty_banks("o")
@@ -398,13 +403,11 @@ def tile_vlstmcell_v_kernel(
         dx_i(1, first)
         quantise_dx("i", 0)
         dx_i(1, second)
-        minus_dc_i(3)
+        minus_dc_i(4)
         quantise_dx("i", 1)
         multiply("i")
         empty_banks("i")
         dx_c(0, first)
-        slope_of_tanh_x(1)
-        minus_dc_i(4)
         dx_c(0, second)
         dx_c(1, quarter(0))
         quantise_dx("c", 0)

@@ -23,6 +23,7 @@ GROUPS = [(0, 0, 1), (0, 1, 2), (0, 2, 4), (1, 0, 2), (1, 2, 4)]
 LOADS = [("c", 0), ("i", 0), ("f", 0), ("cell", 0), 0, ("o", 0), ("grad", 0), 1, ("c", 1), ("i", 1), ("f", 1), ("cell", 1), ("o", 1), ("grad", 1), 2, ("c", 2), ("i", 2), ("f", 2), ("cell", 2), ("o", 2), ("grad", 2), 3, ("c", 3), ("i", 3), ("f", 3), ("cell", 3), ("o", 3), ("grad", 3), 4, ("c", 4), ("i", 4), ("f", 4), ("cell", 4), ("o", 4), ("grad", 4)]
 M_TILE = 128
 M_TILES = FEATURES // M_TILE
+AHEAD = 6
 BANKS = 8
 IN_PIECES = [(0, 0, 256), (0, 256, 256), (0, 512, 512), (1, 0, 512), (1, 512, 512)]
 HALF = UNITS // 2
@@ -254,20 +255,19 @@ def tile_vlstmcell_v_kernel(
 
         sums = {}
 
-        def multiply(g, by_pass=False):
+        def multiply(g):
             n = GATES.index(g)
-            order = [(m, c) for m in range(M_TILES) for c in range(PASSES)]
-            if by_pass:
-                order = [(m, c) for c in range(PASSES) for m in range(M_TILES)]
+            order = [(m, c) for c in range(PASSES) for m in range(AHEAD)]
+            order += [(m, c) for m in range(AHEAD, M_TILES) for c in range(PASSES)]
             for m, c in order:
-                    if c == 0:
-                        sums[g, m] = psum.tile([M_TILE, UNITS], F32, name="bank")
-                    features = slice(m * M_TILE, (m + 1) * M_TILE)
-                    nc.tensor.matmul_mx(
-                        out=sums[g, m][:], lhsT=in_codes[:, c, features].bitcast(E4M3_X4), lhsT_scale=in_scales[:, c, features],
-                        rhs=dx_codes[:, n, c, :].bitcast(E5M2_X4), rhs_scale=dx_scales[:, n, c, :],
-                        start=(c == 0), stop=(c == PASSES - 1),
-                    )
+                if c == 0:
+                    sums[g, m] = psum.tile([M_TILE, UNITS], F32, name="bank")
+                features = slice(m * M_TILE, (m + 1) * M_TILE)
+                nc.tensor.matmul_mx(
+                    out=sums[g, m][:], lhsT=in_codes[:, c, features].bitcast(E4M3_X4), lhsT_scale=in_scales[:, c, features],
+                    rhs=dx_codes[:, n, c, :].bitcast(E5M2_X4), rhs_scale=dx_scales[:, n, c, :],
+                    start=(c == 0), stop=(c == PASSES - 1),
+                )
 
         def empty_bank(g, m, by_vector=False):
             n = GATES.index(g)
@@ -417,6 +417,6 @@ def tile_vlstmcell_v_kernel(
         dx_c(1, quarter(3))
         quantise_dx("c", 1, quarter(2))
         quantise_dx("c", 1, quarter(3))
-        multiply("c", by_pass=True)
+        multiply("c")
         for m in range(M_TILES):
             empty_bank("c", m, by_vector=(m % 2 == 1))

@@ -23,7 +23,7 @@ GROUPS = [(0, 0, 1), (0, 1, 2), (0, 2, 4), (1, 0, 2), (1, 2, 4)]
 LOADS = [("c", 0), ("i", 0), ("f", 0), ("cell", 0), 0, ("o", 0), ("grad", 0), 1, ("c", 1), ("i", 1), ("f", 1), ("cell", 1), ("o", 1), ("grad", 1), 2, ("c", 2), ("i", 2), ("f", 2), ("cell", 2), ("o", 2), ("grad", 2), 3, ("c", 3), ("i", 3), ("f", 3), ("cell", 3), ("o", 3), ("grad", 3), 4, ("c", 4), ("i", 4), ("f", 4), ("cell", 4), ("o", 4), ("grad", 4)]
 M_TILE = 128
 M_TILES = FEATURES // M_TILE
-AHEAD = 6
+AHEAD = 4
 BANKS = 8
 IN_PIECES = [(0, 0, 256), (0, 256, 256), (0, 512, 512), (1, 0, 512), (1, 512, 512)]
 HALF = UNITS // 2
@@ -223,6 +223,12 @@ def tile_vlstmcell_v_kernel(
                 start=True, stop=True,
             )
 
+        def scale_tanh_c_by_scalar(c):
+            activate(tanh_c[c][:], tanh_c[c][:], ACT.Copy, scale=-HS_SLOPE)
+
+        def dx_o_from_plane(c, units):
+            dx_product("o", c, units, tanh_c[c][:, :, units], open_o[c][:, :, units])
+
         def dx_o(c, n):
             dx_product("o", c, quarter(n), scaled_tanh_c[c, n][:], open_o[c][:, :, quarter(n)])
 
@@ -284,17 +290,18 @@ def tile_vlstmcell_v_kernel(
 
         first, second = halves()
         early, late = pairs()
-        def scalar_front(k):
+        def gates(k):
             tanh_x(k)
             s_ramp_i(k)
-            if k == 0:
-                s_abs_i(k)
             s_abs_f(k)
+            s_abs_i(k)
             s_ramp_f(k)
             s_abs_o(k)
+            if k > 0:
+                tanh_of_cell(k - 1)
             s_ramp_o(k)
             if k > 0:
-                s_abs_i(k)
+                square_of_tanh(k - 1)
 
         def masks(k):
             mask(open_f, k)
@@ -304,60 +311,54 @@ def tile_vlstmcell_v_kernel(
             opened(open_f, cell, k)
             opened(open_o, grad, k)
 
-        def scalar_cell(k):
-            tanh_of_cell(k)
-            square_of_tanh(k)
 
-        scalar_front(0)
-        scalar_front(1)
+        gates(0)
         input_product(0)
         open_i(0)
         regroup_inputs(0)
         forget_product(0)
         masks(0)
         regroup_inputs(1)
-        o_grad(0)
         opens(0)
+        o_grad(0)
         quantise_inputs(0)
-        quantise_inputs(1)
-        scalar_cell(0)
-        scalar_front(2)
+        gates(1)
         input_product(1)
+        quantise_inputs(1)
+        open_i(1)
         forget_product(1)
         masks(1)
-        o_grad(1)
         opens(1)
-        open_i(1)
-        scalar_cell(1)
-        scalar_front(3)
+        o_grad(1)
+        gates(2)
         regroup_inputs(2)
         minus_dc(0)
         quantise_inputs(2)
-        minus_dc_i(0)
         input_product(2)
+        minus_dc_i(0)
+        open_i(2)
         forget_product(2)
         masks(2)
         regroup_inputs(3)
-        o_grad(2)
         opens(2)
+        o_grad(2)
         quantise_inputs(3)
         minus_dc(1)
-        open_i(2)
-        minus_dc_i(1)
-        scalar_cell(2)
-        scalar_front(4)
+        gates(3)
         input_product(3)
+        minus_dc_i(1)
+        open_i(3)
         forget_product(3)
         masks(3)
+        opens(3)
         regroup_inputs(4)
         o_grad(3)
-        opens(3)
         quantise_inputs(4)
         scale_tanh_c(0, 0)
         scale_tanh_c(0, 1)
-        open_i(3)
         minus_dc(2)
-        scalar_cell(3)
+        gates(4)
+        square_tanh_x(0, early)
         input_product(4)
         dx_f(0, first)
         dx_f(0, second)
@@ -370,11 +371,11 @@ def tile_vlstmcell_v_kernel(
         o_grad(4)
         opened(open_f, cell, 4)
         open_i(4)
-        scalar_cell(4)
-        square_tanh_x(0)
+        tanh_of_cell(4)
+        square_tanh_x(0, late)
+        square_of_tanh(4)
         slope_of_tanh_x(0)
         square_tanh_x(1)
-        slope_of_tanh_x(1)
         mask(open_o, 4)
         dx_o(0, 0)
         minus_dc(3)
@@ -390,6 +391,7 @@ def tile_vlstmcell_v_kernel(
         quantise_dx("f", 1)
         multiply("f")
         empty_banks("f")
+        slope_of_tanh_x(1)
         dx_o(1, 0)
         quantise_dx("o", 0)
         for n in (1, 2, 3):

import math
from contextlib import ExitStack

import concourse.mybir as mybir
from concourse.masks import make_identity

F32 = mybir.dt.float32
BF16 = mybir.dt.bfloat16
U32 = mybir.dt.uint32
U8 = mybir.dt.uint8
E4M3_X4 = mybir.dt.float8_e4m3fn_x4
E5M2_X4 = mybir.dt.float8_e5m2_x4
ALU = mybir.AluOpType
ACT = mybir.ActivationFunctionType

TOKENS, FEATURES, UNITS = 1024, 1024, 512
GATES = "ifco"
P = 128
PACK = 4
K_PASS = P * PACK
PASSES = TOKENS // K_PASS
GROUPS = [(0, 0, 1), (0, 1, 2), (0, 2, 4), (1, 0, 2), (1, 2, 4)]
LOADS = [("c", 0), ("i", 0), ("f", 0), ("cell", 0), 0, ("o", 0), ("grad", 0), 1, ("c", 1), ("i", 1), ("f", 1), ("cell", 1), ("o", 1), ("grad", 1), 2, ("c", 2), ("i", 2), ("f", 2), ("cell", 2), ("o", 2), ("grad", 2), 3, ("c", 3), ("i", 3), ("f", 3), ("cell", 3), ("o", 3), ("grad", 3), 4, ("c", 4), ("i", 4), ("f", 4), ("cell", 4), ("o", 4), ("grad", 4)]
M_TILE = 128
M_TILES = FEATURES // M_TILE
AHEAD = 4
BANKS = 8
IN_PIECES = [(0, 0, 256), (0, 256, 256), (0, 512, 512), (1, 0, 512), (1, 512, 512)]
HALF = UNITS // 2
QUARTER = UNITS // 4
RUN = 8
HS_SLOPE, HS_EDGE = 0.2, 2.5

FLOPS = 2 * TOKENS * FEATURES * len(GATES) * UNITS
BYTES = 2 * TOKENS * (FEATURES + 2 * UNITS) + 4 * TOKENS * len(GATES) * UNITS + 4 * FEATURES * len(GATES) * UNITS


def tile_vlstmcell_v_kernel(
    tc, inputs, h_tm1, c_tm1, z_tm1, kernel, recurrent_kernel, recurrent_latent, bias, x, grad_out, out
):
    nc = tc.nc
    with ExitStack() as stack:
        keep = stack.enter_context(tc.tile_pool(name="keep", bufs=1))
        work = stack.enter_context(tc.tile_pool(name="work", bufs=2))
        psum = stack.enter_context(tc.psum_pool(name="psum", bufs=BANKS))
        stack.enter_context(tc.manual_schedule())

        def token_rows(ap, c):
            return ap[c * K_PASS : (c + 1) * K_PASS, :].rearrange("(p j) w -> p j w", j=PACK)

        def full_plane(name, dtype):
            return [keep.tile([P, PACK, UNITS], dtype, name="%s_%d" % (name, c)) for c in range(PASSES)]

        x_of = {g: full_plane("x_" + g, F32) for g in GATES}
        cell = full_plane("cell", BF16)
        grad = full_plane("grad", BF16)
        ramp_i = full_plane("ramp_i", F32)
        tanh_c = full_plane("tanh_c", F32)
        open_o = full_plane("open_o", BF16)
        open_f = full_plane("open_f", BF16)

        def part(planes, k):
            c, first, end = GROUPS[k]
            return planes[c][:, first:end, :]

        raw_in = {}

        def load_inputs(piece):
            c, first, width = IN_PIECES[piece]
            raw_in[piece] = work.tile([P, PACK, width], BF16, name="raw_in", bufs=3)
            nc.sync.dma_start(out=raw_in[piece][:], in_=token_rows(inputs, c)[:, :, first : first + width])

        def load(name, k):
            c, first, end = GROUPS[k]
            if name in GATES:
                column = GATES.index(name) * UNITS
                planes, source = x_of[name], token_rows(x, c)[:, first:end, column : column + UNITS]
            else:
                planes, tensor = (cell, c_tm1) if name == "cell" else (grad, grad_out)
                source = token_rows(tensor, c)[:, first:end, :]
            nc.sync.dma_start(out=part(planes, k), in_=source)

        for item in LOADS:
            if isinstance(item, int):
                load_inputs(item)
            else:
                load(item[0], item[1])

        identity = keep.tile([P, P], F32)
        make_identity(nc, identity[:])
        minus_identity = keep.tile([P, P], F32)
        nc.vector.tensor_scalar(out=minus_identity[:], in0=identity[:], scalar1=-1.0, scalar2=None, op0=ALU.mult)
        minus_slope = keep.tile([P, P], F32)
        nc.vector.tensor_scalar(out=minus_slope[:], in0=identity[:], scalar1=-HS_SLOPE, scalar2=None, op0=ALU.mult)

        in_codes = keep.tile([P, PASSES, FEATURES], U32, align_bytes=64)
        in_scales = keep.tile([P, PASSES, FEATURES], U8, align_bytes=64)
        dx_codes = keep.tile([P, len(GATES), PASSES, UNITS], U32, align_bytes=64)
        dx_scales = keep.tile([P, len(GATES), PASSES, UNITS], U8, align_bytes=64)
        grouped_in = {}

        def regroup_inputs(piece, by_scalar=False):
            width = IN_PIECES[piece][2]
            grouped_in[piece] = work.tile([P, width, PACK], BF16, align_bytes=64, name="grouped_in", bufs=2)
            (nc.scalar.copy if by_scalar else nc.vector.tensor_copy)(
                out=grouped_in[piece][:].rearrange("p (w i) j -> p w j i", i=4),
                in_=raw_in[piece][:].rearrange("p j (w i) -> p w j i", i=4),
            )

        def quantise_inputs(piece):
            c, first, width = IN_PIECES[piece]
            features = slice(first, first + width)
            nc.vector.quantize_mx(
                out=in_codes[:, c, features].bitcast(E4M3_X4),
                scales=in_scales[:, c, features],
                in_=grouped_in[piece][:].rearrange("p w j -> p (w j)"),
            )

        plane = {}
        new_cell = {}

        def upper_half(ap):
            return ap.bitcast(BF16).rearrange("p j (u h) -> p j u h", h=2)[:, :, :, 1]

        def stt(target, in0, scalar, op0, in1):
            nc.vector.scalar_tensor_tensor(out=target, in0=in0, scalar=scalar, in1=in1, op0=op0, op1=ALU.mult)

        def activate(target, source, func, scale=1.0, bias=0.0):
            nc.scalar.activation(out=target, in_=source, func=func, scale=scale, bias=bias)

        def tanh_x(k):
            activate(part(x_of["c"], k), part(x_of["c"], k), ACT.Tanh, scale=-1.0)

        def s_ramp_i(k):
            activate(part(ramp_i, k), part(x_of["i"], k), ACT.Relu, scale=HS_SLOPE, bias=0.5)

        def s_abs_f(k):
            activate(part(open_f, k), upper_half(part(x_of["f"], k)), ACT.Abs)

        def s_ramp_f(k):
            activate(part(x_of["f"], k), part(x_of["f"], k), ACT.Relu, scale=HS_SLOPE, bias=0.5)

        def s_abs_o(k):
            activate(part(open_o, k), upper_half(part(x_of["o"], k)), ACT.Abs)

        def s_ramp_o(k):
            activate(part(x_of["o"], k), part(x_of["o"], k), ACT.Relu, scale=HS_SLOPE * HS_SLOPE, bias=0.5 * HS_SLOPE)

        def s_abs_i(k):
            c, first, end = GROUPS[k]
            plane["abs_i", k] = work.tile([P, end - first, UNITS], BF16, name="abs_i", bufs=2)
            activate(plane["abs_i", k][:], upper_half(part(x_of["i"], k)), ACT.Abs)

        def tanh_of_cell(k):
            c, first, end = GROUPS[k]
            for j in range(first, end):
                activate(tanh_c[c][:, j, :], new_cell[c, j][:], ACT.Tanh)

        def square_of_tanh(k):
            activate(part(x_of["f"], k), part(tanh_c, k), ACT.Square)

        def input_product(k):
            c, first, end = GROUPS[k]
            i_tanh_x = work.tile([P, end - first, UNITS], F32, name="i_tanh_x", bufs=2)
            stt(i_tanh_x[:], part(ramp_i, k), 1.0, ALU.min, part(x_of["c"], k))
            for j in range(first, end):
                new_cell[c, j] = psum.tile([P, UNITS], F32, name="bank")
                nc.tensor.matmul(out=new_cell[c, j][:], lhsT=minus_identity[:], rhs=i_tanh_x[:, j - first, :], start=True, stop=False)

        def forget_product(k):
            c, first, end = GROUPS[k]
            stt(part(x_of["f"], k), part(x_of["f"], k), 1.0, ALU.min, part(cell, k))
            for j in range(first, end):
                nc.tensor.matmul(out=new_cell[c, j][:], lhsT=identity[:], rhs=x_of["f"][c][:, j, :], start=False, stop=True)

        def open_i(k):
            stt(part(x_of["i"], k), plane["abs_i", k][:], HS_EDGE, ALU.is_lt, part(x_of["c"], k))

        def mask(planes, k):
            nc.vector.tensor_scalar(out=part(planes, k), in0=part(planes, k), scalar1=HS_EDGE, scalar2=-1.0, op0=ALU.is_lt, op1=ALU.mult)

        def o_grad(k):
            stt(part(x_of["o"], k), part(x_of["o"], k), HS_SLOPE, ALU.min, part(grad, k))

        def opened(planes, factor, k):
            nc.vector.tensor_tensor(out=part(planes, k), in0=part(planes, k), in1=part(factor, k), op=ALU.mult)

        def minus_dc(k):
            stt(part(x_of["f"], k), part(x_of["f"], k), 1.0, ALU.subtract, part(x_of["o"], k))

        def minus_dc_i(k):
            stt(part(ramp_i, k), part(ramp_i, k), 1.0, ALU.min, part(x_of["f"], k))

        grouped = {}
        scaled_tanh_c = {}

        def runs(ap):
            return ap.rearrange("p j (w i) -> p w j i", i=RUN)

        def target(g, c, units):
            if (g, c) not in grouped:
                grouped[g, c] = work.tile([P, UNITS, PACK], BF16, align_bytes=64, name="grouped_dx", bufs=3)
            return grouped[g, c][:, units, :]

        def dx_product(g, c, units, in0, in1):
            nc.vector.tensor_tensor(
                out=target(g, c, units).rearrange("p (w i) j -> p w j i", i=RUN), in0=runs(in0), in1=runs(in1), op=ALU.mult
            )

        def halves():
            return (slice(0, HALF), slice(HALF, UNITS))

        def pairs():
            return (slice(0, PACK // 2), slice(PACK // 2, PACK))

        def quarter(n):
            return slice(n * QUARTER, (n + 1) * QUARTER)

        def scale_tanh_c(c, n):
            scaled_tanh_c[c, n] = psum.tile([P, PACK, QUARTER], F32, name="bank")
            nc.tensor.matmul(
                out=scaled_tanh_c[c, n][:].rearrange("p j u -> p (j u)"), lhsT=minus_slope[:], rhs=tanh_c[c][:, :, quarter(n)],
                start=True, stop=True,
            )

        def scale_tanh_c_by_scalar(c):
            activate(tanh_c[c][:], tanh_c[c][:], ACT.Copy, scale=-HS_SLOPE)

        def dx_o_from_plane(c, units):
            dx_product("o", c, units, tanh_c[c][:, :, units], open_o[c][:, :, units])

        def dx_o(c, n):
            dx_product("o", c, quarter(n), scaled_tanh_c[c, n][:], open_o[c][:, :, quarter(n)])

        def dx_f(c, units):
            dx_product("f", c, units, x_of["f"][c][:, :, units], open_f[c][:, :, units])

        def dx_i(c, units):
            dx_product("i", c, units, x_of["f"][c][:, :, units], x_of["i"][c][:, :, units])

        def square_tanh_x(c, tokens=slice(0, PACK)):
            plane_c = x_of["c"][c][:, tokens, :]
            nc.scalar.activation(out=plane_c, in_=plane_c, func=ACT.Square, scale=math.sqrt(1.0 / HS_SLOPE))

        def slope_of_tanh_x(c, tokens=slice(0, PACK)):
            plane_c = x_of["c"][c][:, tokens, :]
            if (0, 0)[c]:
                nc.vector.tensor_scalar(out=plane_c, in0=plane_c, scalar1=-1.0 / HS_SLOPE, scalar2=None, op0=ALU.add)
            else:
                nc.scalar.activation(out=plane_c, in_=plane_c, func=ACT.Copy, bias=-1.0 / HS_SLOPE)

        def dx_c(c, units):
            dx_product("c", c, units, x_of["c"][c][:, :, units], ramp_i[c][:, :, units])

        def quantise_dx(g, c, units=slice(0, UNITS)):
            n = GATES.index(g)
            nc.vector.quantize_mx(
                out=dx_codes[:, n, c, units].bitcast(E5M2_X4), scales=dx_scales[:, n, c, units],
                in_=grouped[g, c][:, units, :].rearrange("p u j -> p (u j)"),
            )

        sums = {}

        def multiply(g):
            n = GATES.index(g)
            order = [(m, c) for c in range(PASSES) for m in range(AHEAD)]
            order += [(m, c) for m in range(AHEAD, M_TILES) for c in range(PASSES)]
            for m, c in order:
                if c == 0:
                    sums[g, m] = psum.tile([M_TILE, UNITS], F32, name="bank")
                features = slice(m * M_TILE, (m + 1) * M_TILE)
                nc.tensor.matmul_mx(
                    out=sums[g, m][:], lhsT=in_codes[:, c, features].bitcast(E4M3_X4), lhsT_scale=in_scales[:, c, features],
                    rhs=dx_codes[:, n, c, :].bitcast(E5M2_X4), rhs_scale=dx_scales[:, n, c, :],
                    start=(c == 0), stop=(c == PASSES - 1),
                )

        def empty_bank(g, m, by_vector=False):
            n = GATES.index(g)
            result = work.tile([M_TILE, UNITS], F32, name="result", bufs=8)
            if by_vector:
                nc.vector.tensor_copy(out=result[:], in_=sums[g, m][:])
            else:
                nc.scalar.copy(out=result[:], in_=sums[g, m][:])
            nc.sync.dma_start(out=out[m * M_TILE : (m + 1) * M_TILE, n * UNITS : (n + 1) * UNITS], in_=result[:])

        def empty_banks(g):
            for m in range(M_TILES):
                empty_bank(g, m)

        first, second = halves()
        early, late = pairs()
        def gates(k):
            tanh_x(k)
            s_ramp_i(k)
            s_abs_f(k)
            s_abs_i(k)
            s_ramp_f(k)
            s_abs_o(k)
            if k > 0:
                tanh_of_cell(k - 1)
            s_ramp_o(k)
            if k > 0:
                square_of_tanh(k - 1)

        def masks(k):
            mask(open_f, k)
            mask(open_o, k)

        def opens(k):
            opened(open_f, cell, k)
            opened(open_o, grad, k)


        gates(0)
        input_product(0)
        open_i(0)
        regroup_inputs(0)
        forget_product(0)
        masks(0)
        regroup_inputs(1)
        opens(0)
        o_grad(0)
        quantise_inputs(0)
        gates(1)
        input_product(1)
        quantise_inputs(1)
        open_i(1)
        forget_product(1)
        masks(1)
        opens(1)
        o_grad(1)
        gates(2)
        regroup_inputs(2)
        minus_dc(0)
        quantise_inputs(2)
        input_product(2)
        minus_dc_i(0)
        open_i(2)
        forget_product(2)
        masks(2)
        regroup_inputs(3)
        opens(2)
        o_grad(2)
        quantise_inputs(3)
        minus_dc(1)
        gates(3)
        input_product(3)
        minus_dc_i(1)
        open_i(3)
        forget_product(3)
        masks(3)
        opens(3)
        regroup_inputs(4)
        o_grad(3)
        quantise_inputs(4)
        scale_tanh_c(0, 0)
        scale_tanh_c(0, 1)
        minus_dc(2)
        gates(4)
        square_tanh_x(0, early)
        input_product(4)
        dx_f(0, first)
        dx_f(0, second)
        forget_product(4)
        minus_dc_i(2)
        quantise_dx("f", 0)
        scale_tanh_c(0, 2)
        scale_tanh_c(0, 3)
        mask(open_f, 4)
        o_grad(4)
        opened(open_f, cell, 4)
        open_i(4)
        tanh_of_cell(4)
        square_tanh_x(0, late)
        square_of_tanh(4)
        slope_of_tanh_x(0)
        square_tanh_x(1)
        mask(open_o, 4)
        dx_o(0, 0)
        minus_dc(3)
        dx_o(0, 1)
        dx_o(0, 2)
        minus_dc(4)
        for n in range(4):
            scale_tanh_c(1, n)
        opened(open_o, grad, 4)
        dx_f(1, first)
        dx_f(1, second)
        dx_o(0, 3)
        quantise_dx("f", 1)
        multiply("f")
        empty_banks("f")
        slope_of_tanh_x(1)
        dx_o(1, 0)
        quantise_dx("o", 0)
        for n in (1, 2, 3):
            dx_o(1, n)
        minus_dc_i(3)
        quantise_dx("o", 1)
        multiply("o")
        empty_banks("o")
        dx_i(0, first)
        dx_i(0, second)
        dx_i(1, first)
        quantise_dx("i", 0)
        dx_i(1, second)
        minus_dc_i(4)
        quantise_dx("i", 1)
        multiply("i")
        empty_banks("i")
        dx_c(0, first)
        dx_c(0, second)
        dx_c(1, quarter(0))
        quantise_dx("c", 0)
        dx_c(1, quarter(1))
        dx_c(1, quarter(2))
        quantise_dx("c", 1, first)
        dx_c(1, quarter(3))
        quantise_dx("c", 1, quarter(2))
        quantise_dx("c", 1, quarter(3))
        multiply("c")
        for m in range(M_TILES):
            empty_bank("c", m, by_vector=(m % 2 == 1))
